import numpy as np
import ml_dtypes


def mxq(x, axis, fmt="e4m3"):
    dtype, down = {"e4m3": (ml_dtypes.float8_e4m3fn, 7), "e5m2": (ml_dtypes.float8_e5m2, 14)}[fmt]
    v = np.moveaxis(np.asarray(x, np.float32).astype(ml_dtypes.bfloat16).astype(np.float64), axis, -1)
    blocks = v.reshape(v.shape[:-1] + (-1, 32))
    amax = np.abs(blocks).max(-1, keepdims=True)
    byte = np.maximum(np.where(amax > 0, np.frexp(amax)[1] - 1 + 127, 0) - down, 1)
    scale = np.exp2(byte - 127.0)
    codes = (blocks / scale).astype(np.float32).astype(dtype).astype(np.float64)
    return np.moveaxis((codes * scale).reshape(v.shape), -1, axis)


WIDE = False


def mx_kscale(k):
    if not WIDE:
        return np.ones(k)
    levels = np.array([10, -10, 5, -5, 0])
    a = np.random.permutation(np.resize(levels, k // 512 * 4)).reshape(k // 512, 4)
    idx = np.arange(k)
    return np.exp2(a[idx // 512, idx % 128 // 32])


BF16 = ml_dtypes.bfloat16


def bf(x):
    return np.asarray(x, np.float32).astype(BF16)


def f64(x):
    return np.asarray(x).astype(np.float64)


S, B, D0, D1, D2, O = 8, 128, 512, 8192, 128, 128


def sample(eps, logvar, mean):
    return eps * np.exp(0.5 * logvar) + mean


def setup_inputs():
    s = mx_kscale(D1)
    return {
        "h0": bf(np.maximum(np.random.standard_normal((S, B, D1)), 0.0) * 1.1 * s),
        "wm1": bf(np.random.standard_normal((D1, D2)) * 0.8 / np.sqrt(D1) / s[:, None]),
        "wv1": bf(2.0 * np.log(0.6 / np.sqrt(D1)) + 0.5 * np.random.standard_normal((D1, D2))),
        "bm1": bf(np.random.standard_normal(D2) * 0.3),
        "bv1": bf(2.0 * np.log(0.3) + 0.5 * np.random.standard_normal(D2)),
        "we1": bf(np.random.standard_normal((S, D1, D2)) / s[None, :, None]),
        "be1": bf(np.random.standard_normal((S, 1, D2))),
    }


def reference(h0, wm1, wv1, bm1, bv1, we1, be1):
    w1 = sample(f64(we1), f64(wv1), f64(wm1))
    b1 = sample(f64(be1), f64(bv1), f64(bm1))
    return np.maximum((mxq(f64(h0), 2, "e4m3") @ mxq(w1, 1, "e4m3")) + b1, 0.0)

@@ -1,0 +1,194 @@
+import concourse.mybir as mybir
+from concourse.masks import make_identity
+
+F32 = mybir.dt.float32
+BF16 = mybir.dt.bfloat16
+U32 = mybir.dt.uint32
+U8 = mybir.dt.uint8
+FP8X4 = mybir.dt.float8_e4m3fn_x4
+ACT = mybir.ActivationFunctionType
+ALU = mybir.AluOpType
+
+S = 8
+B = 128
+K = 8192
+N = 128
+
+P = 128
+PACK = 4
+K_PASS = P * PACK
+PASSES = K // K_PASS
+GROUP = 4
+GROUPS = PASSES // GROUP
+K_GROUP = GROUP * K_PASS
+HALF = S // 2
+PAIR = 2
+
+FLOPS = 2 * S * B * K * N
+
+
+def tile_bnn_pb_k_kernel(tc, h0, wm1, wv1, bm1, bv1, we1, be1, out):
+    nc = tc.nc
+
+    wv_rows = wv1.rearrange("(g c p j) n -> g p c j n", c=GROUP, p=P, j=PACK)
+    wm_rows = wm1.rearrange("(g c p j) n -> g p c j n", c=GROUP, p=P, j=PACK)
+    we_rows = we1.rearrange("s (c p j) n -> c p s j n", p=P, j=PACK)
+    h_rows = h0.rearrange("s b k -> b s k")
+
+    with (
+        tc.tile_pool(name="consts", bufs=1) as consts,
+        tc.tile_pool(name="shared_raw", bufs=1) as shared_raw,
+        tc.tile_pool(name="shared", bufs=2) as shared,
+        tc.tile_pool(name="we_pool", bufs=3) as we_pool,
+        tc.tile_pool(name="h_pool", bufs=3) as h_pool,
+        tc.tile_pool(name="prod_pool", bufs=1) as prod_pool,
+        tc.tile_pool(name="grouped", bufs=2) as grouped,
+        tc.tile_pool(name="quantised", bufs=GROUP + 2) as quantised,
+        tc.psum_pool(name="psum_t", bufs=4) as psum_t,
+        tc.psum_pool(name="psum_acc", bufs=4) as psum_acc,
+    ):
+        ident = consts.tile([P, P], F32)
+        make_identity(nc, ident[:])
+
+        def load_shared(g):
+            wv_raw = shared_raw.tile([P, GROUP, PACK, N], BF16)
+            nc.sync.dma_start(out=wv_raw[:], in_=wv_rows[g])
+            wm_raw = shared_raw.tile([P, GROUP, PACK, N], BF16)
+            nc.sync.dma_start(out=wm_raw[:], in_=wm_rows[g])
+            return wv_raw, wm_raw
+
+        def load_we(c):
+            we_raw = we_pool.tile([P, S, PACK, N], BF16)
+            nc.sync.dma_start(out=we_raw[:], in_=we_rows[c])
+            return we_raw
+
+        def load_h(g):
+            halves = []
+            for half in range(2):
+                h_raw = h_pool.tile([B, HALF, K_GROUP], BF16)
+                nc.sync.dma_start(
+                    out=h_raw[:],
+                    in_=h_rows[:, half * HALF : (half + 1) * HALF, g * K_GROUP : (g + 1) * K_GROUP],
+                )
+                halves.append(h_raw)
+            return halves
+
+        shared_next = load_shared(0)
+        we_ahead = [load_we(0), load_we(1)]
+        h_next = load_h(0)
+
+        be_all = consts.tile([P, S, N], BF16)
+        nc.sync.dma_start(
+            out=be_all[:].rearrange("p s n -> p (s n)"),
+            in_=be1.rearrange("s o n -> (s o n)").partition_broadcast(P),
+        )
+        bv_all = consts.tile([P, N], BF16)
+        nc.sync.dma_start(out=bv_all[:], in_=bv1.partition_broadcast(P))
+        bm_all = consts.tile([P, N], BF16)
+        nc.sync.dma_start(out=bm_all[:], in_=bm1.partition_broadcast(P))
+        b_std = consts.tile([P, N], F32)
+        nc.scalar.activation(out=b_std[:], in_=bv_all[:], func=ACT.Exp, scale=0.5)
+        sums = consts.tile([P, S, N], F32)
+        nc.gpsimd.tensor_tensor(
+            out=sums[:], in0=be_all[:], in1=b_std[:].unsqueeze(1).to_broadcast([P, S, N]), op=ALU.mult
+        )
+        nc.gpsimd.tensor_tensor(
+            out=sums[:], in0=sums[:], in1=bm_all[:].unsqueeze(1).to_broadcast([P, S, N]), op=ALU.add
+        )
+
+        for g in range(GROUPS):
+            wv_raw, wm_raw = shared_next
+            h_halves = h_next
+
+            w_std = shared.tile([P, GROUP, N, PACK], F32)
+            w_mean = shared.tile([P, GROUP, N, PACK], BF16)
+            for cc in range(GROUP):
+                nc.scalar.activation(
+                    out=w_std[:, cc], in_=wv_raw[:, cc].rearrange("p j n -> p n j"), func=ACT.Exp, scale=0.5
+                )
+                nc.scalar.copy(out=w_mean[:, cc], in_=wm_raw[:, cc].rearrange("p j n -> p n j"))
+
+            if g + 1 < GROUPS:
+                shared_next = load_shared(g + 1)
+
+            codes = []
+            for cc in range(GROUP):
+                c = g * GROUP + cc
+                we_raw = we_ahead[c]
+                if c + 2 < PASSES:
+                    we_ahead.append(load_we(c + 2))
+
+                prod = prod_pool.tile([P, S, N, PACK], F32)
+                nc.vector.tensor_tensor(
+                    out=prod[:],
+                    in0=we_raw[:].rearrange("p s j n -> p s n j"),
+                    in1=w_std[:, cc].unsqueeze(1).to_broadcast([P, S, N, PACK]),
+                    op=ALU.mult,
+                )
+                w_bf = grouped.tile([P, S, N, PACK], BF16, align_bytes=64)
+                nc.vector.tensor_tensor(
+                    out=w_bf[:],
+                    in0=prod[:],
+                    in1=w_mean[:, cc].unsqueeze(1).to_broadcast([P, S, N, PACK]),
+                    op=ALU.add,
+                )
+                w_codes = quantised.tile([P, S, N], U32, align_bytes=64)
+                w_scales = quantised.tile([P, S, N], U8, align_bytes=64)
+                nc.vector.quantize_mx(
+                    out=w_codes[:].rearrange("p s n -> p (s n)").bitcast(FP8X4),
+                    scales=w_scales[:].rearrange("p s n -> p (s n)"),
+                    in_=w_bf[:].rearrange("p s n j -> p (s n j)"),
+                )
+
+                h_bf = grouped.tile([P, S, B, PACK], BF16, align_bytes=64)
+                h_words = h_bf[:].bitcast(F32)
+                for pair in range(S // PAIR):
+                    h_t = psum_t.tile([P, PAIR, 2, B], F32)
+                    for i in range(PAIR):
+                        s = pair * PAIR + i
+                        raw_words = h_halves[s // HALF][:].bitcast(F32)
+                        first = cc * (K_PASS // 2)
+                        for u in range(2):
+                            nc.tensor.transpose(
+                                h_t[:, i, u, :],
+                                raw_words[:, s % HALF, first + u : first + K_PASS // 2 : 2],
+                                ident[:],
+                            )
+                    nc.scalar.copy(
+                        out=h_words[:, pair * PAIR : (pair + 1) * PAIR],
+                        in_=h_t[:].rearrange("p i u b -> p i b u"),
+                    )
+                if cc == GROUP - 1 and g + 1 < GROUPS:
+                    h_next = load_h(g + 1)
+                h_codes = quantised.tile([P, S, B], U32, align_bytes=64)
+                h_scales = quantised.tile([P, S, B], U8, align_bytes=64)
+                nc.vector.quantize_mx(
+                    out=h_codes[:].rearrange("p s b -> p (s b)").bitcast(FP8X4),
+                    scales=h_scales[:].rearrange("p s b -> p (s b)"),
+                    in_=h_bf[:].rearrange("p s b j -> p (s b j)"),
+                )
+                codes.append((h_codes, h_scales, w_codes, w_scales))
+
+            for half in range(2):
+                acc = psum_acc.tile([B, HALF, N], F32)
+                for i in range(HALF):
+                    s = half * HALF + i
+                    for cc in range(GROUP):
+                        h_codes, h_scales, w_codes, w_scales = codes[cc]
+                        nc.tensor.matmul_mx(
+                            out=acc[:, i, :],
+                            lhsT=h_codes[:, s, :].bitcast(FP8X4),
+                            lhsT_scale=h_scales[:, s, :],
+                            rhs=w_codes[:, s, :].bitcast(FP8X4),
+                            rhs_scale=w_scales[:, s, :],
+                            start=(cc == 0),
+                            stop=(cc == GROUP - 1),
+                        )
+                these = sums[:, half * HALF : (half + 1) * HALF, :]
+                nc.vector.tensor_tensor(out=these, in0=acc[:], in1=these, op=ALU.add)
+
+        result = consts.tile([B, S, N], F32)
+        for half in range(2):
+            these = slice(half * HALF, (half + 1) * HALF)
+            nc.scalar.activation(out=result[:, these, :], in_=sums[:, these, :], func=ACT.Relu)
+            nc.sync.dma_start(out=out.rearrange("s b n -> b s n")[:, these, :], in_=result[:, these, :])

@@ -20,9 +20,10 @@ K_PASS = P * PACK
 PASSES = K // K_PASS
 GROUP = 4
 GROUPS = PASSES // GROUP
-K_GROUP = GROUP * K_PASS
 HALF = S // 2
 PAIR = 2
+S_VECTOR = 6
+S_GPSIMD = S - S_VECTOR
 
 FLOPS = 2 * S * B * K * N
 
@@ -33,23 +34,23 @@ def tile_bnn_pb_k_kernel(tc, h0, wm1, wv1, bm1, bv1, we1, be1, out):
     wv_rows = wv1.rearrange("(g c p j) n -> g p c j n", c=GROUP, p=P, j=PACK)
     wm_rows = wm1.rearrange("(g c p j) n -> g p c j n", c=GROUP, p=P, j=PACK)
     we_rows = we1.rearrange("s (c p j) n -> c p s j n", p=P, j=PACK)
-    h_rows = h0.rearrange("s b k -> b s k")
+    h_cols = h0.rearrange("s b (c k) -> c b s k", k=K_PASS)
 
     with (
         tc.tile_pool(name="consts", bufs=1) as consts,
-        tc.tile_pool(name="shared_raw", bufs=1) as shared_raw,
-        tc.tile_pool(name="shared", bufs=2) as shared,
-        tc.tile_pool(name="we_pool", bufs=3) as we_pool,
+        tc.tile_pool(name="shared_raw", bufs=2) as shared_raw,
+        tc.tile_pool(name="flipped_pool", bufs=2) as flipped_pool,
+        tc.tile_pool(name="gpsimd_pool", bufs=2) as gpsimd_pool,
+        tc.tile_pool(name="we_pool", bufs=4) as we_pool,
         tc.tile_pool(name="h_pool", bufs=3) as h_pool,
         tc.tile_pool(name="prod_pool", bufs=1) as prod_pool,
         tc.tile_pool(name="grouped", bufs=2) as grouped,
-        tc.tile_pool(name="quantised", bufs=GROUP + 2) as quantised,
-        tc.psum_pool(name="psum_t", bufs=4) as psum_t,
-        tc.psum_pool(name="psum_acc", bufs=4) as psum_acc,
+        tc.tile_pool(name="quantised", bufs=GROUP + 1) as quantised,
+        tc.psum_pool(name="psum_t", bufs=2) as psum_t,
+        tc.psum_pool(name="psum_w", bufs=2) as psum_w,
+        tc.psum_pool(name="psum_acc", bufs=2) as psum_acc,
+        tc.manual_schedule(),
     ):
-        ident = consts.tile([P, P], F32)
-        make_identity(nc, ident[:])
-
         def load_shared(g):
             wv_raw = shared_raw.tile([P, GROUP, PACK, N], BF16)
             nc.sync.dma_start(out=wv_raw[:], in_=wv_rows[g])
@@ -62,119 +63,101 @@ def tile_bnn_pb_k_kernel(tc, h0, wm1, wv1, bm1, bv1, we1, be1, out):
             nc.sync.dma_start(out=we_raw[:], in_=we_rows[c])
             return we_raw
 
-        def load_h(g):
-            halves = []
-            for half in range(2):
-                h_raw = h_pool.tile([B, HALF, K_GROUP], BF16)
-                nc.sync.dma_start(
-                    out=h_raw[:],
-                    in_=h_rows[:, half * HALF : (half + 1) * HALF, g * K_GROUP : (g + 1) * K_GROUP],
+        def load_h(c):
+            h_raw = h_pool.tile([B, S, K_PASS], BF16)
+            nc.sync.dma_start(out=h_raw[:], in_=h_cols[c])
+            return h_raw
+
+        def operands_in_sbuf(c):
+            wv_raw, wm_raw = shared_tiles[c // GROUP]
+            std_sb = gpsimd_pool.tile([P, N, PACK], F32)
+            nc.scalar.activation(
+                out=std_sb[:], in_=wv_raw[:, c % GROUP].rearrange("p j n -> p n j"), func=ACT.Exp, scale=0.5
+            )
+            mean_sb = gpsimd_pool.tile([P, N, PACK], BF16)
+            nc.scalar.copy(out=mean_sb[:], in_=wm_raw[:, c % GROUP].rearrange("p j n -> p n j"))
+            return std_sb[:], mean_sb[:]
+
+        def flip_shared(c):
+            wv_raw, wm_raw = shared_tiles[c // GROUP]
+            flipped = psum_t.tile([N, 2, PACK, P], BF16, tag="t")
+            for j in range(PACK):
+                nc.tensor.transpose(flipped[:, 0, j, :], wv_raw[:, c % GROUP, j, :], ident_bf[:])
+                nc.tensor.transpose(flipped[:, 1, j, :], wm_raw[:, c % GROUP, j, :], ident_bf[:])
+            std_flipped = flipped_pool.tile([N, PACK, P], F32)
+            nc.scalar.activation(out=std_flipped[:], in_=flipped[:, 0], func=ACT.Exp, scale=0.5)
+            mean_flipped = flipped_pool.tile([N, PACK, P], BF16)
+            nc.scalar.copy(out=mean_flipped[:], in_=flipped[:, 1])
+            return std_flipped, mean_flipped
+
+        def operands_in_psum(std_flipped, mean_flipped):
+            std_ps = psum_w.tile([P, PACK, N], F32)
+            mean_ps = psum_w.tile([P, PACK, N], BF16)
+            for j in range(PACK):
+                nc.tensor.transpose(std_ps[:, j, :], std_flipped[:, j, :], ident_f32[:])
+                nc.tensor.transpose(mean_ps[:, j, :], mean_flipped[:, j, :], ident_bf[:])
+            return std_ps[:].rearrange("p j n -> p n j"), mean_ps[:].rearrange("p j n -> p n j")
+
+        def sample_weights(engine, prod, first, count, we_raw, operands, w_bf):
+            std, mean = operands
+            shape = [P, count, N, PACK]
+            engine.tensor_tensor(
+                out=prod[:],
+                in0=we_raw[:, first : first + count].rearrange("p s j n -> p s n j"),
+                in1=std.unsqueeze(1).to_broadcast(shape),
+                op=ALU.mult,
+            )
+            engine.tensor_tensor(
+                out=w_bf[:, first : first + count],
+                in0=prod[:],
+                in1=mean.unsqueeze(1).to_broadcast(shape),
+                op=ALU.add,
+            )
+
+        def gpsimd_share(c, operands):
+            w_bf = grouped.tile([P, S, N, PACK], BF16, align_bytes=64)
+            prod_g = prod_pool.tile([P, S_GPSIMD, N, PACK], F32)
+            sample_weights(nc.gpsimd, prod_g, S_VECTOR, S_GPSIMD, we_tiles[c], operands, w_bf)
+            return w_bf
+
+        def vector_share(c, operands, w_bf):
+            prod_v = prod_pool.tile([P, S_VECTOR, N, PACK], F32)
+            sample_weights(nc.vector, prod_v, 0, S_VECTOR, we_tiles[c], operands, w_bf)
+
+        def flip_h(h_raw):
+            h_bf = grouped.tile([P, S, B, PACK], BF16, align_bytes=64)
+            h_words = h_bf[:].bitcast(F32)
+            raw_words = h_raw[:].bitcast(F32)
+            for pair in range(S // PAIR):
+                h_t = psum_t.tile([P, PAIR, 2, B], F32, tag="t")
+                for i in range(PAIR):
+                    for u in range(2):
+                        nc.tensor.transpose(
+                            h_t[:, i, u, :], raw_words[:, pair * PAIR + i, u : K_PASS // 2 : 2], ident_f32[:]
+                        )
+                nc.scalar.copy(
+                    out=h_words[:, pair * PAIR : (pair + 1) * PAIR], in_=h_t[:].rearrange("p i u b -> p i b u")
                 )
-                halves.append(h_raw)
-            return halves
+            return h_bf
 
-        shared_next = load_shared(0)
-        we_ahead = [load_we(0), load_we(1)]
-        h_next = load_h(0)
+        def quantise(values, kind):
+            codes = quantised.tile([P, S, P], U32, align_bytes=64, tag=kind + "_codes")
+            scales = quantised.tile([P, S, P], U8, align_bytes=64, tag=kind + "_scales")
+            nc.vector.quantize_mx(
+                out=codes[:].rearrange("p s m -> p (s m)").bitcast(FP8X4),
+                scales=scales[:].rearrange("p s m -> p (s m)"),
+                in_=values[:].rearrange("p s m j -> p (s m j)"),
+            )
+            return codes, scales
 
-        be_all = consts.tile([P, S, N], BF16)
-        nc.sync.dma_start(
-            out=be_all[:].rearrange("p s n -> p (s n)"),
-            in_=be1.rearrange("s o n -> (s o n)").partition_broadcast(P),
-        )
-        bv_all = consts.tile([P, N], BF16)
-        nc.sync.dma_start(out=bv_all[:], in_=bv1.partition_broadcast(P))
-        bm_all = consts.tile([P, N], BF16)
-        nc.sync.dma_start(out=bm_all[:], in_=bm1.partition_broadcast(P))
-        b_std = consts.tile([P, N], F32)
-        nc.scalar.activation(out=b_std[:], in_=bv_all[:], func=ACT.Exp, scale=0.5)
-        sums = consts.tile([P, S, N], F32)
-        nc.gpsimd.tensor_tensor(
-            out=sums[:], in0=be_all[:], in1=b_std[:].unsqueeze(1).to_broadcast([P, S, N]), op=ALU.mult
-        )
-        nc.gpsimd.tensor_tensor(
-            out=sums[:], in0=sums[:], in1=bm_all[:].unsqueeze(1).to_broadcast([P, S, N]), op=ALU.add
-        )
-
-        for g in range(GROUPS):
-            wv_raw, wm_raw = shared_next
-            h_halves = h_next
-
-            w_std = shared.tile([P, GROUP, N, PACK], F32)
-            w_mean = shared.tile([P, GROUP, N, PACK], BF16)
-            for cc in range(GROUP):
-                nc.scalar.activation(
-                    out=w_std[:, cc], in_=wv_raw[:, cc].rearrange("p j n -> p n j"), func=ACT.Exp, scale=0.5
-                )
-                nc.scalar.copy(out=w_mean[:, cc], in_=wm_raw[:, cc].rearrange("p j n -> p n j"))
-
-            if g + 1 < GROUPS:
-                shared_next = load_shared(g + 1)
-
-            codes = []
-            for cc in range(GROUP):
-                c = g * GROUP + cc
-                we_raw = we_ahead[c]
-                if c + 2 < PASSES:
-                    we_ahead.append(load_we(c + 2))
-
-                prod = prod_pool.tile([P, S, N, PACK], F32)
-                nc.vector.tensor_tensor(
-                    out=prod[:],
-                    in0=we_raw[:].rearrange("p s j n -> p s n j"),
-                    in1=w_std[:, cc].unsqueeze(1).to_broadcast([P, S, N, PACK]),
-                    op=ALU.mult,
-                )
-                w_bf = grouped.tile([P, S, N, PACK], BF16, align_bytes=64)
-                nc.vector.tensor_tensor(
-                    out=w_bf[:],
-                    in0=prod[:],
-                    in1=w_mean[:, cc].unsqueeze(1).to_broadcast([P, S, N, PACK]),
-                    op=ALU.add,
-                )
-                w_codes = quantised.tile([P, S, N], U32, align_bytes=64)
-                w_scales = quantised.tile([P, S, N], U8, align_bytes=64)
-                nc.vector.quantize_mx(
-                    out=w_codes[:].rearrange("p s n -> p (s n)").bitcast(FP8X4),
-                    scales=w_scales[:].rearrange("p s n -> p (s n)"),
-                    in_=w_bf[:].rearrange("p s n j -> p (s n j)"),
-                )
-
-                h_bf = grouped.tile([P, S, B, PACK], BF16, align_bytes=64)
-                h_words = h_bf[:].bitcast(F32)
-                for pair in range(S // PAIR):
-                    h_t = psum_t.tile([P, PAIR, 2, B], F32)
-                    for i in range(PAIR):
-                        s = pair * PAIR + i
-                        raw_words = h_halves[s // HALF][:].bitcast(F32)
-                        first = cc * (K_PASS // 2)
-                        for u in range(2):
-                            nc.tensor.transpose(
-                                h_t[:, i, u, :],
-                                raw_words[:, s % HALF, first + u : first + K_PASS // 2 : 2],
-                                ident[:],
-                            )
-                    nc.scalar.copy(
-                        out=h_words[:, pair * PAIR : (pair + 1) * PAIR],
-                        in_=h_t[:].rearrange("p i u b -> p i b u"),
-                    )
-                if cc == GROUP - 1 and g + 1 < GROUPS:
-                    h_next = load_h(g + 1)
-                h_codes = quantised.tile([P, S, B], U32, align_bytes=64)
-                h_scales = quantised.tile([P, S, B], U8, align_bytes=64)
-                nc.vector.quantize_mx(
-                    out=h_codes[:].rearrange("p s b -> p (s b)").bitcast(FP8X4),
-                    scales=h_scales[:].rearrange("p s b -> p (s b)"),
-                    in_=h_bf[:].rearrange("p s b j -> p (s b j)"),
-                )
-                codes.append((h_codes, h_scales, w_codes, w_scales))
-
+        def multiply_group(operand_list):
+            banks = []
             for half in range(2):
                 acc = psum_acc.tile([B, HALF, N], F32)
                 for i in range(HALF):
                     s = half * HALF + i
                     for cc in range(GROUP):
-                        h_codes, h_scales, w_codes, w_scales = codes[cc]
+                        (h_codes, h_scales), (w_codes, w_scales) = operand_list[cc]
                         nc.tensor.matmul_mx(
                             out=acc[:, i, :],
                             lhsT=h_codes[:, s, :].bitcast(FP8X4),
@@ -184,11 +167,80 @@ def tile_bnn_pb_k_kernel(tc, h0, wm1, wv1, bm1, bv1, we1, be1, out):
                             start=(cc == 0),
                             stop=(cc == GROUP - 1),
                         )
-                these = sums[:, half * HALF : (half + 1) * HALF, :]
-                nc.vector.tensor_tensor(out=these, in0=acc[:], in1=these, op=ALU.add)
+                banks.append(acc)
+            return banks
 
-        result = consts.tile([B, S, N], F32)
+        def add_to_sums(banks):
+            for half in range(2):
+                part = sums[:, half * HALF : (half + 1) * HALF, :]
+                nc.vector.tensor_tensor(out=part, in0=banks[half][:], in1=part, op=ALU.add)
+
+        ident_bf = consts.tile([P, P], BF16)
+        make_identity(nc, ident_bf[:])
+        ident_f32 = consts.tile([P, P], F32)
+        make_identity(nc, ident_f32[:])
+
+        shared_tiles = {0: load_shared(0)}
+        we_tiles = {0: load_we(0)}
+        h_tiles = {0: load_h(0)}
+        be_all = consts.tile([P, S, N], BF16)
+        nc.sync.dma_start(
+            out=be_all[:].rearrange("p s n -> p (s n)"),
+            in_=be1.rearrange("s o n -> (s o n)").partition_broadcast(P),
+        )
+        bv_all = consts.tile([P, N], BF16)
+        nc.sync.dma_start(out=bv_all[:], in_=bv1.partition_broadcast(P))
+        bm_all = consts.tile([P, N], BF16)
+        nc.sync.dma_start(out=bm_all[:], in_=bm1.partition_broadcast(P))
+        we_tiles[1] = load_we(1)
+        h_tiles[1] = load_h(1)
+        we_tiles[2] = load_we(2)
+
+        std_flipped, mean_flipped = flip_shared(0)
+        for_vector = {0: operands_in_psum(std_flipped, mean_flipped)}
+        w_tiles = {0: gpsimd_share(0, operands_in_sbuf(0))}
+        h_flipped = {0: flip_h(h_tiles[0])}
+        w_tiles[1] = gpsimd_share(1, operands_in_sbuf(1))
+
+        b_std = consts.tile([P, N], F32)
+        nc.scalar.activation(out=b_std[:], in_=bv_all[:], func=ACT.Exp, scale=0.5)
+        sums = consts.tile([B, S, N], F32)
+        nc.gpsimd.tensor_tensor(
+            out=sums[:], in0=be_all[:], in1=b_std[:].unsqueeze(1).to_broadcast([P, S, N]), op=ALU.mult
+        )
+        nc.gpsimd.tensor_tensor(
+            out=sums[:], in0=sums[:], in1=bm_all[:].unsqueeze(1).to_broadcast([P, S, N]), op=ALU.add
+        )
+
+        group_operands = []
+        finished_banks = []
+        for c in range(PASSES):
+            if c % GROUP == 0 and c // GROUP + 1 < GROUPS:
+                shared_tiles[c // GROUP + 1] = load_shared(c // GROUP + 1)
+            if c + 3 < PASSES:
+                we_tiles[c + 3] = load_we(c + 3)
+            if c + 2 < PASSES:
+                h_tiles[c + 2] = load_h(c + 2)
+                for_gpsimd = operands_in_sbuf(c + 2)
+            if c + 1 < PASSES:
+                std_flipped, mean_flipped = flip_shared(c + 1)
+                h_flipped[c + 1] = flip_h(h_tiles[c + 1])
+                for_vector[c + 1] = operands_in_psum(std_flipped, mean_flipped)
+
+            vector_share(c, for_vector[c], w_tiles[c])
+            if finished_banks:
+                add_to_sums(finished_banks)
+                finished_banks = []
+            group_operands.append((quantise(h_flipped[c], "h"), quantise(w_tiles[c], "w")))
+
+            if c + 2 < PASSES:
+                w_tiles[c + 2] = gpsimd_share(c + 2, for_gpsimd)
+            if c % GROUP == GROUP - 1:
+                finished_banks = multiply_group(group_operands)
+                group_operands = []
+
+        add_to_sums(finished_banks)
         for half in range(2):
-            these = slice(half * HALF, (half + 1) * HALF)
-            nc.scalar.activation(out=result[:, these, :], in_=sums[:, these, :], func=ACT.Relu)
-            nc.sync.dma_start(out=out.rearrange("s b n -> b s n")[:, these, :], in_=result[:, these, :])
+            part = sums[:, half * HALF : (half + 1) * HALF, :]
+            nc.scalar.activation(out=part, in_=part, func=ACT.Relu)
+            nc.sync.dma_start(out=out.rearrange("s b n -> b s n")[:, half * HALF : (half + 1) * HALF, :], in_=part)

@@ -22,7 +22,7 @@ GROUP = 4
 GROUPS = PASSES // GROUP
 HALF = S // 2
 PAIR = 2
-S_VECTOR = 6
+S_VECTOR = 5
 S_GPSIMD = S - S_VECTOR
 
 FLOPS = 2 * S * B * K * N

@@ -19,11 +19,10 @@ PACK = 4
 K_PASS = P * PACK
 PASSES = K // K_PASS
 GROUP = 4
-GROUPS = PASSES // GROUP
 HALF = S // 2
 PAIR = 2
-S_VECTOR = 5
-S_GPSIMD = S - S_VECTOR
+N_VECTOR = 88
+N_GPSIMD = N - N_VECTOR
 
 FLOPS = 2 * S * B * K * N
 
@@ -31,18 +30,16 @@ FLOPS = 2 * S * B * K * N
 def tile_bnn_pb_k_kernel(tc, h0, wm1, wv1, bm1, bv1, we1, be1, out):
     nc = tc.nc
 
-    wv_rows = wv1.rearrange("(g c p j) n -> g p c j n", c=GROUP, p=P, j=PACK)
-    wm_rows = wm1.rearrange("(g c p j) n -> g p c j n", c=GROUP, p=P, j=PACK)
+    wv_rows = wv1.rearrange("(c p j) n -> c p j n", p=P, j=PACK)
+    wm_rows = wm1.rearrange("(c p j) n -> c p j n", p=P, j=PACK)
     we_rows = we1.rearrange("s (c p j) n -> c p s j n", p=P, j=PACK)
     h_cols = h0.rearrange("s b (c k) -> c b s k", k=K_PASS)
 
     with (
         tc.tile_pool(name="consts", bufs=1) as consts,
-        tc.tile_pool(name="shared_raw", bufs=2) as shared_raw,
+        tc.tile_pool(name="raw", bufs=4) as raw,
         tc.tile_pool(name="flipped_pool", bufs=2) as flipped_pool,
         tc.tile_pool(name="gpsimd_pool", bufs=2) as gpsimd_pool,
-        tc.tile_pool(name="we_pool", bufs=4) as we_pool,
-        tc.tile_pool(name="h_pool", bufs=3) as h_pool,
         tc.tile_pool(name="prod_pool", bufs=1) as prod_pool,
         tc.tile_pool(name="grouped", bufs=2) as grouped,
         tc.tile_pool(name="quantised", bufs=GROUP + 1) as quantised,
@@ -51,39 +48,39 @@ def tile_bnn_pb_k_kernel(tc, h0, wm1, wv1, bm1, bv1, we1, be1, out):
         tc.psum_pool(name="psum_acc", bufs=2) as psum_acc,
         tc.manual_schedule(),
     ):
-        def load_shared(g):
-            wv_raw = shared_raw.tile([P, GROUP, PACK, N], BF16)
-            nc.sync.dma_start(out=wv_raw[:], in_=wv_rows[g])
-            wm_raw = shared_raw.tile([P, GROUP, PACK, N], BF16)
-            nc.sync.dma_start(out=wm_raw[:], in_=wm_rows[g])
-            return wv_raw, wm_raw
-
-        def load_we(c):
-            we_raw = we_pool.tile([P, S, PACK, N], BF16)
+        def load_weights(c):
+            wv_raw = raw.tile([P, PACK, N], BF16)
+            nc.sync.dma_start(out=wv_raw[:], in_=wv_rows[c])
+            wm_raw = raw.tile([P, PACK, N], BF16)
+            nc.sync.dma_start(out=wm_raw[:], in_=wm_rows[c])
+            we_raw = raw.tile([P, S, PACK, N], BF16)
             nc.sync.dma_start(out=we_raw[:], in_=we_rows[c])
-            return we_raw
+            return wv_raw, wm_raw, we_raw
 
         def load_h(c):
-            h_raw = h_pool.tile([B, S, K_PASS], BF16)
+            h_raw = raw.tile([B, S, K_PASS], BF16)
             nc.sync.dma_start(out=h_raw[:], in_=h_cols[c])
             return h_raw
 
         def operands_in_sbuf(c):
-            wv_raw, wm_raw = shared_tiles[c // GROUP]
-            std_sb = gpsimd_pool.tile([P, N, PACK], F32)
+            wv_raw, wm_raw, we_raw = weights[c]
+            std_sb = gpsimd_pool.tile([P, 2, N_GPSIMD, 2], F32)
             nc.scalar.activation(
-                out=std_sb[:], in_=wv_raw[:, c % GROUP].rearrange("p j n -> p n j"), func=ACT.Exp, scale=0.5
+                out=std_sb[:],
+                in_=wv_raw[:, :, N_VECTOR:N].rearrange("p (h i) n -> p h n i", h=2),
+                func=ACT.Exp,
+                scale=0.5,
             )
-            mean_sb = gpsimd_pool.tile([P, N, PACK], BF16)
-            nc.scalar.copy(out=mean_sb[:], in_=wm_raw[:, c % GROUP].rearrange("p j n -> p n j"))
+            mean_sb = gpsimd_pool.tile([P, N_GPSIMD, 2, 2], BF16)
+            nc.scalar.copy(out=mean_sb[:], in_=wm_raw[:, :, N_VECTOR:N].rearrange("p (h i) n -> p n h i", h=2))
             return std_sb[:], mean_sb[:]
 
         def flip_shared(c):
-            wv_raw, wm_raw = shared_tiles[c // GROUP]
+            wv_raw, wm_raw, we_raw = weights[c]
             flipped = psum_t.tile([N, 2, PACK, P], BF16, tag="t")
             for j in range(PACK):
-                nc.tensor.transpose(flipped[:, 0, j, :], wv_raw[:, c % GROUP, j, :], ident_bf[:])
-                nc.tensor.transpose(flipped[:, 1, j, :], wm_raw[:, c % GROUP, j, :], ident_bf[:])
+                nc.tensor.transpose(flipped[:, 0, j, :], wv_raw[:, j, :], ident_bf[:])
+                nc.tensor.transpose(flipped[:, 1, j, :], wm_raw[:, j, :], ident_bf[:])
             std_flipped = flipped_pool.tile([N, PACK, P], F32)
             nc.scalar.activation(out=std_flipped[:], in_=flipped[:, 0], func=ACT.Exp, scale=0.5)
             mean_flipped = flipped_pool.tile([N, PACK, P], BF16)
@@ -96,33 +93,36 @@ def tile_bnn_pb_k_kernel(tc, h0, wm1, wv1, bm1, bv1, we1, be1, out):
             for j in range(PACK):
                 nc.tensor.transpose(std_ps[:, j, :], std_flipped[:, j, :], ident_f32[:])
                 nc.tensor.transpose(mean_ps[:, j, :], mean_flipped[:, j, :], ident_bf[:])
-            return std_ps[:].rearrange("p j n -> p n j"), mean_ps[:].rearrange("p j n -> p n j")
+            return (
+                std_ps[:, :, 0:N_VECTOR].rearrange("p (h i) n -> p h n i", h=2),
+                mean_ps[:, :, 0:N_VECTOR].rearrange("p (h i) n -> p n h i", h=2),
+            )
 
         def sample_weights(engine, prod, first, count, we_raw, operands, w_bf):
             std, mean = operands
-            shape = [P, count, N, PACK]
+            for h in range(2):
+                engine.tensor_tensor(
+                    out=prod[:, h],
+                    in0=we_raw[:, :, 2 * h : 2 * h + 2, first : first + count].rearrange("p s i n -> p s n i"),
+                    in1=std[:, h].unsqueeze(1).to_broadcast([P, S, count, 2]),
+                    op=ALU.mult,
+                )
             engine.tensor_tensor(
-                out=prod[:],
-                in0=we_raw[:, first : first + count].rearrange("p s j n -> p s n j"),
-                in1=std.unsqueeze(1).to_broadcast(shape),
-                op=ALU.mult,
-            )
-            engine.tensor_tensor(
-                out=w_bf[:, first : first + count],
-                in0=prod[:],
-                in1=mean.unsqueeze(1).to_broadcast(shape),
+                out=w_bf[:, :, first : first + count, :].rearrange("p s n (h i) -> p s n h i", h=2),
+                in0=prod[:].rearrange("p h s n i -> p s n h i"),
+                in1=mean.unsqueeze(1).to_broadcast([P, S, count, 2, 2]),
                 op=ALU.add,
             )
 
         def gpsimd_share(c, operands):
             w_bf = grouped.tile([P, S, N, PACK], BF16, align_bytes=64)
-            prod_g = prod_pool.tile([P, S_GPSIMD, N, PACK], F32)
-            sample_weights(nc.gpsimd, prod_g, S_VECTOR, S_GPSIMD, we_tiles[c], operands, w_bf)
+            prod_g = prod_pool.tile([P, 2, S, N_GPSIMD, 2], F32)
+            sample_weights(nc.gpsimd, prod_g, N_VECTOR, N_GPSIMD, weights[c][2], operands, w_bf)
             return w_bf
 
         def vector_share(c, operands, w_bf):
-            prod_v = prod_pool.tile([P, S_VECTOR, N, PACK], F32)
-            sample_weights(nc.vector, prod_v, 0, S_VECTOR, we_tiles[c], operands, w_bf)
+            prod_v = prod_pool.tile([P, 2, S, N_VECTOR, 2], F32)
+            sample_weights(nc.vector, prod_v, 0, N_VECTOR, weights[c][2], operands, w_bf)
 
         def flip_h(h_raw):
             h_bf = grouped.tile([P, S, B, PACK], BF16, align_bytes=64)
@@ -156,16 +156,15 @@ def tile_bnn_pb_k_kernel(tc, h0, wm1, wv1, bm1, bv1, we1, be1, out):
                 acc = psum_acc.tile([B, HALF, N], F32)
                 for i in range(HALF):
                     s = half * HALF + i
-                    for cc in range(GROUP):
-                        (h_codes, h_scales), (w_codes, w_scales) = operand_list[cc]
+                    for index, ((h_codes, h_scales), (w_codes, w_scales)) in enumerate(operand_list):
                         nc.tensor.matmul_mx(
                             out=acc[:, i, :],
                             lhsT=h_codes[:, s, :].bitcast(FP8X4),
                             lhsT_scale=h_scales[:, s, :],
                             rhs=w_codes[:, s, :].bitcast(FP8X4),
                             rhs_scale=w_scales[:, s, :],
-                            start=(cc == 0),
-                            stop=(cc == GROUP - 1),
+                            start=(index == 0),
+                            stop=(index == len(operand_list) - 1),
                         )
                 banks.append(acc)
             return banks
@@ -180,8 +179,7 @@ def tile_bnn_pb_k_kernel(tc, h0, wm1, wv1, bm1, bv1, we1, be1, out):
         ident_f32 = consts.tile([P, P], F32)
         make_identity(nc, ident_f32[:])
 
-        shared_tiles = {0: load_shared(0)}
-        we_tiles = {0: load_we(0)}
+        weights = {0: load_weights(0)}
         h_tiles = {0: load_h(0)}
         be_all = consts.tile([P, S, N], BF16)
         nc.sync.dma_start(
@@ -192,9 +190,9 @@ def tile_bnn_pb_k_kernel(tc, h0, wm1, wv1, bm1, bv1, we1, be1, out):
         nc.sync.dma_start(out=bv_all[:], in_=bv1.partition_broadcast(P))
         bm_all = consts.tile([P, N], BF16)
         nc.sync.dma_start(out=bm_all[:], in_=bm1.partition_broadcast(P))
-        we_tiles[1] = load_we(1)
+        weights[1] = load_weights(1)
         h_tiles[1] = load_h(1)
-        we_tiles[2] = load_we(2)
+        weights[2] = load_weights(2)
 
         std_flipped, mean_flipped = flip_shared(0)
         for_vector = {0: operands_in_psum(std_flipped, mean_flipped)}
@@ -215,10 +213,8 @@ def tile_bnn_pb_k_kernel(tc, h0, wm1, wv1, bm1, bv1, we1, be1, out):
         group_operands = []
         finished_banks = []
         for c in range(PASSES):
-            if c % GROUP == 0 and c // GROUP + 1 < GROUPS:
-                shared_tiles[c // GROUP + 1] = load_shared(c // GROUP + 1)
             if c + 3 < PASSES:
-                we_tiles[c + 3] = load_we(c + 3)
+                weights[c + 3] = load_weights(c + 3)
             if c + 2 < PASSES:
                 h_tiles[c + 2] = load_h(c + 2)
                 for_gpsimd = operands_in_sbuf(c + 2)
@@ -235,7 +231,7 @@ def tile_bnn_pb_k_kernel(tc, h0, wm1, wv1, bm1, bv1, we1, be1, out):
 
             if c + 2 < PASSES:
                 w_tiles[c + 2] = gpsimd_share(c + 2, for_gpsimd)
-            if c % GROUP == GROUP - 1:
+            if c % GROUP == GROUP - 2 or c == PASSES - 1:
                 finished_banks = multiply_group(group_operands)
                 group_operands = []
 

@@ -21,7 +21,7 @@ PASSES = K // K_PASS
 GROUP = 4
 HALF = S // 2
 PAIR = 2
-N_VECTOR = 88
+N_VECTOR = 92
 N_GPSIMD = N - N_VECTOR
 
 FLOPS = 2 * S * B * K * N
@@ -40,7 +40,8 @@ def tile_bnn_pb_k_kernel(tc, h0, wm1, wv1, bm1, bv1, we1, be1, out):
         tc.tile_pool(name="raw", bufs=4) as raw,
         tc.tile_pool(name="flipped_pool", bufs=2) as flipped_pool,
         tc.tile_pool(name="gpsimd_pool", bufs=2) as gpsimd_pool,
-        tc.tile_pool(name="prod_pool", bufs=1) as prod_pool,
+        tc.tile_pool(name="prod_v_pool", bufs=2) as prod_v_pool,
+        tc.tile_pool(name="prod_g_pool", bufs=1) as prod_g_pool,
         tc.tile_pool(name="grouped", bufs=2) as grouped,
         tc.tile_pool(name="quantised", bufs=GROUP + 1) as quantised,
         tc.psum_pool(name="psum_t", bufs=2) as psum_t,
@@ -98,8 +99,7 @@ def tile_bnn_pb_k_kernel(tc, h0, wm1, wv1, bm1, bv1, we1, be1, out):
                 mean_ps[:, :, 0:N_VECTOR].rearrange("p (h i) n -> p n h i", h=2),
             )
 
-        def sample_weights(engine, prod, first, count, we_raw, operands, w_bf):
-            std, mean = operands
+        def multiply(engine, prod, first, count, we_raw, std):
             for h in range(2):
                 engine.tensor_tensor(
                     out=prod[:, h],
@@ -107,6 +107,8 @@ def tile_bnn_pb_k_kernel(tc, h0, wm1, wv1, bm1, bv1, we1, be1, out):
                     in1=std[:, h].unsqueeze(1).to_broadcast([P, S, count, 2]),
                     op=ALU.mult,
                 )
+
+        def add_mean(engine, prod, first, count, mean, w_bf):
             engine.tensor_tensor(
                 out=w_bf[:, :, first : first + count, :].rearrange("p s n (h i) -> p s n h i", h=2),
                 in0=prod[:].rearrange("p h s n i -> p s n h i"),
@@ -115,14 +117,25 @@ def tile_bnn_pb_k_kernel(tc, h0, wm1, wv1, bm1, bv1, we1, be1, out):
             )
 
         def gpsimd_share(c, operands):
+            std, mean = operands
             w_bf = grouped.tile([P, S, N, PACK], BF16, align_bytes=64)
-            prod_g = prod_pool.tile([P, 2, S, N_GPSIMD, 2], F32)
-            sample_weights(nc.gpsimd, prod_g, N_VECTOR, N_GPSIMD, weights[c][2], operands, w_bf)
+            prod_g = prod_g_pool.tile([P, 2, S, N_GPSIMD, 2], F32)
+            multiply(nc.gpsimd, prod_g, N_VECTOR, N_GPSIMD, weights[c][2], std)
+            add_mean(nc.gpsimd, prod_g, N_VECTOR, N_GPSIMD, mean, w_bf)
             return w_bf
 
-        def vector_share(c, operands, w_bf):
-            prod_v = prod_pool.tile([P, 2, S, N_VECTOR, 2], F32)
-            sample_weights(nc.vector, prod_v, 0, N_VECTOR, weights[c][2], operands, w_bf)
+        def vector_multiply(c):
+            prod_v = prod_v_pool.tile([P, 2, S, N_VECTOR, 2], F32)
+            multiply(nc.vector, prod_v, 0, N_VECTOR, weights[c][2], for_vector[c][0])
+            return prod_v
+
+        def vector_add(c, prod_v):
+            add_mean(nc.vector, prod_v, 0, N_VECTOR, for_vector[c][1], w_tiles[c])
+
+        def prepare(c):
+            std_flipped, mean_flipped = flip_shared(c)
+            for_vector[c] = operands_in_psum(std_flipped, mean_flipped)
+            h_flipped[c] = flip_h(h_tiles[c])
 
         def flip_h(h_raw):
             h_bf = grouped.tile([P, S, B, PACK], BF16, align_bytes=64)
@@ -153,7 +166,7 @@ def tile_bnn_pb_k_kernel(tc, h0, wm1, wv1, bm1, bv1, we1, be1, out):
         def multiply_group(operand_list):
             banks = []
             for half in range(2):
-                acc = psum_acc.tile([B, HALF, N], F32)
+                acc = psum_acc.tile([B, HALF, N], F32, tag="acc")
                 for i in range(HALF):
                     s = half * HALF + i
                     for index, ((h_codes, h_scales), (w_codes, w_scales)) in enumerate(operand_list):
@@ -178,56 +191,70 @@ def tile_bnn_pb_k_kernel(tc, h0, wm1, wv1, bm1, bv1, we1, be1, out):
         make_identity(nc, ident_bf[:])
         ident_f32 = consts.tile([P, P], F32)
         make_identity(nc, ident_f32[:])
+        bias_rows = consts.tile([P, P], BF16)
+        nc.vector.memset(bias_rows[:], 0.0)
 
         weights = {0: load_weights(0)}
         h_tiles = {0: load_h(0)}
-        be_all = consts.tile([P, S, N], BF16)
-        nc.sync.dma_start(
-            out=be_all[:].rearrange("p s n -> p (s n)"),
-            in_=be1.rearrange("s o n -> (s o n)").partition_broadcast(P),
-        )
-        bv_all = consts.tile([P, N], BF16)
-        nc.sync.dma_start(out=bv_all[:], in_=bv1.partition_broadcast(P))
-        bm_all = consts.tile([P, N], BF16)
-        nc.sync.dma_start(out=bm_all[:], in_=bm1.partition_broadcast(P))
-        weights[1] = load_weights(1)
-        h_tiles[1] = load_h(1)
-        weights[2] = load_weights(2)
+        nc.sync.dma_start(out=bias_rows[0:S, :], in_=be1.rearrange("s o n -> (s o) n"))
+        nc.sync.dma_start(out=bias_rows[S : S + 1, :], in_=bv1.unsqueeze(0))
+        nc.sync.dma_start(out=bias_rows[S + 1 : S + 2, :], in_=bm1.unsqueeze(0))
+        for c in range(1, 3):
+            weights[c] = load_weights(c)
+            h_tiles[c] = load_h(c)
 
-        std_flipped, mean_flipped = flip_shared(0)
-        for_vector = {0: operands_in_psum(std_flipped, mean_flipped)}
-        w_tiles = {0: gpsimd_share(0, operands_in_sbuf(0))}
-        h_flipped = {0: flip_h(h_tiles[0])}
-        w_tiles[1] = gpsimd_share(1, operands_in_sbuf(1))
+        for_vector = {}
+        h_flipped = {}
+        w_tiles = {}
+        for c in range(2):
+            for_gpsimd = operands_in_sbuf(c)
+            prepare(c)
+            w_tiles[c] = gpsimd_share(c, for_gpsimd)
+        products = {0: vector_multiply(0)}
+        h_quantised = {0: quantise(h_flipped[0], "h")}
 
-        b_std = consts.tile([P, N], F32)
-        nc.scalar.activation(out=b_std[:], in_=bv_all[:], func=ACT.Exp, scale=0.5)
+        bias_cols = psum_t.tile([N, P], BF16, tag="t")
+        nc.tensor.transpose(bias_cols[:], bias_rows[:], ident_bf[:])
+        b_std = consts.tile([N, 1], F32)
+        nc.scalar.activation(out=b_std[:], in_=bias_cols[:, S : S + 1], func=ACT.Exp, scale=0.5)
+        b_mean = consts.tile([N, 1], F32)
+        nc.scalar.copy(out=b_mean[:], in_=bias_cols[:, S + 1 : S + 2])
+        b1_cols = consts.tile([N, S], F32)
+        nc.scalar.activation(out=b1_cols[:], in_=bias_cols[:, 0:S], func=ACT.Identity, scale=b_std[:], bias=b_mean[:])
         sums = consts.tile([B, S, N], F32)
-        nc.gpsimd.tensor_tensor(
-            out=sums[:], in0=be_all[:], in1=b_std[:].unsqueeze(1).to_broadcast([P, S, N]), op=ALU.mult
-        )
-        nc.gpsimd.tensor_tensor(
-            out=sums[:], in0=sums[:], in1=bm_all[:].unsqueeze(1).to_broadcast([P, S, N]), op=ALU.add
-        )
+        for half in range(2):
+            b1_all = psum_acc.tile([B, HALF, N], F32, tag="acc")
+            for i in range(HALF):
+                s = half * HALF + i
+                nc.tensor.matmul(
+                    out=b1_all[:, i, :],
+                    lhsT=b1_cols[:, s : s + 1].to_broadcast([N, B]),
+                    rhs=ident_f32[:],
+                    start=True,
+                    stop=True,
+                )
+            nc.scalar.copy(out=sums[:, half * HALF : (half + 1) * HALF, :], in_=b1_all[:])
 
         group_operands = []
         finished_banks = []
         for c in range(PASSES):
             if c + 3 < PASSES:
                 weights[c + 3] = load_weights(c + 3)
+                h_tiles[c + 3] = load_h(c + 3)
             if c + 2 < PASSES:
-                h_tiles[c + 2] = load_h(c + 2)
                 for_gpsimd = operands_in_sbuf(c + 2)
-            if c + 1 < PASSES:
-                std_flipped, mean_flipped = flip_shared(c + 1)
-                h_flipped[c + 1] = flip_h(h_tiles[c + 1])
-                for_vector[c + 1] = operands_in_psum(std_flipped, mean_flipped)
 
-            vector_share(c, for_vector[c], w_tiles[c])
+            vector_add(c, products[c])
+            if c + 2 < PASSES:
+                prepare(c + 2)
+            if c + 1 < PASSES:
+                products[c + 1] = vector_multiply(c + 1)
             if finished_banks:
                 add_to_sums(finished_banks)
                 finished_banks = []
-            group_operands.append((quantise(h_flipped[c], "h"), quantise(w_tiles[c], "w")))
+            group_operands.append((h_quantised[c], quantise(w_tiles[c], "w")))
+            if c + 1 < PASSES:
+                h_quantised[c + 1] = quantise(h_flipped[c + 1], "h")
 
             if c + 2 < PASSES:
                 w_tiles[c + 2] = gpsimd_share(c + 2, for_gpsimd)

@@ -21,7 +21,7 @@ PASSES = K // K_PASS
 GROUP = 4
 HALF = S // 2
 PAIR = 2
-N_VECTOR = 92
+N_VECTOR = 88
 N_GPSIMD = N - N_VECTOR
 
 FLOPS = 2 * S * B * K * N
@@ -65,16 +65,15 @@ def tile_bnn_pb_k_kernel(tc, h0, wm1, wv1, bm1, bv1, we1, be1, out):
 
         def operands_in_sbuf(c):
             wv_raw, wm_raw, we_raw = weights[c]
-            std_sb = gpsimd_pool.tile([P, 2, N_GPSIMD, 2], F32)
+            std_sb = gpsimd_pool.tile([P, N_GPSIMD, PACK], F32)
             nc.scalar.activation(
-                out=std_sb[:],
-                in_=wv_raw[:, :, N_VECTOR:N].rearrange("p (h i) n -> p h n i", h=2),
-                func=ACT.Exp,
-                scale=0.5,
+                out=std_sb[:], in_=wv_raw[:, :, N_VECTOR:N].rearrange("p j n -> p n j"), func=ACT.Exp, scale=0.5
             )
-            mean_sb = gpsimd_pool.tile([P, N_GPSIMD, 2, 2], BF16)
-            nc.scalar.copy(out=mean_sb[:], in_=wm_raw[:, :, N_VECTOR:N].rearrange("p (h i) n -> p n h i", h=2))
-            return std_sb[:], mean_sb[:]
+            mean_sb = gpsimd_pool.tile([P, N_GPSIMD, PACK], BF16)
+            nc.scalar.copy(out=mean_sb[:], in_=wm_raw[:, :, N_VECTOR:N].rearrange("p j n -> p n j"))
+            noise_sb = gpsimd_pool.tile([P, S, N_GPSIMD, PACK], BF16)
+            nc.scalar.copy(out=noise_sb[:], in_=we_raw[:, :, :, N_VECTOR:N].rearrange("p s j n -> p s n j"))
+            return std_sb, mean_sb, noise_sb
 
         def flip_shared(c):
             wv_raw, wm_raw, we_raw = weights[c]
@@ -117,11 +116,19 @@ def tile_bnn_pb_k_kernel(tc, h0, wm1, wv1, bm1, bv1, we1, be1, out):
             )
 
         def gpsimd_share(c, operands):
-            std, mean = operands
+            std_sb, mean_sb, noise_sb = operands
             w_bf = grouped.tile([P, S, N, PACK], BF16, align_bytes=64)
-            prod_g = prod_g_pool.tile([P, 2, S, N_GPSIMD, 2], F32)
-            multiply(nc.gpsimd, prod_g, N_VECTOR, N_GPSIMD, weights[c][2], std)
-            add_mean(nc.gpsimd, prod_g, N_VECTOR, N_GPSIMD, mean, w_bf)
+            prod_g = prod_g_pool.tile([P, S, N_GPSIMD, PACK], F32)
+            shape = [P, S, N_GPSIMD, PACK]
+            nc.gpsimd.tensor_tensor(
+                out=prod_g[:], in0=noise_sb[:], in1=std_sb[:].unsqueeze(1).to_broadcast(shape), op=ALU.mult
+            )
+            nc.gpsimd.tensor_tensor(
+                out=w_bf[:, :, N_VECTOR:N, :],
+                in0=prod_g[:],
+                in1=mean_sb[:].unsqueeze(1).to_broadcast(shape),
+                op=ALU.add,
+            )
             return w_bf
 
         def vector_multiply(c):

@@ -18,9 +18,11 @@ P = 128
 PACK = 4
 K_PASS = P * PACK
 PASSES = K // K_PASS
-GROUP = 4
-HALF = S // 2
+HALF = 4
 PAIR = 2
+STEPS = (S // HALF) * PASSES
+BIAS_STEP = PASSES - 6
+AHEAD = 5
 N_VECTOR = 88
 N_GPSIMD = N - N_VECTOR
 
@@ -34,135 +36,157 @@ def tile_bnn_pb_k_kernel(tc, h0, wm1, wv1, bm1, bv1, we1, be1, out):
     wm_rows = wm1.rearrange("(c p j) n -> c p j n", p=P, j=PACK)
     we_rows = we1.rearrange("s (c p j) n -> c p s j n", p=P, j=PACK)
     h_cols = h0.rearrange("s b (c k) -> c b s k", k=K_PASS)
+    out_rows = out.rearrange("s b n -> b s n")
 
     with (
         tc.tile_pool(name="consts", bufs=1) as consts,
-        tc.tile_pool(name="raw", bufs=4) as raw,
-        tc.tile_pool(name="flipped_pool", bufs=2) as flipped_pool,
-        tc.tile_pool(name="gpsimd_pool", bufs=2) as gpsimd_pool,
+        tc.tile_pool(name="kept", bufs=PASSES) as kept,
+        tc.tile_pool(name="raw", bufs=AHEAD + 1) as raw,
+        tc.tile_pool(name="noise_pool", bufs=3) as noise_pool,
         tc.tile_pool(name="prod_v_pool", bufs=2) as prod_v_pool,
         tc.tile_pool(name="prod_g_pool", bufs=1) as prod_g_pool,
         tc.tile_pool(name="grouped", bufs=2) as grouped,
-        tc.tile_pool(name="quantised", bufs=GROUP + 1) as quantised,
+        tc.tile_pool(name="quantised", bufs=4) as quantised,
         tc.psum_pool(name="psum_t", bufs=2) as psum_t,
-        tc.psum_pool(name="psum_w", bufs=2) as psum_w,
-        tc.psum_pool(name="psum_acc", bufs=2) as psum_acc,
+        tc.psum_pool(name="psum_w", bufs=1) as psum_w,
+        tc.psum_pool(name="psum_acc", bufs=1) as psum_acc,
         tc.manual_schedule(),
     ):
-        def load_weights(c):
-            wv_raw = raw.tile([P, PACK, N], BF16)
-            nc.sync.dma_start(out=wv_raw[:], in_=wv_rows[c])
-            wm_raw = raw.tile([P, PACK, N], BF16)
-            nc.sync.dma_start(out=wm_raw[:], in_=wm_rows[c])
-            we_raw = raw.tile([P, S, PACK, N], BF16)
-            nc.sync.dma_start(out=we_raw[:], in_=we_rows[c])
-            return wv_raw, wm_raw, we_raw
+        raws = {}
+        shared_sb = {}
+        shared_flipped = {}
+        noise = {}
+        std_in_psum = {}
+        mean_in_psum = {}
+        h_flipped = {}
+        w_tiles = {}
+        products_v = {}
+        products_g = {}
+        h_quantised = {}
+        w_quantised = {}
+        banks = {}
 
-        def load_h(c):
-            h_raw = raw.tile([B, S, K_PASS], BF16)
-            nc.sync.dma_start(out=h_raw[:], in_=h_cols[c])
-            return h_raw
+        def samples(i):
+            first = (i // PASSES) * HALF
+            return slice(first, first + HALF)
 
-        def operands_in_sbuf(c):
-            wv_raw, wm_raw, we_raw = weights[c]
-            std_sb = gpsimd_pool.tile([P, N_GPSIMD, PACK], F32)
-            nc.scalar.activation(
-                out=std_sb[:], in_=wv_raw[:, :, N_VECTOR:N].rearrange("p j n -> p n j"), func=ACT.Exp, scale=0.5
-            )
-            mean_sb = gpsimd_pool.tile([P, N_GPSIMD, PACK], BF16)
-            nc.scalar.copy(out=mean_sb[:], in_=wm_raw[:, :, N_VECTOR:N].rearrange("p j n -> p n j"))
-            noise_sb = gpsimd_pool.tile([P, S, N_GPSIMD, PACK], BF16)
+        def load(i):
+            c = i % PASSES
+            if i < PASSES:
+                wv_raw = raw.tile([P, PACK, N], BF16)
+                nc.sync.dma_start(out=wv_raw[:], in_=wv_rows[c])
+                wm_raw = raw.tile([P, PACK, N], BF16)
+                nc.sync.dma_start(out=wm_raw[:], in_=wm_rows[c])
+            else:
+                wv_raw = wm_raw = None
+            we_raw = raw.tile([P, HALF, PACK, N], BF16)
+            nc.sync.dma_start(out=we_raw[:], in_=we_rows[c][:, samples(i)])
+            h_raw = raw.tile([B, HALF, K_PASS], BF16)
+            nc.sync.dma_start(out=h_raw[:], in_=h_cols[c][:, samples(i)])
+            raws[i] = wv_raw, wm_raw, we_raw, h_raw
+
+        def operands_in_sbuf(i):
+            wv_raw, wm_raw, we_raw, h_raw = raws[i]
+            if i < PASSES:
+                std_sb = kept.tile([P, N_GPSIMD, PACK], F32)
+                nc.scalar.activation(
+                    out=std_sb[:], in_=wv_raw[:, :, N_VECTOR:N].rearrange("p j n -> p n j"), func=ACT.Exp, scale=0.5
+                )
+                mean_sb = kept.tile([P, N_GPSIMD, PACK], BF16)
+                nc.scalar.copy(out=mean_sb[:], in_=wm_raw[:, :, N_VECTOR:N].rearrange("p j n -> p n j"))
+                shared_sb[i] = std_sb, mean_sb
+            noise_sb = noise_pool.tile([P, HALF, N_GPSIMD, PACK], BF16)
             nc.scalar.copy(out=noise_sb[:], in_=we_raw[:, :, :, N_VECTOR:N].rearrange("p s j n -> p s n j"))
-            return std_sb, mean_sb, noise_sb
+            noise[i] = noise_sb
 
-        def flip_shared(c):
-            wv_raw, wm_raw, we_raw = weights[c]
+        def flip_shared(i):
+            wv_raw, wm_raw, we_raw, h_raw = raws[i]
             flipped = psum_t.tile([N, 2, PACK, P], BF16, tag="t")
             for j in range(PACK):
                 nc.tensor.transpose(flipped[:, 0, j, :], wv_raw[:, j, :], ident_bf[:])
+            for j in range(PACK):
                 nc.tensor.transpose(flipped[:, 1, j, :], wm_raw[:, j, :], ident_bf[:])
-            std_flipped = flipped_pool.tile([N, PACK, P], F32)
+            std_flipped = kept.tile([N, PACK, P], F32)
             nc.scalar.activation(out=std_flipped[:], in_=flipped[:, 0], func=ACT.Exp, scale=0.5)
-            mean_flipped = flipped_pool.tile([N, PACK, P], BF16)
+            mean_flipped = kept.tile([N, PACK, P], BF16)
             nc.scalar.copy(out=mean_flipped[:], in_=flipped[:, 1])
-            return std_flipped, mean_flipped
+            shared_flipped[i] = std_flipped, mean_flipped
 
-        def operands_in_psum(std_flipped, mean_flipped):
+        def std_to_psum(i):
+            std_flipped, mean_flipped = shared_flipped[i % PASSES]
             std_ps = psum_w.tile([P, PACK, N], F32)
-            mean_ps = psum_w.tile([P, PACK, N], BF16)
             for j in range(PACK):
                 nc.tensor.transpose(std_ps[:, j, :], std_flipped[:, j, :], ident_f32[:])
-                nc.tensor.transpose(mean_ps[:, j, :], mean_flipped[:, j, :], ident_bf[:])
-            return (
-                std_ps[:, :, 0:N_VECTOR].rearrange("p (h i) n -> p h n i", h=2),
-                mean_ps[:, :, 0:N_VECTOR].rearrange("p (h i) n -> p n h i", h=2),
-            )
+            std_in_psum[i] = std_ps[:, :, 0:N_VECTOR].rearrange("p (h i) n -> p h n i", h=2)
 
-        def multiply(engine, prod, first, count, we_raw, std):
+        def mean_to_psum(i):
+            std_flipped, mean_flipped = shared_flipped[i % PASSES]
+            mean_ps = psum_w.tile([P, PACK, N], BF16)
+            for j in range(PACK):
+                nc.tensor.transpose(mean_ps[:, j, :], mean_flipped[:, j, :], ident_bf[:])
+            mean_in_psum[i] = mean_ps[:, :, 0:N_VECTOR].rearrange("p (h i) n -> p n h i", h=2)
+
+        def vector_multiply(i):
+            we_raw = raws[i][2]
+            prod_v = prod_v_pool.tile([P, 2, HALF, N_VECTOR, 2], F32)
             for h in range(2):
-                engine.tensor_tensor(
-                    out=prod[:, h],
-                    in0=we_raw[:, :, 2 * h : 2 * h + 2, first : first + count].rearrange("p s i n -> p s n i"),
-                    in1=std[:, h].unsqueeze(1).to_broadcast([P, S, count, 2]),
+                nc.vector.tensor_tensor(
+                    out=prod_v[:, h],
+                    in0=we_raw[:, :, 2 * h : 2 * h + 2, 0:N_VECTOR].rearrange("p s i n -> p s n i"),
+                    in1=std_in_psum[i][:, h].unsqueeze(1).to_broadcast([P, HALF, N_VECTOR, 2]),
                     op=ALU.mult,
                 )
+            products_v[i] = prod_v
 
-        def add_mean(engine, prod, first, count, mean, w_bf):
-            engine.tensor_tensor(
-                out=w_bf[:, :, first : first + count, :].rearrange("p s n (h i) -> p s n h i", h=2),
-                in0=prod[:].rearrange("p h s n i -> p s n h i"),
-                in1=mean.unsqueeze(1).to_broadcast([P, S, count, 2, 2]),
+        def vector_add(i):
+            nc.vector.tensor_tensor(
+                out=w_tiles[i][:, :, 0:N_VECTOR, :].rearrange("p s n (h i) -> p s n h i", h=2),
+                in0=products_v[i][:].rearrange("p h s n i -> p s n h i"),
+                in1=mean_in_psum[i].unsqueeze(1).to_broadcast([P, HALF, N_VECTOR, 2, 2]),
                 op=ALU.add,
             )
 
-        def gpsimd_share(c, operands):
-            std_sb, mean_sb, noise_sb = operands
-            w_bf = grouped.tile([P, S, N, PACK], BF16, align_bytes=64)
-            prod_g = prod_g_pool.tile([P, S, N_GPSIMD, PACK], F32)
-            shape = [P, S, N_GPSIMD, PACK]
+        def gpsimd_multiply(i):
+            std_sb, mean_sb = shared_sb[i % PASSES]
+            prod_g = prod_g_pool.tile([P, HALF, N_GPSIMD, PACK], F32)
             nc.gpsimd.tensor_tensor(
-                out=prod_g[:], in0=noise_sb[:], in1=std_sb[:].unsqueeze(1).to_broadcast(shape), op=ALU.mult
+                out=prod_g[:],
+                in0=noise[i][:],
+                in1=std_sb[:].unsqueeze(1).to_broadcast([P, HALF, N_GPSIMD, PACK]),
+                op=ALU.mult,
             )
+            products_g[i] = prod_g
+
+        def gpsimd_add(i):
+            std_sb, mean_sb = shared_sb[i % PASSES]
+            w_bf = grouped.tile([P, HALF, N, PACK], BF16, align_bytes=64)
             nc.gpsimd.tensor_tensor(
                 out=w_bf[:, :, N_VECTOR:N, :],
-                in0=prod_g[:],
-                in1=mean_sb[:].unsqueeze(1).to_broadcast(shape),
+                in0=products_g[i][:],
+                in1=mean_sb[:].unsqueeze(1).to_broadcast([P, HALF, N_GPSIMD, PACK]),
                 op=ALU.add,
             )
-            return w_bf
+            w_tiles[i] = w_bf
 
-        def vector_multiply(c):
-            prod_v = prod_v_pool.tile([P, 2, S, N_VECTOR, 2], F32)
-            multiply(nc.vector, prod_v, 0, N_VECTOR, weights[c][2], for_vector[c][0])
-            return prod_v
-
-        def vector_add(c, prod_v):
-            add_mean(nc.vector, prod_v, 0, N_VECTOR, for_vector[c][1], w_tiles[c])
-
-        def prepare(c):
-            std_flipped, mean_flipped = flip_shared(c)
-            for_vector[c] = operands_in_psum(std_flipped, mean_flipped)
-            h_flipped[c] = flip_h(h_tiles[c])
-
-        def flip_h(h_raw):
-            h_bf = grouped.tile([P, S, B, PACK], BF16, align_bytes=64)
+        def flip_h(i):
+            h_bf = grouped.tile([P, HALF, B, PACK], BF16, align_bytes=64)
             h_words = h_bf[:].bitcast(F32)
-            raw_words = h_raw[:].bitcast(F32)
-            for pair in range(S // PAIR):
+            raw_words = raws[i][3][:].bitcast(F32)
+            for pair in range(HALF // PAIR):
                 h_t = psum_t.tile([P, PAIR, 2, B], F32, tag="t")
-                for i in range(PAIR):
+                for m in range(PAIR):
                     for u in range(2):
                         nc.tensor.transpose(
-                            h_t[:, i, u, :], raw_words[:, pair * PAIR + i, u : K_PASS // 2 : 2], ident_f32[:]
+                            h_t[:, m, u, :], raw_words[:, pair * PAIR + m, u : K_PASS // 2 : 2], ident_f32[:]
                         )
                 nc.scalar.copy(
-                    out=h_words[:, pair * PAIR : (pair + 1) * PAIR], in_=h_t[:].rearrange("p i u b -> p i b u")
+                    out=h_words[:, pair * PAIR : (pair + 1) * PAIR], in_=h_t[:].rearrange("p m u b -> p m b u")
                 )
-            return h_bf
+            h_flipped[i] = h_bf
 
         def quantise(values, kind):
-            codes = quantised.tile([P, S, P], U32, align_bytes=64, tag=kind + "_codes")
-            scales = quantised.tile([P, S, P], U8, align_bytes=64, tag=kind + "_scales")
+            codes = quantised.tile([P, HALF, P], U32, align_bytes=64, tag=kind + "_codes")
+            scales = quantised.tile([P, HALF, P], U8, align_bytes=64, tag=kind + "_scales")
             nc.vector.quantize_mx(
                 out=codes[:].rearrange("p s m -> p (s m)").bitcast(FP8X4),
                 scales=scales[:].rearrange("p s m -> p (s m)"),
@@ -170,29 +194,56 @@ def tile_bnn_pb_k_kernel(tc, h0, wm1, wv1, bm1, bv1, we1, be1, out):
             )
             return codes, scales
 
-        def multiply_group(operand_list):
-            banks = []
-            for half in range(2):
-                acc = psum_acc.tile([B, HALF, N], F32, tag="acc")
-                for i in range(HALF):
-                    s = half * HALF + i
-                    for index, ((h_codes, h_scales), (w_codes, w_scales)) in enumerate(operand_list):
-                        nc.tensor.matmul_mx(
-                            out=acc[:, i, :],
-                            lhsT=h_codes[:, s, :].bitcast(FP8X4),
-                            lhsT_scale=h_scales[:, s, :],
-                            rhs=w_codes[:, s, :].bitcast(FP8X4),
-                            rhs_scale=w_scales[:, s, :],
-                            start=(index == 0),
-                            stop=(index == len(operand_list) - 1),
-                        )
-                banks.append(acc)
-            return banks
+        def matmuls(i):
+            c = i % PASSES
+            h_codes, h_scales = h_quantised[i]
+            w_codes, w_scales = w_quantised[i]
+            for s in range(HALF):
+                if c == 0:
+                    banks[s] = psum_acc.tile([B, N], F32, tag="acc%d" % s, name="acc%d" % s)
+                nc.tensor.matmul_mx(
+                    out=banks[s][:],
+                    lhsT=h_codes[:, s, :].bitcast(FP8X4),
+                    lhsT_scale=h_scales[:, s, :],
+                    rhs=w_codes[:, s, :].bitcast(FP8X4),
+                    rhs_scale=w_scales[:, s, :],
+                    start=(c == 0),
+                    stop=(c == PASSES - 1),
+                )
 
-        def add_to_sums(banks):
-            for half in range(2):
-                part = sums[:, half * HALF : (half + 1) * HALF, :]
-                nc.vector.tensor_tensor(out=part, in0=banks[half][:], in1=part, op=ALU.add)
+        def finish_half(half):
+            first = half * HALF
+            result = consts.tile([B, HALF, N], F32, name="result%d" % half)
+            for s in range(HALF):
+                nc.vector.tensor_tensor(out=result[:, s, :], in0=banks[s][:], in1=b1_all[:, first + s, :], op=ALU.add)
+            for pair in range(HALF // PAIR):
+                part = result[:, pair * PAIR : (pair + 1) * PAIR, :]
+                nc.vector.tensor_scalar_max(part, part, 0.0)
+                nc.sync.dma_start(out=out_rows[:, first + pair * PAIR : first + (pair + 1) * PAIR, :], in_=part)
+
+        def make_bias_columns():
+            bias_cols = psum_t.tile([N, P], BF16, tag="t")
+            nc.tensor.transpose(bias_cols[:], bias_rows[:], ident_bf[:])
+            b_std = consts.tile([N, 1], F32)
+            nc.scalar.activation(out=b_std[:], in_=bias_cols[:, S : S + 1], func=ACT.Exp, scale=0.5)
+            b_mean = consts.tile([N, 1], F32)
+            nc.scalar.copy(out=b_mean[:], in_=bias_cols[:, S + 1 : S + 2])
+            nc.scalar.activation(
+                out=b1_cols[:], in_=bias_cols[:, 0:S], func=ACT.Identity, scale=b_std[:], bias=b_mean[:]
+            )
+
+        def spread_bias(half):
+            b1_ps = psum_t.tile([B, HALF, N], F32, tag="t")
+            for m in range(HALF):
+                s = half * HALF + m
+                nc.tensor.matmul(
+                    out=b1_ps[:, m, :],
+                    lhsT=b1_cols[:, s : s + 1].to_broadcast([N, B]),
+                    rhs=ident_f32[:],
+                    start=True,
+                    stop=True,
+                )
+            nc.scalar.copy(out=b1_all[:, half * HALF : (half + 1) * HALF, :], in_=b1_ps[:])
 
         ident_bf = consts.tile([P, P], BF16)
         make_identity(nc, ident_bf[:])
@@ -200,77 +251,70 @@ def tile_bnn_pb_k_kernel(tc, h0, wm1, wv1, bm1, bv1, we1, be1, out):
         make_identity(nc, ident_f32[:])
         bias_rows = consts.tile([P, P], BF16)
         nc.vector.memset(bias_rows[:], 0.0)
+        b1_cols = consts.tile([N, S], F32)
+        b1_all = consts.tile([B, S, N], F32)
+        warm = consts.tile([P, 1], F32)
+        nc.vector.memset(warm[:], 0.0)
+        nc.scalar.activation(out=warm[:], in_=warm[:], func=ACT.Exp)
 
-        weights = {0: load_weights(0)}
-        h_tiles = {0: load_h(0)}
+        load(0)
+        load(1)
         nc.sync.dma_start(out=bias_rows[0:S, :], in_=be1.rearrange("s o n -> (s o) n"))
         nc.sync.dma_start(out=bias_rows[S : S + 1, :], in_=bv1.unsqueeze(0))
         nc.sync.dma_start(out=bias_rows[S + 1 : S + 2, :], in_=bm1.unsqueeze(0))
-        for c in range(1, 3):
-            weights[c] = load_weights(c)
-            h_tiles[c] = load_h(c)
+        for i in range(2, AHEAD):
+            load(i)
 
-        for_vector = {}
-        h_flipped = {}
-        w_tiles = {}
-        for c in range(2):
-            for_gpsimd = operands_in_sbuf(c)
-            prepare(c)
-            w_tiles[c] = gpsimd_share(c, for_gpsimd)
-        products = {0: vector_multiply(0)}
-        h_quantised = {0: quantise(h_flipped[0], "h")}
+        flip_shared(0)
+        std_to_psum(0)
+        mean_to_psum(0)
+        operands_in_sbuf(0)
+        flip_h(0)
+        gpsimd_multiply(0)
+        gpsimd_add(0)
+        vector_multiply(0)
+        h_quantised[0] = quantise(h_flipped[0], "h")
+        operands_in_sbuf(1)
+        flip_shared(1)
+        flip_h(1)
+        std_to_psum(1)
+        gpsimd_multiply(1)
+        gpsimd_add(1)
+        operands_in_sbuf(2)
+        gpsimd_multiply(2)
 
-        bias_cols = psum_t.tile([N, P], BF16, tag="t")
-        nc.tensor.transpose(bias_cols[:], bias_rows[:], ident_bf[:])
-        b_std = consts.tile([N, 1], F32)
-        nc.scalar.activation(out=b_std[:], in_=bias_cols[:, S : S + 1], func=ACT.Exp, scale=0.5)
-        b_mean = consts.tile([N, 1], F32)
-        nc.scalar.copy(out=b_mean[:], in_=bias_cols[:, S + 1 : S + 2])
-        b1_cols = consts.tile([N, S], F32)
-        nc.scalar.activation(out=b1_cols[:], in_=bias_cols[:, 0:S], func=ACT.Identity, scale=b_std[:], bias=b_mean[:])
-        sums = consts.tile([B, S, N], F32)
-        for half in range(2):
-            b1_all = psum_acc.tile([B, HALF, N], F32, tag="acc")
-            for i in range(HALF):
-                s = half * HALF + i
-                nc.tensor.matmul(
-                    out=b1_all[:, i, :],
-                    lhsT=b1_cols[:, s : s + 1].to_broadcast([N, B]),
-                    rhs=ident_f32[:],
-                    start=True,
-                    stop=True,
-                )
-            nc.scalar.copy(out=sums[:, half * HALF : (half + 1) * HALF, :], in_=b1_all[:])
+        for i in range(STEPS):
+            if i + AHEAD < STEPS:
+                load(i + AHEAD)
+            if i > 0:
+                matmuls(i - 1)
+            if i + 3 < STEPS:
+                operands_in_sbuf(i + 3)
+            if i + 2 < STEPS:
+                if i + 2 < PASSES:
+                    flip_shared(i + 2)
 
-        group_operands = []
-        finished_banks = []
-        for c in range(PASSES):
-            if c + 3 < PASSES:
-                weights[c + 3] = load_weights(c + 3)
-                h_tiles[c + 3] = load_h(c + 3)
-            if c + 2 < PASSES:
-                for_gpsimd = operands_in_sbuf(c + 2)
+            vector_add(i)
+            if i + 1 < STEPS:
+                mean_to_psum(i + 1)
+                vector_multiply(i + 1)
+            if i + 2 < STEPS:
+                flip_h(i + 2)
+                std_to_psum(i + 2)
+            if i == PASSES:
+                finish_half(0)
+            w_quantised[i] = quantise(w_tiles[i], "w")
+            if i + 1 < STEPS:
+                h_quantised[i + 1] = quantise(h_flipped[i + 1], "h")
 
-            vector_add(c, products[c])
-            if c + 2 < PASSES:
-                prepare(c + 2)
-            if c + 1 < PASSES:
-                products[c + 1] = vector_multiply(c + 1)
-            if finished_banks:
-                add_to_sums(finished_banks)
-                finished_banks = []
-            group_operands.append((h_quantised[c], quantise(w_tiles[c], "w")))
-            if c + 1 < PASSES:
-                h_quantised[c + 1] = quantise(h_flipped[c + 1], "h")
+            if i + 2 < STEPS:
+                gpsimd_add(i + 2)
+            if i + 3 < STEPS:
+                gpsimd_multiply(i + 3)
+            if i == BIAS_STEP:
+                make_bias_columns()
+            if i in (BIAS_STEP + 1, BIAS_STEP + 2):
+                spread_bias(i - BIAS_STEP - 1)
 
-            if c + 2 < PASSES:
-                w_tiles[c + 2] = gpsimd_share(c + 2, for_gpsimd)
-            if c % GROUP == GROUP - 2 or c == PASSES - 1:
-                finished_banks = multiply_group(group_operands)
-                group_operands = []
-
-        add_to_sums(finished_banks)
-        for half in range(2):
-            part = sums[:, half * HALF : (half + 1) * HALF, :]
-            nc.scalar.activation(out=part, in_=part, func=ACT.Relu)
-            nc.sync.dma_start(out=out.rearrange("s b n -> b s n")[:, half * HALF : (half + 1) * HALF, :], in_=part)
+        matmuls(STEPS - 1)
+        finish_half(1)

@@ -20,9 +20,10 @@ K_PASS = P * PACK
 PASSES = K // K_PASS
 HALF = 4
 PAIR = 2
-STEPS = (S // HALF) * PASSES
-BIAS_STEP = PASSES - 6
-AHEAD = 5
+UNITS = (S // HALF) * PASSES
+WINDOWS = UNITS // 2
+HALF_WINDOWS = PASSES // 2
+BIAS_WINDOW = HALF_WINDOWS - 4
 N_VECTOR = 88
 N_GPSIMD = N - N_VECTOR
 
@@ -35,24 +36,26 @@ def tile_bnn_pb_k_kernel(tc, h0, wm1, wv1, bm1, bv1, we1, be1, out):
     wv_rows = wv1.rearrange("(c p j) n -> c p j n", p=P, j=PACK)
     wm_rows = wm1.rearrange("(c p j) n -> c p j n", p=P, j=PACK)
     we_rows = we1.rearrange("s (c p j) n -> c p s j n", p=P, j=PACK)
-    h_cols = h0.rearrange("s b (c k) -> c b s k", k=K_PASS)
     out_rows = out.rearrange("s b n -> b s n")
 
     with (
         tc.tile_pool(name="consts", bufs=1) as consts,
         tc.tile_pool(name="kept", bufs=PASSES) as kept,
-        tc.tile_pool(name="raw", bufs=AHEAD + 1) as raw,
-        tc.tile_pool(name="noise_pool", bufs=3) as noise_pool,
-        tc.tile_pool(name="prod_v_pool", bufs=2) as prod_v_pool,
+        tc.tile_pool(name="kept_sb", bufs=HALF_WINDOWS) as kept_sb,
+        tc.tile_pool(name="raw", bufs=3) as raw,
+        tc.tile_pool(name="noise_pool", bufs=2) as noise_pool,
+        tc.tile_pool(name="prod_v_pool", bufs=3) as prod_v_pool,
         tc.tile_pool(name="prod_g_pool", bufs=1) as prod_g_pool,
-        tc.tile_pool(name="grouped", bufs=2) as grouped,
-        tc.tile_pool(name="quantised", bufs=4) as quantised,
+        tc.tile_pool(name="w_pool", bufs=2) as w_pool,
+        tc.tile_pool(name="h_pool", bufs=2) as h_pool,
+        tc.tile_pool(name="quantised", bufs=2) as quantised,
         tc.psum_pool(name="psum_t", bufs=2) as psum_t,
         tc.psum_pool(name="psum_w", bufs=1) as psum_w,
         tc.psum_pool(name="psum_acc", bufs=1) as psum_acc,
         tc.manual_schedule(),
     ):
         raws = {}
+        h_raws = {}
         shared_sb = {}
         shared_flipped = {}
         noise = {}
@@ -66,150 +69,174 @@ def tile_bnn_pb_k_kernel(tc, h0, wm1, wv1, bm1, bv1, we1, be1, out):
         w_quantised = {}
         banks = {}
 
-        def samples(i):
-            first = (i // PASSES) * HALF
+        def samples(m):
+            first = (m // HALF_WINDOWS) * HALF
             return slice(first, first + HALF)
 
-        def load(i):
-            c = i % PASSES
-            if i < PASSES:
-                wv_raw = raw.tile([P, PACK, N], BF16)
-                nc.sync.dma_start(out=wv_raw[:], in_=wv_rows[c])
-                wm_raw = raw.tile([P, PACK, N], BF16)
-                nc.sync.dma_start(out=wm_raw[:], in_=wm_rows[c])
-            else:
-                wv_raw = wm_raw = None
-            we_raw = raw.tile([P, HALF, PACK, N], BF16)
-            nc.sync.dma_start(out=we_raw[:], in_=we_rows[c][:, samples(i)])
-            h_raw = raw.tile([B, HALF, K_PASS], BF16)
-            nc.sync.dma_start(out=h_raw[:], in_=h_cols[c][:, samples(i)])
-            raws[i] = wv_raw, wm_raw, we_raw, h_raw
+        def load_weights(m):
+            wv_raw = raw.tile([P, 2, PACK, N], BF16)
+            wm_raw = raw.tile([P, 2, PACK, N], BF16)
+            we_raw = raw.tile([P, 2, HALF, PACK, N], BF16)
+            for q in range(2):
+                c = (2 * m + q) % PASSES
+                if m < HALF_WINDOWS:
+                    nc.sync.dma_start(out=wv_raw[:, q], in_=wv_rows[c])
+                nc.sync.dma_start(out=we_raw[:, q], in_=we_rows[c][:, samples(m)])
+                if m < HALF_WINDOWS:
+                    nc.sync.dma_start(out=wm_raw[:, q], in_=wm_rows[c])
+            raws[m] = wv_raw, wm_raw, we_raw
 
-        def operands_in_sbuf(i):
-            wv_raw, wm_raw, we_raw, h_raw = raws[i]
-            if i < PASSES:
-                std_sb = kept.tile([P, N_GPSIMD, PACK], F32)
+        def load_h(m):
+            c = (2 * m) % PASSES
+            h_raw = raw.tile([B, HALF, 2, K_PASS], BF16)
+            nc.sync.dma_start(
+                out=h_raw[:].rearrange("b s q k -> b s (q k)"),
+                in_=h0.rearrange("s b k -> b s k")[:, samples(m), c * K_PASS : (c + 2) * K_PASS],
+            )
+            h_raws[m] = h_raw
+
+        def shared_in_sbuf(m):
+            wv_raw, wm_raw, we_raw = raws[m]
+            if m < HALF_WINDOWS:
+                std_sb = kept_sb.tile([P, 2, N_GPSIMD, PACK], F32)
                 nc.scalar.activation(
-                    out=std_sb[:], in_=wv_raw[:, :, N_VECTOR:N].rearrange("p j n -> p n j"), func=ACT.Exp, scale=0.5
+                    out=std_sb[:], in_=wv_raw[:, :, :, N_VECTOR:N].rearrange("p q j n -> p q n j"), func=ACT.Exp, scale=0.5
                 )
-                mean_sb = kept.tile([P, N_GPSIMD, PACK], BF16)
-                nc.scalar.copy(out=mean_sb[:], in_=wm_raw[:, :, N_VECTOR:N].rearrange("p j n -> p n j"))
-                shared_sb[i] = std_sb, mean_sb
-            noise_sb = noise_pool.tile([P, HALF, N_GPSIMD, PACK], BF16)
-            nc.scalar.copy(out=noise_sb[:], in_=we_raw[:, :, :, N_VECTOR:N].rearrange("p s j n -> p s n j"))
-            noise[i] = noise_sb
+                mean_sb = kept_sb.tile([P, 2, N_GPSIMD, PACK], BF16)
+                nc.scalar.copy(out=mean_sb[:], in_=wm_raw[:, :, :, N_VECTOR:N].rearrange("p q j n -> p q n j"))
+                shared_sb[m] = std_sb, mean_sb
 
-        def flip_shared(i):
-            wv_raw, wm_raw, we_raw, h_raw = raws[i]
+        def noise_in_sbuf(m):
+            wv_raw, wm_raw, we_raw = raws[m]
+            noise_sb = noise_pool.tile([P, 2, HALF, N_GPSIMD, PACK], BF16)
+            nc.scalar.copy(
+                out=noise_sb[:].rearrange("p q s n j -> p (q s) n j"),
+                in_=we_raw[:, :, :, :, N_VECTOR:N].rearrange("p q s j n -> p (q s) n j"),
+            )
+            noise[m] = noise_sb
+
+        def flip_shared(u):
+            wv_raw, wm_raw, we_raw = raws[u // 2]
             flipped = psum_t.tile([N, 2, PACK, P], BF16, tag="t")
             for j in range(PACK):
-                nc.tensor.transpose(flipped[:, 0, j, :], wv_raw[:, j, :], ident_bf[:])
+                nc.tensor.transpose(flipped[:, 0, j, :], wv_raw[:, u % 2, j, :], ident_bf[:])
             for j in range(PACK):
-                nc.tensor.transpose(flipped[:, 1, j, :], wm_raw[:, j, :], ident_bf[:])
+                nc.tensor.transpose(flipped[:, 1, j, :], wm_raw[:, u % 2, j, :], ident_bf[:])
             std_flipped = kept.tile([N, PACK, P], F32)
             nc.scalar.activation(out=std_flipped[:], in_=flipped[:, 0], func=ACT.Exp, scale=0.5)
             mean_flipped = kept.tile([N, PACK, P], BF16)
             nc.scalar.copy(out=mean_flipped[:], in_=flipped[:, 1])
-            shared_flipped[i] = std_flipped, mean_flipped
+            shared_flipped[u] = std_flipped, mean_flipped
 
-        def std_to_psum(i):
-            std_flipped, mean_flipped = shared_flipped[i % PASSES]
+        def std_to_psum(u):
+            std_flipped, mean_flipped = shared_flipped[u % PASSES]
             std_ps = psum_w.tile([P, PACK, N], F32)
             for j in range(PACK):
                 nc.tensor.transpose(std_ps[:, j, :], std_flipped[:, j, :], ident_f32[:])
-            std_in_psum[i] = std_ps[:, :, 0:N_VECTOR].rearrange("p (h i) n -> p h n i", h=2)
+            std_in_psum[u] = std_ps[:, :, 0 : columns(u)].rearrange("p (h i) n -> p h n i", h=2)
 
-        def mean_to_psum(i):
-            std_flipped, mean_flipped = shared_flipped[i % PASSES]
+        def mean_to_psum(u):
+            std_flipped, mean_flipped = shared_flipped[u % PASSES]
             mean_ps = psum_w.tile([P, PACK, N], BF16)
             for j in range(PACK):
                 nc.tensor.transpose(mean_ps[:, j, :], mean_flipped[:, j, :], ident_bf[:])
-            mean_in_psum[i] = mean_ps[:, :, 0:N_VECTOR].rearrange("p (h i) n -> p n h i", h=2)
+            mean_in_psum[u] = mean_ps[:, :, 0 : columns(u)].rearrange("p (h i) n -> p n h i", h=2)
 
-        def vector_multiply(i):
-            we_raw = raws[i][2]
-            prod_v = prod_v_pool.tile([P, 2, HALF, N_VECTOR, 2], F32)
+        def columns(u):
+            return N if u < 2 else N_VECTOR
+
+        def vector_multiply(u):
+            count = columns(u)
+            we_raw = raws[u // 2][2]
+            prod_v = prod_v_pool.tile([P, 2, HALF, count, 2], F32)
             for h in range(2):
                 nc.vector.tensor_tensor(
                     out=prod_v[:, h],
-                    in0=we_raw[:, :, 2 * h : 2 * h + 2, 0:N_VECTOR].rearrange("p s i n -> p s n i"),
-                    in1=std_in_psum[i][:, h].unsqueeze(1).to_broadcast([P, HALF, N_VECTOR, 2]),
+                    in0=we_raw[:, u % 2, :, 2 * h : 2 * h + 2, 0:count].rearrange("p s i n -> p s n i"),
+                    in1=std_in_psum[u][:, h].unsqueeze(1).to_broadcast([P, HALF, count, 2]),
                     op=ALU.mult,
                 )
-            products_v[i] = prod_v
+            products_v[u] = prod_v
 
-        def vector_add(i):
+        def vector_add(u):
+            count = columns(u)
             nc.vector.tensor_tensor(
-                out=w_tiles[i][:, :, 0:N_VECTOR, :].rearrange("p s n (h i) -> p s n h i", h=2),
-                in0=products_v[i][:].rearrange("p h s n i -> p s n h i"),
-                in1=mean_in_psum[i].unsqueeze(1).to_broadcast([P, HALF, N_VECTOR, 2, 2]),
+                out=w_tile(u // 2)[:, u % 2, :, 0:count, :].rearrange("p s n (h i) -> p s n h i", h=2),
+                in0=products_v[u][:].rearrange("p h s n i -> p s n h i"),
+                in1=mean_in_psum[u].unsqueeze(1).to_broadcast([P, HALF, count, 2, 2]),
                 op=ALU.add,
             )
 
-        def gpsimd_multiply(i):
-            std_sb, mean_sb = shared_sb[i % PASSES]
-            prod_g = prod_g_pool.tile([P, HALF, N_GPSIMD, PACK], F32)
+        def w_tile(m):
+            if m not in w_tiles:
+                w_tiles[m] = w_pool.tile([P, 2, HALF, N, PACK], BF16, align_bytes=64, name="w_bf")
+            return w_tiles[m]
+
+        def for_gpsimd(shared):
+            flat = shared[:].rearrange("p q n j -> p q (n j)")
+            return flat.unsqueeze(2).to_broadcast([P, 2, HALF, N_GPSIMD * PACK])
+
+        def gpsimd_multiply(m):
+            prod_g = prod_g_pool.tile([P, 2, HALF, N_GPSIMD * PACK], F32)
             nc.gpsimd.tensor_tensor(
                 out=prod_g[:],
-                in0=noise[i][:],
-                in1=std_sb[:].unsqueeze(1).to_broadcast([P, HALF, N_GPSIMD, PACK]),
+                in0=noise[m][:].rearrange("p q s n j -> p q s (n j)"),
+                in1=for_gpsimd(shared_sb[m % HALF_WINDOWS][0]),
                 op=ALU.mult,
             )
-            products_g[i] = prod_g
+            products_g[m] = prod_g
 
-        def gpsimd_add(i):
-            std_sb, mean_sb = shared_sb[i % PASSES]
-            w_bf = grouped.tile([P, HALF, N, PACK], BF16, align_bytes=64)
+        def gpsimd_add(m):
             nc.gpsimd.tensor_tensor(
-                out=w_bf[:, :, N_VECTOR:N, :],
-                in0=products_g[i][:],
-                in1=mean_sb[:].unsqueeze(1).to_broadcast([P, HALF, N_GPSIMD, PACK]),
+                out=w_tile(m)[:, :, :, N_VECTOR:N, :].rearrange("p q s n j -> p q s (n j)"),
+                in0=products_g[m][:],
+                in1=for_gpsimd(shared_sb[m % HALF_WINDOWS][1]),
                 op=ALU.add,
             )
-            w_tiles[i] = w_bf
 
-        def flip_h(i):
-            h_bf = grouped.tile([P, HALF, B, PACK], BF16, align_bytes=64)
-            h_words = h_bf[:].bitcast(F32)
-            raw_words = raws[i][3][:].bitcast(F32)
+        def flip_h(m, q):
+            if q == 0:
+                h_flipped[m] = h_pool.tile([P, 2, HALF, B, PACK], BF16, align_bytes=64, name="h_bf")
+            h_words = h_flipped[m][:, q].bitcast(F32)
+            raw_words = h_raws[m][:, :, q].bitcast(F32)
             for pair in range(HALF // PAIR):
                 h_t = psum_t.tile([P, PAIR, 2, B], F32, tag="t")
-                for m in range(PAIR):
+                for i in range(PAIR):
                     for u in range(2):
                         nc.tensor.transpose(
-                            h_t[:, m, u, :], raw_words[:, pair * PAIR + m, u : K_PASS // 2 : 2], ident_f32[:]
+                            h_t[:, i, u, :], raw_words[:, pair * PAIR + i, u : K_PASS // 2 : 2], ident_f32[:]
                         )
                 nc.scalar.copy(
-                    out=h_words[:, pair * PAIR : (pair + 1) * PAIR], in_=h_t[:].rearrange("p m u b -> p m b u")
+                    out=h_words[:, pair * PAIR : (pair + 1) * PAIR], in_=h_t[:].rearrange("p i u b -> p i b u")
                 )
-            h_flipped[i] = h_bf
 
         def quantise(values, kind):
-            codes = quantised.tile([P, HALF, P], U32, align_bytes=64, tag=kind + "_codes")
-            scales = quantised.tile([P, HALF, P], U8, align_bytes=64, tag=kind + "_scales")
+            codes = quantised.tile([P, 2, HALF, P], U32, align_bytes=64, tag=kind + "_codes")
+            scales = quantised.tile([P, 2, HALF, P], U8, align_bytes=64, tag=kind + "_scales")
             nc.vector.quantize_mx(
-                out=codes[:].rearrange("p s m -> p (s m)").bitcast(FP8X4),
-                scales=scales[:].rearrange("p s m -> p (s m)"),
-                in_=values[:].rearrange("p s m j -> p (s m j)"),
+                out=codes[:].rearrange("p q s m -> p (q s m)").bitcast(FP8X4),
+                scales=scales[:].rearrange("p q s m -> p (q s m)"),
+                in_=values[:].rearrange("p q s m j -> p (q s m j)"),
             )
             return codes, scales
 
-        def matmuls(i):
-            c = i % PASSES
-            h_codes, h_scales = h_quantised[i]
-            w_codes, w_scales = w_quantised[i]
-            for s in range(HALF):
-                if c == 0:
-                    banks[s] = psum_acc.tile([B, N], F32, tag="acc%d" % s, name="acc%d" % s)
-                nc.tensor.matmul_mx(
-                    out=banks[s][:],
-                    lhsT=h_codes[:, s, :].bitcast(FP8X4),
-                    lhsT_scale=h_scales[:, s, :],
-                    rhs=w_codes[:, s, :].bitcast(FP8X4),
-                    rhs_scale=w_scales[:, s, :],
-                    start=(c == 0),
-                    stop=(c == PASSES - 1),
-                )
+        def matmuls(m):
+            h_codes, h_scales = h_quantised[m]
+            w_codes, w_scales = w_quantised[m]
+            for q in range(2):
+                c = (2 * m + q) % PASSES
+                for s in range(HALF):
+                    if c == 0:
+                        banks[s] = psum_acc.tile([B, N], F32, tag="acc%d" % s, name="acc%d" % s)
+                    nc.tensor.matmul_mx(
+                        out=banks[s][:],
+                        lhsT=h_codes[:, q, s, :].bitcast(FP8X4),
+                        lhsT_scale=h_scales[:, q, s, :],
+                        rhs=w_codes[:, q, s, :].bitcast(FP8X4),
+                        rhs_scale=w_scales[:, q, s, :],
+                        start=(c == 0),
+                        stop=(c == PASSES - 1),
+                    )
 
         def finish_half(half):
             first = half * HALF
@@ -257,64 +284,97 @@ def tile_bnn_pb_k_kernel(tc, h0, wm1, wv1, bm1, bv1, we1, be1, out):
         nc.vector.memset(warm[:], 0.0)
         nc.scalar.activation(out=warm[:], in_=warm[:], func=ACT.Exp)
 
-        load(0)
-        load(1)
+        load_weights(0)
+        load_weights(1)
+        load_h(0)
+        load_h(1)
         nc.sync.dma_start(out=bias_rows[0:S, :], in_=be1.rearrange("s o n -> (s o) n"))
         nc.sync.dma_start(out=bias_rows[S : S + 1, :], in_=bv1.unsqueeze(0))
         nc.sync.dma_start(out=bias_rows[S + 1 : S + 2, :], in_=bm1.unsqueeze(0))
-        for i in range(2, AHEAD):
-            load(i)
+        load_weights(2)
+        load_h(2)
 
         flip_shared(0)
         std_to_psum(0)
         mean_to_psum(0)
-        operands_in_sbuf(0)
-        flip_h(0)
-        gpsimd_multiply(0)
-        gpsimd_add(0)
         vector_multiply(0)
-        h_quantised[0] = quantise(h_flipped[0], "h")
-        operands_in_sbuf(1)
         flip_shared(1)
-        flip_h(1)
         std_to_psum(1)
+        vector_multiply(1)
+        flip_shared(2)
+        flip_shared(3)
+        std_to_psum(2)
+        shared_in_sbuf(1)
+        noise_in_sbuf(1)
         gpsimd_multiply(1)
         gpsimd_add(1)
-        operands_in_sbuf(2)
+        vector_add(0)
+        mean_to_psum(1)
+        vector_multiply(2)
+        flip_h(0, 0)
+        std_to_psum(3)
+        vector_add(1)
+        flip_h(0, 1)
+        vector_multiply(3)
+        mean_to_psum(2)
+        flip_h(1, 0)
+        flip_h(1, 1)
+        h_quantised[0] = quantise(h_flipped[0], "h")
+        w_quantised[0] = quantise(w_tiles[0], "w")
+        h_quantised[1] = quantise(h_flipped[1], "h")
+        flip_shared(4)
+        std_to_psum(4)
+        flip_shared(5)
+        shared_in_sbuf(2)
+        noise_in_sbuf(2)
         gpsimd_multiply(2)
+        gpsimd_add(2)
+        load_weights(3)
+        load_h(3)
+        shared_in_sbuf(0)
+        flip_h(2, 0)
+        flip_h(2, 1)
 
-        for i in range(STEPS):
-            if i + AHEAD < STEPS:
-                load(i + AHEAD)
-            if i > 0:
-                matmuls(i - 1)
-            if i + 3 < STEPS:
-                operands_in_sbuf(i + 3)
-            if i + 2 < STEPS:
-                if i + 2 < PASSES:
-                    flip_shared(i + 2)
+        for m in range(1, WINDOWS):
+            if m + 3 < WINDOWS:
+                load_weights(m + 3)
+                load_h(m + 3)
+            matmuls(m - 1)
+            if m + 2 < WINDOWS:
+                shared_in_sbuf(m + 2)
+                noise_in_sbuf(m + 2)
+                gpsimd_multiply(m + 2)
+            more = 2 * m + 2 < UNITS
 
-            vector_add(i)
-            if i + 1 < STEPS:
-                mean_to_psum(i + 1)
-                vector_multiply(i + 1)
-            if i + 2 < STEPS:
-                flip_h(i + 2)
-                std_to_psum(i + 2)
-            if i == PASSES:
+            vector_add(2 * m)
+            mean_to_psum(2 * m + 1)
+            if 2 * m + 4 < PASSES:
+                flip_shared(2 * m + 4)
+                flip_shared(2 * m + 5)
+            if more:
+                vector_multiply(2 * m + 2)
+                std_to_psum(2 * m + 3)
+            vector_add(2 * m + 1)
+            if m + 2 < WINDOWS:
+                flip_h(m + 2, 0)
+                flip_h(m + 2, 1)
+            if more:
+                mean_to_psum(2 * m + 2)
+                vector_multiply(2 * m + 3)
+            if 2 * m + 4 < UNITS:
+                std_to_psum(2 * m + 4)
+            if m == HALF_WINDOWS:
                 finish_half(0)
-            w_quantised[i] = quantise(w_tiles[i], "w")
-            if i + 1 < STEPS:
-                h_quantised[i + 1] = quantise(h_flipped[i + 1], "h")
+            w_quantised[m] = quantise(w_tiles[m], "w")
+            if more:
+                h_quantised[m + 1] = quantise(h_flipped[m + 1], "h")
+            if m + 2 < WINDOWS:
+                gpsimd_add(m + 2)
 
-            if i + 2 < STEPS:
-                gpsimd_add(i + 2)
-            if i + 3 < STEPS:
-                gpsimd_multiply(i + 3)
-            if i == BIAS_STEP:
+            if m == BIAS_WINDOW:
                 make_bias_columns()
-            if i in (BIAS_STEP + 1, BIAS_STEP + 2):
-                spread_bias(i - BIAS_STEP - 1)
+            if m in (BIAS_WINDOW + 1, BIAS_WINDOW + 2):
+                spread_bias(m - BIAS_WINDOW - 1)
 
-        matmuls(STEPS - 1)
+        matmuls(WINDOWS - 1)
         finish_half(1)

@@ -20,12 +20,12 @@ K_PASS = P * PACK
 PASSES = K // K_PASS
 HALF = 4
 PAIR = 2
-UNITS = (S // HALF) * PASSES
-WINDOWS = UNITS // 2
+WINDOWS = (S // HALF) * PASSES // 2
 HALF_WINDOWS = PASSES // 2
 BIAS_WINDOW = HALF_WINDOWS - 4
-N_VECTOR = 88
-N_GPSIMD = N - N_VECTOR
+SLOTS = 2 * HALF
+N_VECTOR = (4, 3)
+N_GPSIMD = 2
 
 FLOPS = 2 * S * B * K * N
 
@@ -36,48 +36,55 @@ def tile_bnn_pb_k_kernel(tc, h0, wm1, wv1, bm1, bv1, we1, be1, out):
     wv_rows = wv1.rearrange("(c p j) n -> c p j n", p=P, j=PACK)
     wm_rows = wm1.rearrange("(c p j) n -> c p j n", p=P, j=PACK)
     we_rows = we1.rearrange("s (c p j) n -> c p s j n", p=P, j=PACK)
+    h_rows = h0.rearrange("s b k -> b s k")
     out_rows = out.rearrange("s b n -> b s n")
 
     with (
         tc.tile_pool(name="consts", bufs=1) as consts,
-        tc.tile_pool(name="kept", bufs=PASSES) as kept,
-        tc.tile_pool(name="kept_sb", bufs=HALF_WINDOWS) as kept_sb,
-        tc.tile_pool(name="raw", bufs=3) as raw,
-        tc.tile_pool(name="noise_pool", bufs=2) as noise_pool,
-        tc.tile_pool(name="prod_v_pool", bufs=3) as prod_v_pool,
-        tc.tile_pool(name="prod_g_pool", bufs=1) as prod_g_pool,
+        tc.tile_pool(name="kept", bufs=HALF_WINDOWS) as kept,
+        tc.tile_pool(name="raw_v", bufs=3) as raw_v,
+        tc.tile_pool(name="raw_e", bufs=3) as raw_e,
+        tc.tile_pool(name="raw_h", bufs=3) as raw_h,
+        tc.tile_pool(name="products", bufs=1) as products,
         tc.tile_pool(name="w_pool", bufs=2) as w_pool,
         tc.tile_pool(name="h_pool", bufs=2) as h_pool,
         tc.tile_pool(name="quantised", bufs=2) as quantised,
-        tc.psum_pool(name="psum_t", bufs=2) as psum_t,
-        tc.psum_pool(name="psum_w", bufs=1) as psum_w,
+        tc.psum_pool(name="psum_t", bufs=3) as psum_t,
+        tc.psum_pool(name="psum_a", bufs=1) as psum_a,
         tc.psum_pool(name="psum_acc", bufs=1) as psum_acc,
         tc.manual_schedule(),
     ):
         raws = {}
         h_raws = {}
+        std_flipped = {}
+        mean_flipped = {}
         shared_sb = {}
-        shared_flipped = {}
-        noise = {}
-        std_in_psum = {}
-        mean_in_psum = {}
+        in_psum = {}
+        noise_flipped = {}
+        prod_a = {}
+        prod_t = {}
+        prod_g = {}
         h_flipped = {}
         w_tiles = {}
-        products_v = {}
-        products_g = {}
         h_quantised = {}
         w_quantised = {}
         banks = {}
+
+        def vector_count(m):
+            return N_VECTOR[m // HALF_WINDOWS]
+
+        def flipped_samples(m, q):
+            return range(vector_count(m), HALF) if q == 0 else range(HALF - N_GPSIMD)
 
         def samples(m):
             first = (m // HALF_WINDOWS) * HALF
             return slice(first, first + HALF)
 
         def load_weights(m):
-            wv_raw = raw.tile([P, 2, PACK, N], BF16)
-            wm_raw = raw.tile([P, 2, PACK, N], BF16)
-            we_raw = raw.tile([P, 2, HALF, PACK, N], BF16)
-            for q in range(2):
+            wv_raw = raw_v.tile([P, 2, PACK, N], BF16)
+            wm_raw = raw_v.tile([P, 2, PACK, N], BF16)
+            we_raw = raw_e.tile([P, 2, HALF, PACK, N], BF16)
+            for q in (0, 1) if m == 0 else (1, 0):
                 c = (2 * m + q) % PASSES
                 if m < HALF_WINDOWS:
                     nc.sync.dma_start(out=wv_raw[:, q], in_=wv_rows[c])
@@ -88,137 +95,177 @@ def tile_bnn_pb_k_kernel(tc, h0, wm1, wv1, bm1, bv1, we1, be1, out):
 
         def load_h(m):
             c = (2 * m) % PASSES
-            h_raw = raw.tile([B, HALF, 2, K_PASS], BF16)
+            h_raw = raw_h.tile([B, HALF, 2, K_PASS], BF16)
             nc.sync.dma_start(
                 out=h_raw[:].rearrange("b s q k -> b s (q k)"),
-                in_=h0.rearrange("s b k -> b s k")[:, samples(m), c * K_PASS : (c + 2) * K_PASS],
+                in_=h_rows[:, samples(m), c * K_PASS : (c + 2) * K_PASS],
             )
             h_raws[m] = h_raw
 
         def shared_in_sbuf(m):
             wv_raw, wm_raw, we_raw = raws[m]
-            if m < HALF_WINDOWS:
-                std_sb = kept_sb.tile([P, 2, N_GPSIMD, PACK], F32)
-                nc.scalar.activation(
-                    out=std_sb[:], in_=wv_raw[:, :, :, N_VECTOR:N].rearrange("p q j n -> p q n j"), func=ACT.Exp, scale=0.5
-                )
-                mean_sb = kept_sb.tile([P, 2, N_GPSIMD, PACK], BF16)
-                nc.scalar.copy(out=mean_sb[:], in_=wm_raw[:, :, :, N_VECTOR:N].rearrange("p q j n -> p q n j"))
-                shared_sb[m] = std_sb, mean_sb
+            std_sb = kept.tile([P, PACK, N], F32)
+            nc.scalar.activation(out=std_sb[:], in_=wv_raw[:, 1], func=ACT.Exp, scale=0.5)
+            mean_sb = kept.tile([P, N, PACK], BF16)
+            nc.scalar.copy(out=mean_sb[:], in_=wm_raw[:, 1].rearrange("p j n -> p n j"))
+            shared_sb[m] = std_sb, mean_sb
 
-        def noise_in_sbuf(m):
+        def flip_shared(m, q):
             wv_raw, wm_raw, we_raw = raws[m]
-            noise_sb = noise_pool.tile([P, 2, HALF, N_GPSIMD, PACK], BF16)
-            nc.scalar.copy(
-                out=noise_sb[:].rearrange("p q s n j -> p (q s) n j"),
-                in_=we_raw[:, :, :, :, N_VECTOR:N].rearrange("p q s j n -> p (q s) n j"),
-            )
-            noise[m] = noise_sb
-
-        def flip_shared(u):
-            wv_raw, wm_raw, we_raw = raws[u // 2]
             flipped = psum_t.tile([N, 2, PACK, P], BF16, tag="t")
             for j in range(PACK):
-                nc.tensor.transpose(flipped[:, 0, j, :], wv_raw[:, u % 2, j, :], ident_bf[:])
+                nc.tensor.transpose(flipped[:, 0, j, :], wv_raw[:, q, j, :], ident_bf[:])
             for j in range(PACK):
-                nc.tensor.transpose(flipped[:, 1, j, :], wm_raw[:, u % 2, j, :], ident_bf[:])
-            std_flipped = kept.tile([N, PACK, P], F32)
-            nc.scalar.activation(out=std_flipped[:], in_=flipped[:, 0], func=ACT.Exp, scale=0.5)
-            mean_flipped = kept.tile([N, PACK, P], BF16)
-            nc.scalar.copy(out=mean_flipped[:], in_=flipped[:, 1])
-            shared_flipped[u] = std_flipped, mean_flipped
+                nc.tensor.transpose(flipped[:, 1, j, :], wm_raw[:, q, j, :], ident_bf[:])
+            std = kept.tile([N, PACK, P], F32, name="std%d" % q)
+            nc.scalar.activation(out=std[:], in_=flipped[:, 0], func=ACT.Exp, scale=0.5)
+            mean = kept.tile([N, PACK, P], F32, name="mean%d" % q)
+            nc.scalar.copy(out=mean[:], in_=flipped[:, 1])
+            std_flipped[m, q] = std
+            mean_flipped[m, q] = mean
 
-        def std_to_psum(u):
-            std_flipped, mean_flipped = shared_flipped[u % PASSES]
-            std_ps = psum_w.tile([P, PACK, N], F32)
+        def std_to_psum(m):
+            std_ps = psum_a.tile([P, PACK, N], F32, tag="a")
             for j in range(PACK):
-                nc.tensor.transpose(std_ps[:, j, :], std_flipped[:, j, :], ident_f32[:])
-            std_in_psum[u] = std_ps[:, :, 0 : columns(u)].rearrange("p (h i) n -> p h n i", h=2)
+                nc.tensor.transpose(std_ps[:, j, :], std_flipped[m % HALF_WINDOWS, 0][:, j, :], ident_f32[:])
+            in_psum[m] = std_ps
 
-        def mean_to_psum(u):
-            std_flipped, mean_flipped = shared_flipped[u % PASSES]
-            mean_ps = psum_w.tile([P, PACK, N], BF16)
+        def mean_to_psum(m):
+            mean_ps = psum_a.tile([P, PACK, N], F32, tag="a")
             for j in range(PACK):
-                nc.tensor.transpose(mean_ps[:, j, :], mean_flipped[:, j, :], ident_bf[:])
-            mean_in_psum[u] = mean_ps[:, :, 0 : columns(u)].rearrange("p (h i) n -> p n h i", h=2)
+                nc.tensor.transpose(mean_ps[:, j, :], mean_flipped[m % HALF_WINDOWS, 0][:, j, :], ident_f32[:])
+            in_psum[m] = mean_ps
 
-        def columns(u):
-            return N if u < 2 else N_VECTOR
-
-        def vector_multiply(u):
-            count = columns(u)
-            we_raw = raws[u // 2][2]
-            prod_v = prod_v_pool.tile([P, 2, HALF, count, 2], F32)
+        def vector_multiply(m, std_all=None):
+            if std_all is None:
+                std_all = in_psum[m]
+            count = vector_count(m)
+            we_raw = raws[m][2]
+            prod = products.tile([P, 2, count, N, 2], F32, name="prod_a")
             for h in range(2):
+                std = std_all[:, 2 * h : 2 * h + 2, :].rearrange("p i n -> p n i")
                 nc.vector.tensor_tensor(
-                    out=prod_v[:, h],
-                    in0=we_raw[:, u % 2, :, 2 * h : 2 * h + 2, 0:count].rearrange("p s i n -> p s n i"),
-                    in1=std_in_psum[u][:, h].unsqueeze(1).to_broadcast([P, HALF, count, 2]),
+                    out=prod[:, h],
+                    in0=we_raw[:, 0, 0:count, 2 * h : 2 * h + 2, :].rearrange("p s i n -> p s n i"),
+                    in1=std.unsqueeze(1).to_broadcast([P, count, N, 2]),
                     op=ALU.mult,
                 )
-            products_v[u] = prod_v
+            prod_a[m] = prod
 
-        def vector_add(u):
-            count = columns(u)
+        def vector_add(m):
+            count = vector_count(m)
+            mean = in_psum[m][:].rearrange("p (h i) n -> p n h i", h=2)
             nc.vector.tensor_tensor(
-                out=w_tile(u // 2)[:, u % 2, :, 0:count, :].rearrange("p s n (h i) -> p s n h i", h=2),
-                in0=products_v[u][:].rearrange("p h s n i -> p s n h i"),
-                in1=mean_in_psum[u].unsqueeze(1).to_broadcast([P, HALF, count, 2, 2]),
+                out=w_tile(m)[:, 0:count].rearrange("p s n (h i) -> p s n h i", h=2),
+                in0=prod_a[m][:].rearrange("p h s n i -> p s n h i"),
+                in1=mean.unsqueeze(1).to_broadcast([P, count, N, 2, 2]),
                 op=ALU.add,
             )
 
         def w_tile(m):
             if m not in w_tiles:
-                w_tiles[m] = w_pool.tile([P, 2, HALF, N, PACK], BF16, align_bytes=64, name="w_bf")
+                w_tiles[m] = w_pool.tile([P, SLOTS, N, PACK], BF16, align_bytes=64, name="w_bf")
             return w_tiles[m]
 
-        def for_gpsimd(shared):
-            flat = shared[:].rearrange("p q n j -> p q (n j)")
-            return flat.unsqueeze(2).to_broadcast([P, 2, HALF, N_GPSIMD * PACK])
+        def flip_noise(m, q):
+            if len(flipped_samples(m, q)) == 0:
+                return
+            we_raw = raws[m][2]
+            flipped = psum_t.tile([N, len(flipped_samples(m, q)), PACK, P], BF16, tag="t")
+            for index, s in enumerate(flipped_samples(m, q)):
+                for j in range(PACK):
+                    nc.tensor.transpose(flipped[:, index, j, :], we_raw[:, q, s, j, :], ident_bf[:])
+            noise_flipped[m, q] = flipped
 
-        def gpsimd_multiply(m):
-            prod_g = prod_g_pool.tile([P, 2, HALF, N_GPSIMD * PACK], F32)
-            nc.gpsimd.tensor_tensor(
-                out=prod_g[:],
-                in0=noise[m][:].rearrange("p q s n j -> p q s (n j)"),
-                in1=for_gpsimd(shared_sb[m % HALF_WINDOWS][0]),
+        def multiply_flipped(m, q):
+            if len(flipped_samples(m, q)) == 0:
+                return
+            shape = [N, len(flipped_samples(m, q)), PACK * P]
+            std = std_flipped[m % HALF_WINDOWS, q][:].rearrange("n j p -> n (j p)")
+            prod = products.tile(shape, F32, name="prod_t%d" % q)
+            nc.vector.tensor_tensor(
+                out=prod[:],
+                in0=noise_flipped[m, q][:].rearrange("n s j p -> n s (j p)"),
+                in1=std.unsqueeze(1).to_broadcast(shape),
                 op=ALU.mult,
             )
-            products_g[m] = prod_g
+            prod_t[m, q] = prod
+
+        def flip_back(m, q):
+            mean = mean_flipped[m % HALF_WINDOWS, q]
+            for index, s in enumerate(flipped_samples(m, q)):
+                w_ps = psum_t.tile([P, PACK, N], F32, tag="t")
+                for j in range(PACK):
+                    nc.tensor.matmul(
+                        out=w_ps[:, j, :],
+                        lhsT=prod_t[m, q][:, index, j * P : (j + 1) * P],
+                        rhs=ident_f32[:],
+                        is_transpose=True,
+                        start=True,
+                        stop=False,
+                    )
+                    nc.tensor.matmul(
+                        out=w_ps[:, j, :],
+                        lhsT=mean[:, j, :],
+                        rhs=ident_f32[:],
+                        is_transpose=True,
+                        start=False,
+                        stop=True,
+                    )
+                nc.scalar.copy(out=w_tile(m)[:, q * HALF + s], in_=w_ps[:].rearrange("p j n -> p n j"))
+
+        def gpsimd_multiply(m):
+            we_raw = raws[m][2]
+            prod = products.tile([P, N_GPSIMD, PACK * N], F32, name="prod_g")
+            std = shared_sb[m % HALF_WINDOWS][0][:].rearrange("p j n -> p (j n)")
+            nc.gpsimd.tensor_tensor(
+                out=prod[:],
+                in0=we_raw[:, 1, HALF - N_GPSIMD : HALF].rearrange("p s j n -> p s (j n)"),
+                in1=std.unsqueeze(1).to_broadcast([P, N_GPSIMD, PACK * N]),
+                op=ALU.mult,
+            )
+            prod_g[m] = prod
 
         def gpsimd_add(m):
+            mean_sb = shared_sb[m % HALF_WINDOWS][1]
             nc.gpsimd.tensor_tensor(
-                out=w_tile(m)[:, :, :, N_VECTOR:N, :].rearrange("p q s n j -> p q s (n j)"),
-                in0=products_g[m][:],
-                in1=for_gpsimd(shared_sb[m % HALF_WINDOWS][1]),
+                out=w_tile(m)[:, SLOTS - N_GPSIMD : SLOTS],
+                in0=prod_g[m][:].rearrange("p s (j n) -> p s n j", j=PACK),
+                in1=mean_sb[:].unsqueeze(1).to_broadcast([P, N_GPSIMD, N, PACK]),
                 op=ALU.add,
             )
 
-        def flip_h(m, q):
-            if q == 0:
-                h_flipped[m] = h_pool.tile([P, 2, HALF, B, PACK], BF16, align_bytes=64, name="h_bf")
-            h_words = h_flipped[m][:, q].bitcast(F32)
+        def flip_h(m, part):
+            q, pair = part // 2, part % 2
+            if part == 0:
+                h_flipped[m] = h_pool.tile([P, SLOTS, B, PACK], BF16, align_bytes=64, name="h_bf")
+            h_words = h_flipped[m][:, q * HALF : (q + 1) * HALF].bitcast(F32)
             raw_words = h_raws[m][:, :, q].bitcast(F32)
-            for pair in range(HALF // PAIR):
-                h_t = psum_t.tile([P, PAIR, 2, B], F32, tag="t")
-                for i in range(PAIR):
-                    for u in range(2):
-                        nc.tensor.transpose(
-                            h_t[:, i, u, :], raw_words[:, pair * PAIR + i, u : K_PASS // 2 : 2], ident_f32[:]
-                        )
-                nc.scalar.copy(
-                    out=h_words[:, pair * PAIR : (pair + 1) * PAIR], in_=h_t[:].rearrange("p i u b -> p i b u")
-                )
+            h_t = psum_t.tile([P, PAIR, 2, B], F32, tag="t")
+            for i in range(PAIR):
+                for u in range(2):
+                    nc.tensor.transpose(
+                        h_t[:, i, u, :], raw_words[:, pair * PAIR + i, u : K_PASS // 2 : 2], ident_f32[:]
+                    )
+            nc.scalar.copy(
+                out=h_words[:, pair * PAIR : (pair + 1) * PAIR], in_=h_t[:].rearrange("p i u b -> p i b u")
+            )
 
         def quantise(values, kind):
-            codes = quantised.tile([P, 2, HALF, P], U32, align_bytes=64, tag=kind + "_codes")
-            scales = quantised.tile([P, 2, HALF, P], U8, align_bytes=64, tag=kind + "_scales")
+            codes = quantised.tile([P, SLOTS, P], U32, align_bytes=64, tag=kind + "_codes")
+            scales = quantised.tile([P, SLOTS, P], U8, align_bytes=64, tag=kind + "_scales")
             nc.vector.quantize_mx(
-                out=codes[:].rearrange("p q s m -> p (q s m)").bitcast(FP8X4),
-                scales=scales[:].rearrange("p q s m -> p (q s m)"),
-                in_=values[:].rearrange("p q s m j -> p (q s m j)"),
+                out=codes[:].rearrange("p s m -> p (s m)").bitcast(FP8X4),
+                scales=scales[:].rearrange("p s m -> p (s m)"),
+                in_=values,
             )
             return codes, scales
+
+        def quantise_w(m):
+            w_quantised[m] = quantise(w_tiles[m][:].rearrange("p s n j -> p (s n j)"), "w")
+
+        def quantise_h(m):
+            h_quantised[m] = quantise(h_flipped[m][:].rearrange("p s b j -> p (s b j)"), "h")
 
         def matmuls(m):
             h_codes, h_scales = h_quantised[m]
@@ -226,14 +273,15 @@ def tile_bnn_pb_k_kernel(tc, h0, wm1, wv1, bm1, bv1, we1, be1, out):
             for q in range(2):
                 c = (2 * m + q) % PASSES
                 for s in range(HALF):
+                    slot = q * HALF + s
                     if c == 0:
                         banks[s] = psum_acc.tile([B, N], F32, tag="acc%d" % s, name="acc%d" % s)
                     nc.tensor.matmul_mx(
                         out=banks[s][:],
-                        lhsT=h_codes[:, q, s, :].bitcast(FP8X4),
-                        lhsT_scale=h_scales[:, q, s, :],
-                        rhs=w_codes[:, q, s, :].bitcast(FP8X4),
-                        rhs_scale=w_scales[:, q, s, :],
+                        lhsT=h_codes[:, slot, :].bitcast(FP8X4),
+                        lhsT_scale=h_scales[:, slot, :],
+                        rhs=w_codes[:, slot, :].bitcast(FP8X4),
+                        rhs_scale=w_scales[:, slot, :],
                         start=(c == 0),
                         stop=(c == PASSES - 1),
                     )
@@ -287,88 +335,93 @@ def tile_bnn_pb_k_kernel(tc, h0, wm1, wv1, bm1, bv1, we1, be1, out):
         load_weights(0)
         load_weights(1)
         load_h(0)
+        load_weights(2)
         load_h(1)
+
+        first_std = consts.tile([P, PACK, N], F32)
+        nc.scalar.activation(out=first_std[:], in_=raws[0][0][:, 0], func=ACT.Exp, scale=0.5)
+        vector_multiply(0, first_std)
+        flip_shared(0, 0)
+        flip_shared(0, 1)
+        mean_to_psum(0)
+        flip_noise(0, 1)
+        shared_in_sbuf(0)
+        multiply_flipped(0, 1)
+        gpsimd_multiply(0)
+        gpsimd_add(0)
+        vector_add(0)
+        flip_shared(1, 1)
+        flip_noise(1, 1)
+        flip_back(0, 1)
+        flip_shared(1, 0)
+        shared_in_sbuf(1)
+        gpsimd_multiply(1)
+        gpsimd_add(1)
+        multiply_flipped(1, 1)
+        std_to_psum(1)
+        vector_multiply(1)
+        for part in range(4):
+            flip_h(0, part)
+        mean_to_psum(1)
+        flip_back(1, 1)
+        quantise_h(0)
+        quantise_w(0)
+        load_weights(3)
+        load_h(2)
         nc.sync.dma_start(out=bias_rows[0:S, :], in_=be1.rearrange("s o n -> (s o) n"))
         nc.sync.dma_start(out=bias_rows[S : S + 1, :], in_=bv1.unsqueeze(0))
         nc.sync.dma_start(out=bias_rows[S + 1 : S + 2, :], in_=bm1.unsqueeze(0))
-        load_weights(2)
-        load_h(2)
-
-        flip_shared(0)
-        std_to_psum(0)
-        mean_to_psum(0)
-        vector_multiply(0)
-        flip_shared(1)
-        std_to_psum(1)
-        vector_multiply(1)
-        flip_shared(2)
-        flip_shared(3)
-        std_to_psum(2)
-        shared_in_sbuf(1)
-        noise_in_sbuf(1)
-        gpsimd_multiply(1)
-        gpsimd_add(1)
-        vector_add(0)
-        mean_to_psum(1)
-        vector_multiply(2)
-        flip_h(0, 0)
-        std_to_psum(3)
-        vector_add(1)
-        flip_h(0, 1)
-        vector_multiply(3)
-        mean_to_psum(2)
-        flip_h(1, 0)
-        flip_h(1, 1)
-        h_quantised[0] = quantise(h_flipped[0], "h")
-        w_quantised[0] = quantise(w_tiles[0], "w")
-        h_quantised[1] = quantise(h_flipped[1], "h")
-        flip_shared(4)
-        std_to_psum(4)
-        flip_shared(5)
         shared_in_sbuf(2)
-        noise_in_sbuf(2)
         gpsimd_multiply(2)
         gpsimd_add(2)
-        load_weights(3)
-        load_h(3)
-        shared_in_sbuf(0)
-        flip_h(2, 0)
-        flip_h(2, 1)
+        flip_noise(2, 1)
+        flip_shared(2, 0)
+        flip_shared(2, 1)
+        for part in range(4):
+            flip_h(1, part)
 
         for m in range(1, WINDOWS):
             if m + 3 < WINDOWS:
                 load_weights(m + 3)
-                load_h(m + 3)
-            matmuls(m - 1)
             if m + 2 < WINDOWS:
-                shared_in_sbuf(m + 2)
-                noise_in_sbuf(m + 2)
-                gpsimd_multiply(m + 2)
-            more = 2 * m + 2 < UNITS
+                load_h(m + 2)
+            more = m + 1 < WINDOWS
+            more2 = m + 2 < WINDOWS
+            fresh = m + 2 < HALF_WINDOWS
 
-            vector_add(2 * m)
-            mean_to_psum(2 * m + 1)
-            if 2 * m + 4 < PASSES:
-                flip_shared(2 * m + 4)
-                flip_shared(2 * m + 5)
+            if fresh:
+                shared_in_sbuf(m + 2)
+            if more and m > 1:
+                flip_noise(m + 1, 1)
+            matmuls(m - 1)
+            if fresh:
+                flip_shared(m + 2, 0)
+            if more2:
+                gpsimd_multiply(m + 2)
+            vector_add(m)
             if more:
-                vector_multiply(2 * m + 2)
-                std_to_psum(2 * m + 3)
-            vector_add(2 * m + 1)
-            if m + 2 < WINDOWS:
-                flip_h(m + 2, 0)
-                flip_h(m + 2, 1)
+                multiply_flipped(m + 1, 1)
+                std_to_psum(m + 1)
+                flip_noise(m + 1, 0)
+                vector_multiply(m + 1)
+                multiply_flipped(m + 1, 0)
+            if fresh:
+                flip_shared(m + 2, 1)
             if more:
-                mean_to_psum(2 * m + 2)
-                vector_multiply(2 * m + 3)
-            if 2 * m + 4 < UNITS:
-                std_to_psum(2 * m + 4)
+                flip_back(m + 1, 1)
+            if more:
+                flip_h(m + 1, 0)
+            if more:
+                mean_to_psum(m + 1)
+                flip_back(m + 1, 0)
+            if more:
+                for part in range(1, 4):
+                    flip_h(m + 1, part)
             if m == HALF_WINDOWS:
                 finish_half(0)
-            w_quantised[m] = quantise(w_tiles[m], "w")
-            if more:
-                h_quantised[m + 1] = quantise(h_flipped[m + 1], "h")
-            if m + 2 < WINDOWS:
+            quantise_w(m)
+            quantise_h(m)
+            if more2:
                 gpsimd_add(m + 2)
 
             if m == BIAS_WINDOW:

@@ -24,8 +24,9 @@ WINDOWS = (S // HALF) * PASSES // 2
 HALF_WINDOWS = PASSES // 2
 BIAS_WINDOW = HALF_WINDOWS - 4
 SLOTS = 2 * HALF
-N_VECTOR = (4, 3)
-N_GPSIMD = 2
+N_FLIPPED = 2
+N_GPSIMD = HALF - N_FLIPPED
+WORDS = N // 2
 
 FLOPS = 2 * S * B * K * N
 
@@ -56,12 +57,14 @@ def tile_bnn_pb_k_kernel(tc, h0, wm1, wv1, bm1, bv1, we1, be1, out):
     ):
         raws = {}
         h_raws = {}
-        std_flipped = {}
-        mean_flipped = {}
-        shared_sb = {}
+        first_flipped = {}
+        second_flipped = {}
+        std_rows = {}
+        mean_rows = {}
+        w_rows = {}
         in_psum = {}
         noise_flipped = {}
-        prod_a = {}
+        prod_v = {}
         prod_t = {}
         prod_g = {}
         h_flipped = {}
@@ -70,27 +73,29 @@ def tile_bnn_pb_k_kernel(tc, h0, wm1, wv1, bm1, bv1, we1, be1, out):
         w_quantised = {}
         banks = {}
 
-        def vector_count(m):
-            return N_VECTOR[m // HALF_WINDOWS]
-
-        def flipped_samples(m, q):
-            return range(vector_count(m), HALF) if q == 0 else range(HALF - N_GPSIMD)
-
         def samples(m):
             first = (m // HALF_WINDOWS) * HALF
             return slice(first, first + HALF)
 
         def load_weights(m):
             wv_raw = raw_v.tile([P, 2, PACK, N], BF16)
-            wm_raw = raw_v.tile([P, 2, PACK, N], BF16)
+            wm_raw = raw_v.tile([P, PACK, N], BF16)
+            if m < HALF_WINDOWS:
+                mean_rows[m] = kept.tile([P, PACK, N], BF16, name="mean_rows")
             we_raw = raw_e.tile([P, 2, HALF, PACK, N], BF16)
-            for q in (0, 1) if m == 0 else (1, 0):
+            for q in range(2):
                 c = (2 * m + q) % PASSES
                 if m < HALF_WINDOWS:
                     nc.sync.dma_start(out=wv_raw[:, q], in_=wv_rows[c])
-                nc.sync.dma_start(out=we_raw[:, q], in_=we_rows[c][:, samples(m)])
+                pieces = 2 if m == 0 and q == 0 else 1
+                first = samples(m).start
+                for i in range(pieces):
+                    part = slice(i * HALF // pieces, (i + 1) * HALF // pieces)
+                    nc.sync.dma_start(
+                        out=we_raw[:, q, part], in_=we_rows[c][:, first + part.start : first + part.stop]
+                    )
                 if m < HALF_WINDOWS:
-                    nc.sync.dma_start(out=wm_raw[:, q], in_=wm_rows[c])
+                    nc.sync.dma_start(out=(wm_raw if q == 0 else mean_rows[m])[:], in_=wm_rows[c])
             raws[m] = wv_raw, wm_raw, we_raw
 
         def load_h(m):
@@ -102,144 +107,172 @@ def tile_bnn_pb_k_kernel(tc, h0, wm1, wv1, bm1, bv1, we1, be1, out):
             )
             h_raws[m] = h_raw
 
-        def shared_in_sbuf(m):
-            wv_raw, wm_raw, we_raw = raws[m]
-            std_sb = kept.tile([P, PACK, N], F32)
-            nc.scalar.activation(out=std_sb[:], in_=wv_raw[:, 1], func=ACT.Exp, scale=0.5)
-            mean_sb = kept.tile([P, N, PACK], BF16)
-            nc.scalar.copy(out=mean_sb[:], in_=wm_raw[:, 1].rearrange("p j n -> p n j"))
-            shared_sb[m] = std_sb, mean_sb
+        def std_in_sbuf(m):
+            std = kept.tile([P, PACK, N], F32, name="std_rows")
+            nc.scalar.activation(out=std[:], in_=raws[m][0][:, 1], func=ACT.Exp, scale=0.5)
+            std_rows[m] = std
 
-        def flip_shared(m, q):
+        def words_of(rows, h):
+            return rows.rearrange("p j n -> p (j n)").bitcast(F32)[:, 2 * WORDS * h : 2 * WORDS * (h + 1)]
+
+        def flip_first(m):
             wv_raw, wm_raw, we_raw = raws[m]
-            flipped = psum_t.tile([N, 2, PACK, P], BF16, tag="t")
+            flipped = psum_t.tile([P, 2, 2, P], F32, tag="t")
+            wv_flipped = flipped[:, 0].rearrange("n h p -> n (h p)").bitcast(BF16)
             for j in range(PACK):
-                nc.tensor.transpose(flipped[:, 0, j, :], wv_raw[:, q, j, :], ident_bf[:])
-            for j in range(PACK):
-                nc.tensor.transpose(flipped[:, 1, j, :], wm_raw[:, q, j, :], ident_bf[:])
-            std = kept.tile([N, PACK, P], F32, name="std%d" % q)
-            nc.scalar.activation(out=std[:], in_=flipped[:, 0], func=ACT.Exp, scale=0.5)
-            mean = kept.tile([N, PACK, P], F32, name="mean%d" % q)
+                nc.tensor.transpose(wv_flipped[:, j * P : (j + 1) * P], wv_raw[:, 0, j, :], ident_bf[:])
+            for h in range(2):
+                nc.tensor.transpose(flipped[:, 1, h, :], words_of(wm_raw[:], h), ident_f32[:])
+            std = kept.tile([N, PACK * P], F32, name="std0")
+            nc.scalar.activation(out=std[:], in_=wv_flipped, func=ACT.Exp, scale=0.5)
+            mean = kept.tile([P, 2, P], F32, name="mean0")
             nc.scalar.copy(out=mean[:], in_=flipped[:, 1])
-            std_flipped[m, q] = std
-            mean_flipped[m, q] = mean
+            first_flipped[m] = std, mean
+
+        def flip_second(m):
+            wv_raw, wm_raw, we_raw = raws[m]
+            flipped = psum_t.tile([P, 2, 2, P], F32, tag="t")
+            for i, rows in enumerate((wv_raw[:, 1], mean_rows[m][:])):
+                for h in range(2):
+                    nc.tensor.transpose(flipped[:, i, h, :], words_of(rows, h), ident_f32[:])
+            wv_flipped = flipped[:, 0].rearrange("f h p -> f (h p)").bitcast(BF16)
+            wm_flipped = flipped[:, 1].rearrange("f h p -> f (h p)").bitcast(BF16)
+            std = kept.tile([P, 2 * P * 2], F32, name="std1")
+            nc.scalar.activation(out=std[:], in_=wv_flipped, func=ACT.Exp, scale=0.5)
+            mean = kept.tile([P, 2, 2, P], F32, name="mean1")
+            nc.scalar.copy(out=mean[:], in_=wm_flipped.rearrange("f (h p e) -> f h e p", h=2, e=2))
+            second_flipped[m] = std, mean
 
         def std_to_psum(m):
+            std = first_flipped[m % HALF_WINDOWS][0]
             std_ps = psum_a.tile([P, PACK, N], F32, tag="a")
             for j in range(PACK):
-                nc.tensor.transpose(std_ps[:, j, :], std_flipped[m % HALF_WINDOWS, 0][:, j, :], ident_f32[:])
-            in_psum[m] = std_ps
+                nc.tensor.transpose(std_ps[:, j, :], std[:, j * P : (j + 1) * P], ident_f32[:])
+            in_psum[m] = std_ps[:]
 
         def mean_to_psum(m):
-            mean_ps = psum_a.tile([P, PACK, N], F32, tag="a")
-            for j in range(PACK):
-                nc.tensor.transpose(mean_ps[:, j, :], mean_flipped[m % HALF_WINDOWS, 0][:, j, :], ident_f32[:])
-            in_psum[m] = mean_ps
+            mean = first_flipped[m % HALF_WINDOWS][1]
+            mean_ps = psum_a.tile([P, PACK * WORDS], F32, tag="a")
+            for h in range(2):
+                nc.tensor.transpose(mean_ps[:, 2 * WORDS * h : 2 * WORDS * (h + 1)], mean[:, h, :], ident_f32[:])
+            in_psum[m] = mean_ps[:].bitcast(BF16).rearrange("p (j n) -> p j n", j=PACK)
 
-        def vector_multiply(m, std_all=None):
-            if std_all is None:
-                std_all = in_psum[m]
-            count = vector_count(m)
+        def vector_multiply(m, std_all, q=0, first=0):
             we_raw = raws[m][2]
-            prod = products.tile([P, 2, count, N, 2], F32, name="prod_a")
+            count = HALF - first
+            prod = products.tile([P, 2, count, N, 2], F32, name="prod_v")
             for h in range(2):
                 std = std_all[:, 2 * h : 2 * h + 2, :].rearrange("p i n -> p n i")
                 nc.vector.tensor_tensor(
                     out=prod[:, h],
-                    in0=we_raw[:, 0, 0:count, 2 * h : 2 * h + 2, :].rearrange("p s i n -> p s n i"),
+                    in0=we_raw[:, q, first:HALF, 2 * h : 2 * h + 2, :].rearrange("p s i n -> p s n i"),
                     in1=std.unsqueeze(1).to_broadcast([P, count, N, 2]),
                     op=ALU.mult,
                 )
-            prod_a[m] = prod
+            prod_v[m, q] = prod
 
-        def vector_add(m):
-            count = vector_count(m)
-            mean = in_psum[m][:].rearrange("p (h i) n -> p n h i", h=2)
+        def vector_add(m, mean_all, q=0, first=0):
+            count = HALF - first
+            mean = mean_all.rearrange("p (h i) n -> p n h i", h=2)
             nc.vector.tensor_tensor(
-                out=w_tile(m)[:, 0:count].rearrange("p s n (h i) -> p s n h i", h=2),
-                in0=prod_a[m][:].rearrange("p h s n i -> p s n h i"),
+                out=w_tile(m)[:, q * HALF + first : (q + 1) * HALF].rearrange("p s n (h i) -> p s n h i", h=2),
+                in0=prod_v[m, q][:].rearrange("p h s n i -> p s n h i"),
                 in1=mean.unsqueeze(1).to_broadcast([P, count, N, 2, 2]),
                 op=ALU.add,
             )
+
+        def h_tile(m):
+            if m not in h_flipped:
+                h_flipped[m] = h_pool.tile(
+                    [P, SLOTS * B * PACK + N_GPSIMD * PACK * N], BF16, align_bytes=64, name="h_bf"
+                )
+            return h_flipped[m]
 
         def w_tile(m):
             if m not in w_tiles:
                 w_tiles[m] = w_pool.tile([P, SLOTS, N, PACK], BF16, align_bytes=64, name="w_bf")
             return w_tiles[m]
 
-        def flip_noise(m, q):
-            if len(flipped_samples(m, q)) == 0:
-                return
+        def flip_noise(m):
             we_raw = raws[m][2]
-            flipped = psum_t.tile([N, len(flipped_samples(m, q)), PACK, P], BF16, tag="t")
-            for index, s in enumerate(flipped_samples(m, q)):
-                for j in range(PACK):
-                    nc.tensor.transpose(flipped[:, index, j, :], we_raw[:, q, s, j, :], ident_bf[:])
-            noise_flipped[m, q] = flipped
+            flipped = psum_t.tile([P, N_FLIPPED, 2, P], F32, tag="t")
+            for s in range(N_FLIPPED):
+                for h in range(2):
+                    nc.tensor.transpose(flipped[:, s, h, :], words_of(we_raw[:, 1, s], h), ident_f32[:])
+            noise_flipped[m] = flipped
 
-        def multiply_flipped(m, q):
-            if len(flipped_samples(m, q)) == 0:
-                return
-            shape = [N, len(flipped_samples(m, q)), PACK * P]
-            std = std_flipped[m % HALF_WINDOWS, q][:].rearrange("n j p -> n (j p)")
-            prod = products.tile(shape, F32, name="prod_t%d" % q)
+        def multiply_flipped(m):
+            shape = [P, N_FLIPPED, 2 * P * 2]
+            noise = noise_flipped[m][:].rearrange("f s h p -> f (s h p)").bitcast(BF16)
+            std = second_flipped[m % HALF_WINDOWS][0][:]
+            prod = products.tile(shape, F32, name="prod_t")
             nc.vector.tensor_tensor(
                 out=prod[:],
-                in0=noise_flipped[m, q][:].rearrange("n s j p -> n s (j p)"),
+                in0=noise.rearrange("f (s x) -> f s x", s=N_FLIPPED),
                 in1=std.unsqueeze(1).to_broadcast(shape),
                 op=ALU.mult,
             )
-            prod_t[m, q] = prod
+            prod_t[m] = prod
 
-        def flip_back(m, q):
-            mean = mean_flipped[m % HALF_WINDOWS, q]
-            for index, s in enumerate(flipped_samples(m, q)):
-                w_ps = psum_t.tile([P, PACK, N], F32, tag="t")
-                for j in range(PACK):
-                    nc.tensor.matmul(
-                        out=w_ps[:, j, :],
-                        lhsT=prod_t[m, q][:, index, j * P : (j + 1) * P],
-                        rhs=ident_f32[:],
-                        is_transpose=True,
-                        start=True,
-                        stop=False,
-                    )
-                    nc.tensor.matmul(
-                        out=w_ps[:, j, :],
-                        lhsT=mean[:, j, :],
-                        rhs=ident_f32[:],
-                        is_transpose=True,
-                        start=False,
-                        stop=True,
-                    )
-                nc.scalar.copy(out=w_tile(m)[:, q * HALF + s], in_=w_ps[:].rearrange("p j n -> p n j"))
+        def flip_back(m):
+            mean = second_flipped[m % HALF_WINDOWS][1]
+            for s in range(N_FLIPPED):
+                w_ps = psum_t.tile([P, 2, 2, 2 * WORDS], F32, tag="t")
+                for h in range(2):
+                    for e in range(2):
+                        first = h * 2 * P + e
+                        nc.tensor.matmul(
+                            out=w_ps[:, e, h, :],
+                            lhsT=prod_t[m][:, s, first : first + 2 * P - 1 : 2],
+                            rhs=ident_f32[:],
+                            is_transpose=True,
+                            start=True,
+                            stop=False,
+                        )
+                        nc.tensor.matmul(
+                            out=w_ps[:, e, h, :],
+                            lhsT=mean[:, h, e, :],
+                            rhs=ident_f32[:],
+                            is_transpose=True,
+                            start=False,
+                            stop=True,
+                        )
+                nc.scalar.copy(
+                    out=w_tile(m)[:, HALF + s].rearrange("p (v e) j -> p v e j", e=2),
+                    in_=w_ps[:].rearrange("p e h (i v) -> p v e (h i)", i=2),
+                )
 
         def gpsimd_multiply(m):
-            we_raw = raws[m][2]
             prod = products.tile([P, N_GPSIMD, PACK * N], F32, name="prod_g")
-            std = shared_sb[m % HALF_WINDOWS][0][:].rearrange("p j n -> p (j n)")
+            std = std_rows[m % HALF_WINDOWS][:].rearrange("p j n -> p (j n)")
             nc.gpsimd.tensor_tensor(
                 out=prod[:],
-                in0=we_raw[:, 1, HALF - N_GPSIMD : HALF].rearrange("p s j n -> p s (j n)"),
+                in0=raws[m][2][:, 1, N_FLIPPED:HALF].rearrange("p s j n -> p s (j n)"),
                 in1=std.unsqueeze(1).to_broadcast([P, N_GPSIMD, PACK * N]),
                 op=ALU.mult,
             )
             prod_g[m] = prod
 
         def gpsimd_add(m):
-            mean_sb = shared_sb[m % HALF_WINDOWS][1]
+            rows = h_tile(m)[:, SLOTS * B * PACK :]
+            mean = mean_rows[m % HALF_WINDOWS][:].rearrange("p j n -> p (j n)")
             nc.gpsimd.tensor_tensor(
-                out=w_tile(m)[:, SLOTS - N_GPSIMD : SLOTS],
-                in0=prod_g[m][:].rearrange("p s (j n) -> p s n j", j=PACK),
-                in1=mean_sb[:].unsqueeze(1).to_broadcast([P, N_GPSIMD, N, PACK]),
+                out=rows.rearrange("p (s x) -> p s x", s=N_GPSIMD),
+                in0=prod_g[m][:],
+                in1=mean.unsqueeze(1).to_broadcast([P, N_GPSIMD, PACK * N]),
                 op=ALU.add,
+            )
+            w_rows[m] = rows
+
+        def interleave_rows(m):
+            nc.scalar.copy(
+                out=w_tile(m)[:, SLOTS - N_GPSIMD : SLOTS], in_=w_rows[m].rearrange("p (s j n) -> p s n j", s=N_GPSIMD, j=PACK)
             )
 
         def flip_h(m, part):
             q, pair = part // 2, part % 2
-            if part == 0:
-                h_flipped[m] = h_pool.tile([P, SLOTS, B, PACK], BF16, align_bytes=64, name="h_bf")
-            h_words = h_flipped[m][:, q * HALF : (q + 1) * HALF].bitcast(F32)
+            first = (q * HALF + pair * PAIR) * B * PACK
+            h_words = h_tile(m)[:, first : first + PAIR * B * PACK].bitcast(F32)
             raw_words = h_raws[m][:, :, q].bitcast(F32)
             h_t = psum_t.tile([P, PAIR, 2, B], F32, tag="t")
             for i in range(PAIR):
@@ -248,7 +281,7 @@ def tile_bnn_pb_k_kernel(tc, h0, wm1, wv1, bm1, bv1, we1, be1, out):
                         h_t[:, i, u, :], raw_words[:, pair * PAIR + i, u : K_PASS // 2 : 2], ident_f32[:]
                     )
             nc.scalar.copy(
-                out=h_words[:, pair * PAIR : (pair + 1) * PAIR], in_=h_t[:].rearrange("p i u b -> p i b u")
+                out=h_words.rearrange("p (i b u) -> p i b u", i=PAIR, u=2), in_=h_t[:].rearrange("p i u b -> p i b u")
             )
 
         def quantise(values, kind):
@@ -265,7 +298,7 @@ def tile_bnn_pb_k_kernel(tc, h0, wm1, wv1, bm1, bv1, we1, be1, out):
             w_quantised[m] = quantise(w_tiles[m][:].rearrange("p s n j -> p (s n j)"), "w")
 
         def quantise_h(m):
-            h_quantised[m] = quantise(h_flipped[m][:].rearrange("p s b j -> p (s b j)"), "h")
+            h_quantised[m] = quantise(h_flipped[m][:, 0 : SLOTS * B * PACK], "h")
 
         def matmuls(m):
             h_codes, h_scales = h_quantised[m]
@@ -295,6 +328,11 @@ def tile_bnn_pb_k_kernel(tc, h0, wm1, wv1, bm1, bv1, we1, be1, out):
                 part = result[:, pair * PAIR : (pair + 1) * PAIR, :]
                 nc.vector.tensor_scalar_max(part, part, 0.0)
                 nc.sync.dma_start(out=out_rows[:, first + pair * PAIR : first + (pair + 1) * PAIR, :], in_=part)
+
+        def load_bias():
+            nc.sync.dma_start(out=bias_rows[0:S, :], in_=be1.rearrange("s o n -> (s o) n"))
+            nc.sync.dma_start(out=bias_rows[S : S + 1, :], in_=bv1.unsqueeze(0))
+            nc.sync.dma_start(out=bias_rows[S + 1 : S + 2, :], in_=bm1.unsqueeze(0))
 
         def make_bias_columns():
             bias_cols = psum_t.tile([N, P], BF16, tag="t")
@@ -333,96 +371,92 @@ def tile_bnn_pb_k_kernel(tc, h0, wm1, wv1, bm1, bv1, we1, be1, out):
         nc.scalar.activation(out=warm[:], in_=warm[:], func=ACT.Exp)
 
         load_weights(0)
-        load_weights(1)
         load_h(0)
-        load_weights(2)
+        load_weights(1)
         load_h(1)
+        load_weights(2)
 
         first_std = consts.tile([P, PACK, N], F32)
         nc.scalar.activation(out=first_std[:], in_=raws[0][0][:, 0], func=ACT.Exp, scale=0.5)
-        vector_multiply(0, first_std)
-        flip_shared(0, 0)
-        flip_shared(0, 1)
-        mean_to_psum(0)
-        flip_noise(0, 1)
-        shared_in_sbuf(0)
-        multiply_flipped(0, 1)
-        gpsimd_multiply(0)
-        gpsimd_add(0)
-        vector_add(0)
-        flip_shared(1, 1)
-        flip_noise(1, 1)
-        flip_back(0, 1)
-        flip_shared(1, 0)
-        shared_in_sbuf(1)
-        gpsimd_multiply(1)
-        gpsimd_add(1)
-        multiply_flipped(1, 1)
+        vector_multiply(0, first_std[:])
+        flip_second(0)
+        flip_noise(0)
+        std_in_sbuf(0)
+        vector_add(0, raws[0][1][:])
+        multiply_flipped(0)
+        flip_first(0)
+        vector_multiply(0, std_rows[0][:], q=1, first=N_FLIPPED)
+        flip_first(1)
+        flip_back(0)
         std_to_psum(1)
-        vector_multiply(1)
-        for part in range(4):
+        vector_add(0, mean_rows[0][:], q=1, first=N_FLIPPED)
+        for part in range(2):
+            flip_h(0, part)
+        flip_noise(1)
+        vector_multiply(1, in_psum[1])
+        flip_second(1)
+        for part in range(2, 4):
             flip_h(0, part)
         mean_to_psum(1)
-        flip_back(1, 1)
-        quantise_h(0)
         quantise_w(0)
-        load_weights(3)
+        multiply_flipped(1)
+        quantise_h(0)
+        std_in_sbuf(1)
+        gpsimd_multiply(1)
+        gpsimd_add(1)
         load_h(2)
-        nc.sync.dma_start(out=bias_rows[0:S, :], in_=be1.rearrange("s o n -> (s o) n"))
-        nc.sync.dma_start(out=bias_rows[S : S + 1, :], in_=bv1.unsqueeze(0))
-        nc.sync.dma_start(out=bias_rows[S + 1 : S + 2, :], in_=bm1.unsqueeze(0))
-        shared_in_sbuf(2)
+        load_weights(3)
+        flip_back(1)
+        flip_first(2)
+        flip_second(2)
+        flip_h(1, 0)
+        flip_h(1, 1)
+        std_in_sbuf(2)
         gpsimd_multiply(2)
-        gpsimd_add(2)
-        flip_noise(2, 1)
-        flip_shared(2, 0)
-        flip_shared(2, 1)
-        for part in range(4):
-            flip_h(1, part)
+        flip_noise(2)
+        interleave_rows(1)
 
         for m in range(1, WINDOWS):
-            if m + 3 < WINDOWS:
-                load_weights(m + 3)
             if m + 2 < WINDOWS:
                 load_h(m + 2)
+            if m + 3 < WINDOWS:
+                load_weights(m + 3)
+            if m == BIAS_WINDOW - 2:
+                load_bias()
             more = m + 1 < WINDOWS
             more2 = m + 2 < WINDOWS
             fresh = m + 2 < HALF_WINDOWS
 
-            if fresh:
-                shared_in_sbuf(m + 2)
-            if more and m > 1:
-                flip_noise(m + 1, 1)
-            matmuls(m - 1)
-            if fresh:
-                flip_shared(m + 2, 0)
+            if more:
+                gpsimd_add(m + 1)
             if more2:
+                if fresh:
+                    std_in_sbuf(m + 2)
                 gpsimd_multiply(m + 2)
-            vector_add(m)
+            matmuls(m - 1)
+            vector_add(m, in_psum[m])
+            flip_h(m, 2)
+            flip_h(m, 3)
             if more:
-                multiply_flipped(m + 1, 1)
+                multiply_flipped(m + 1)
                 std_to_psum(m + 1)
-                flip_noise(m + 1, 0)
-                vector_multiply(m + 1)
-                multiply_flipped(m + 1, 0)
-            if fresh:
-                flip_shared(m + 2, 1)
-            if more:
-                flip_back(m + 1, 1)
-            if more:
+                vector_multiply(m + 1, in_psum[m + 1])
+                interleave_rows(m + 1)
+                flip_back(m + 1)
                 flip_h(m + 1, 0)
-            if more:
                 mean_to_psum(m + 1)
-                flip_back(m + 1, 0)
+            if fresh:
+                flip_first(m + 2)
             if more:
-                for part in range(1, 4):
-                    flip_h(m + 1, part)
+                flip_h(m + 1, 1)
+            if fresh:
+                flip_second(m + 2)
+            if more2:
+                flip_noise(m + 2)
             if m == HALF_WINDOWS:
                 finish_half(0)
             quantise_w(m)
             quantise_h(m)
-            if more2:
-                gpsimd_add(m + 2)
 
             if m == BIAS_WINDOW:
                 make_bias_columns()

@@ -47,6 +47,7 @@ def tile_bnn_pb_k_kernel(tc, h0, wm1, wv1, bm1, bv1, we1, be1, out):
         tc.tile_pool(name="raw_e", bufs=3) as raw_e,
         tc.tile_pool(name="raw_h", bufs=3) as raw_h,
         tc.tile_pool(name="products", bufs=1) as products,
+        tc.tile_pool(name="prod_v_pool", bufs=2) as prod_v_pool,
         tc.tile_pool(name="w_pool", bufs=2) as w_pool,
         tc.tile_pool(name="h_pool", bufs=2) as h_pool,
         tc.tile_pool(name="quantised", bufs=2) as quantised,
@@ -77,15 +78,19 @@ def tile_bnn_pb_k_kernel(tc, h0, wm1, wv1, bm1, bv1, we1, be1, out):
             first = (m // HALF_WINDOWS) * HALF
             return slice(first, first + HALF)
 
+        def shared_window(m):
+            return m if m <= HALF_WINDOWS else m - HALF_WINDOWS
+
         def load_weights(m):
             wv_raw = raw_v.tile([P, 2, PACK, N], BF16)
             wm_raw = raw_v.tile([P, PACK, N], BF16)
-            if m < HALF_WINDOWS:
-                mean_rows[m] = kept.tile([P, PACK, N], BF16, name="mean_rows")
+            made = m <= HALF_WINDOWS
+            if made:
+                mean_rows[m] = (kept if m > 0 else consts).tile([P, PACK, N], BF16, name="mean_rows")
             we_raw = raw_e.tile([P, 2, HALF, PACK, N], BF16)
             for q in range(2):
                 c = (2 * m + q) % PASSES
-                if m < HALF_WINDOWS:
+                if made:
                     nc.sync.dma_start(out=wv_raw[:, q], in_=wv_rows[c])
                 pieces = 2 if m == 0 and q == 0 else 1
                 first = samples(m).start
@@ -94,7 +99,7 @@ def tile_bnn_pb_k_kernel(tc, h0, wm1, wv1, bm1, bv1, we1, be1, out):
                     nc.sync.dma_start(
                         out=we_raw[:, q, part], in_=we_rows[c][:, first + part.start : first + part.stop]
                     )
-                if m < HALF_WINDOWS:
+                if made:
                     nc.sync.dma_start(out=(wm_raw if q == 0 else mean_rows[m])[:], in_=wm_rows[c])
             raws[m] = wv_raw, wm_raw, we_raw
 
@@ -144,39 +149,41 @@ def tile_bnn_pb_k_kernel(tc, h0, wm1, wv1, bm1, bv1, we1, be1, out):
             second_flipped[m] = std, mean
 
         def std_to_psum(m):
-            std = first_flipped[m % HALF_WINDOWS][0]
+            std = first_flipped[shared_window(m)][0]
             std_ps = psum_a.tile([P, PACK, N], F32, tag="a")
             for j in range(PACK):
                 nc.tensor.transpose(std_ps[:, j, :], std[:, j * P : (j + 1) * P], ident_f32[:])
             in_psum[m] = std_ps[:]
 
         def mean_to_psum(m):
-            mean = first_flipped[m % HALF_WINDOWS][1]
+            mean = first_flipped[shared_window(m)][1]
             mean_ps = psum_a.tile([P, PACK * WORDS], F32, tag="a")
             for h in range(2):
                 nc.tensor.transpose(mean_ps[:, 2 * WORDS * h : 2 * WORDS * (h + 1)], mean[:, h, :], ident_f32[:])
             in_psum[m] = mean_ps[:].bitcast(BF16).rearrange("p (j n) -> p j n", j=PACK)
 
-        def vector_multiply(m, std_all, q=0, first=0):
+        def vector_multiply(m, std_all, q=0, slots=range(HALF)):
             we_raw = raws[m][2]
-            count = HALF - first
-            prod = products.tile([P, 2, count, N, 2], F32, name="prod_v")
+            first, count = slots.start, len(slots)
+            prod = prod_v_pool.tile([P, 2, count, N, 2], F32, name="prod_v")
             for h in range(2):
                 std = std_all[:, 2 * h : 2 * h + 2, :].rearrange("p i n -> p n i")
                 nc.vector.tensor_tensor(
                     out=prod[:, h],
-                    in0=we_raw[:, q, first:HALF, 2 * h : 2 * h + 2, :].rearrange("p s i n -> p s n i"),
+                    in0=we_raw[:, q, first : first + count, 2 * h : 2 * h + 2, :].rearrange("p s i n -> p s n i"),
                     in1=std.unsqueeze(1).to_broadcast([P, count, N, 2]),
                     op=ALU.mult,
                 )
-            prod_v[m, q] = prod
+            prod_v[m, q, first] = prod
 
-        def vector_add(m, mean_all, q=0, first=0):
-            count = HALF - first
+        def vector_add(m, mean_all, q=0, slots=range(HALF)):
+            first, count = slots.start, len(slots)
             mean = mean_all.rearrange("p (h i) n -> p n h i", h=2)
             nc.vector.tensor_tensor(
-                out=w_tile(m)[:, q * HALF + first : (q + 1) * HALF].rearrange("p s n (h i) -> p s n h i", h=2),
-                in0=prod_v[m, q][:].rearrange("p h s n i -> p s n h i"),
+                out=w_tile(m)[:, q * HALF + first : q * HALF + first + count].rearrange(
+                    "p s n (h i) -> p s n h i", h=2
+                ),
+                in0=prod_v[m, q, first][:].rearrange("p h s n i -> p s n h i"),
                 in1=mean.unsqueeze(1).to_broadcast([P, count, N, 2, 2]),
                 op=ALU.add,
             )
@@ -204,7 +211,7 @@ def tile_bnn_pb_k_kernel(tc, h0, wm1, wv1, bm1, bv1, we1, be1, out):
         def multiply_flipped(m):
             shape = [P, N_FLIPPED, 2 * P * 2]
             noise = noise_flipped[m][:].rearrange("f s h p -> f (s h p)").bitcast(BF16)
-            std = second_flipped[m % HALF_WINDOWS][0][:]
+            std = second_flipped[shared_window(m)][0][:]
             prod = products.tile(shape, F32, name="prod_t")
             nc.vector.tensor_tensor(
                 out=prod[:],
@@ -214,9 +221,9 @@ def tile_bnn_pb_k_kernel(tc, h0, wm1, wv1, bm1, bv1, we1, be1, out):
             )
             prod_t[m] = prod
 
-        def flip_back(m):
-            mean = second_flipped[m % HALF_WINDOWS][1]
-            for s in range(N_FLIPPED):
+        def flip_back(m, slots=range(N_FLIPPED)):
+            mean = second_flipped[shared_window(m)][1]
+            for s in slots:
                 w_ps = psum_t.tile([P, 2, 2, 2 * WORDS], F32, tag="t")
                 for h in range(2):
                     for e in range(2):
@@ -233,7 +240,7 @@ def tile_bnn_pb_k_kernel(tc, h0, wm1, wv1, bm1, bv1, we1, be1, out):
                             out=w_ps[:, e, h, :],
                             lhsT=mean[:, h, e, :],
                             rhs=ident_f32[:],
-                            is_transpose=True,
+                            is_transpose=(h, e) != (s, s),
                             start=False,
                             stop=True,
                         )
@@ -244,7 +251,7 @@ def tile_bnn_pb_k_kernel(tc, h0, wm1, wv1, bm1, bv1, we1, be1, out):
 
         def gpsimd_multiply(m):
             prod = products.tile([P, N_GPSIMD, PACK * N], F32, name="prod_g")
-            std = std_rows[m % HALF_WINDOWS][:].rearrange("p j n -> p (j n)")
+            std = std_rows[shared_window(m)][:].rearrange("p j n -> p (j n)")
             nc.gpsimd.tensor_tensor(
                 out=prod[:],
                 in0=raws[m][2][:, 1, N_FLIPPED:HALF].rearrange("p s j n -> p s (j n)"),
@@ -255,7 +262,7 @@ def tile_bnn_pb_k_kernel(tc, h0, wm1, wv1, bm1, bv1, we1, be1, out):
 
         def gpsimd_add(m):
             rows = h_tile(m)[:, SLOTS * B * PACK :]
-            mean = mean_rows[m % HALF_WINDOWS][:].rearrange("p j n -> p (j n)")
+            mean = mean_rows[shared_window(m)][:].rearrange("p j n -> p (j n)")
             nc.gpsimd.tensor_tensor(
                 out=rows.rearrange("p (s x) -> p s x", s=N_GPSIMD),
                 in0=prod_g[m][:],
@@ -300,24 +307,23 @@ def tile_bnn_pb_k_kernel(tc, h0, wm1, wv1, bm1, bv1, we1, be1, out):
         def quantise_h(m):
             h_quantised[m] = quantise(h_flipped[m][:, 0 : SLOTS * B * PACK], "h")
 
-        def matmuls(m):
+        def matmuls(m, q):
             h_codes, h_scales = h_quantised[m]
             w_codes, w_scales = w_quantised[m]
-            for q in range(2):
-                c = (2 * m + q) % PASSES
-                for s in range(HALF):
-                    slot = q * HALF + s
-                    if c == 0:
-                        banks[s] = psum_acc.tile([B, N], F32, tag="acc%d" % s, name="acc%d" % s)
-                    nc.tensor.matmul_mx(
-                        out=banks[s][:],
-                        lhsT=h_codes[:, slot, :].bitcast(FP8X4),
-                        lhsT_scale=h_scales[:, slot, :],
-                        rhs=w_codes[:, slot, :].bitcast(FP8X4),
-                        rhs_scale=w_scales[:, slot, :],
-                        start=(c == 0),
-                        stop=(c == PASSES - 1),
-                    )
+            c = (2 * m + q) % PASSES
+            for s in range(HALF):
+                slot = q * HALF + s
+                if c == 0:
+                    banks[s] = psum_acc.tile([B, N], F32, tag="acc%d" % s, name="acc%d" % s)
+                nc.tensor.matmul_mx(
+                    out=banks[s][:],
+                    lhsT=h_codes[:, slot, :].bitcast(FP8X4),
+                    lhsT_scale=h_scales[:, slot, :],
+                    rhs=w_codes[:, slot, :].bitcast(FP8X4),
+                    rhs_scale=w_scales[:, slot, :],
+                    start=(c == 0),
+                    stop=(c == PASSES - 1),
+                )
 
         def finish_half(half):
             first = half * HALF
@@ -376,45 +382,44 @@ def tile_bnn_pb_k_kernel(tc, h0, wm1, wv1, bm1, bv1, we1, be1, out):
         load_h(1)
         load_weights(2)
 
-        first_std = consts.tile([P, PACK, N], F32)
-        nc.scalar.activation(out=first_std[:], in_=raws[0][0][:, 0], func=ACT.Exp, scale=0.5)
-        vector_multiply(0, first_std[:])
-        flip_second(0)
-        flip_noise(0)
-        std_in_sbuf(0)
-        vector_add(0, raws[0][1][:])
-        multiply_flipped(0)
-        flip_first(0)
-        vector_multiply(0, std_rows[0][:], q=1, first=N_FLIPPED)
-        flip_first(1)
-        flip_back(0)
-        std_to_psum(1)
-        vector_add(0, mean_rows[0][:], q=1, first=N_FLIPPED)
+        first_std = consts.tile([P, 2, PACK, N], F32)
+        for q in range(2):
+            nc.scalar.activation(out=first_std[:, q], in_=raws[0][0][:, q], func=ACT.Exp, scale=0.5)
+        wm_raw = raws[0][1]
+        for slots in (range(0, PAIR), range(PAIR, HALF)):
+            vector_multiply(0, first_std[:, 0], slots=slots)
+        vector_add(0, wm_raw[:], slots=range(0, PAIR))
+        vector_multiply(0, first_std[:, 1], q=1)
+        vector_add(0, wm_raw[:], slots=range(PAIR, HALF))
+        vector_add(0, mean_rows[0][:], q=1)
         for part in range(2):
             flip_h(0, part)
-        flip_noise(1)
-        vector_multiply(1, in_psum[1])
-        flip_second(1)
-        for part in range(2, 4):
-            flip_h(0, part)
-        mean_to_psum(1)
+        flip_first(1)
+        flip_h(0, 2)
+        flip_h(0, 3)
+        std_to_psum(1)
         quantise_w(0)
-        multiply_flipped(1)
         quantise_h(0)
+        flip_second(1)
+        flip_noise(1)
+        multiply_flipped(1)
         std_in_sbuf(1)
+        matmuls(0, 0)
         gpsimd_multiply(1)
+        vector_multiply(1, in_psum[1])
+        flip_back(1)
+        mean_to_psum(1)
+        flip_h(1, 0)
+        flip_first(2)
         gpsimd_add(1)
         load_h(2)
         load_weights(3)
-        flip_back(1)
-        flip_first(2)
-        flip_second(2)
-        flip_h(1, 0)
-        flip_h(1, 1)
         std_in_sbuf(2)
-        gpsimd_multiply(2)
+        flip_second(2)
         flip_noise(2)
         interleave_rows(1)
+        gpsimd_multiply(2)
+        flip_h(1, 1)
 
         for m in range(1, WINDOWS):
             if m + 2 < WINDOWS:
@@ -425,7 +430,7 @@ def tile_bnn_pb_k_kernel(tc, h0, wm1, wv1, bm1, bv1, we1, be1, out):
                 load_bias()
             more = m + 1 < WINDOWS
             more2 = m + 2 < WINDOWS
-            fresh = m + 2 < HALF_WINDOWS
+            fresh = m + 2 <= HALF_WINDOWS
 
             if more:
                 gpsimd_add(m + 1)
@@ -433,7 +438,6 @@ def tile_bnn_pb_k_kernel(tc, h0, wm1, wv1, bm1, bv1, we1, be1, out):
                 if fresh:
                     std_in_sbuf(m + 2)
                 gpsimd_multiply(m + 2)
-            matmuls(m - 1)
             vector_add(m, in_psum[m])
             flip_h(m, 2)
             flip_h(m, 3)
@@ -445,23 +449,25 @@ def tile_bnn_pb_k_kernel(tc, h0, wm1, wv1, bm1, bv1, we1, be1, out):
                 flip_back(m + 1)
                 flip_h(m + 1, 0)
                 mean_to_psum(m + 1)
+            if m in (HALF_WINDOWS, HALF_WINDOWS + 1):
+                spread_bias(m - HALF_WINDOWS)
+            matmuls(m - 1, 1)
             if fresh:
                 flip_first(m + 2)
             if more:
                 flip_h(m + 1, 1)
             if fresh:
                 flip_second(m + 2)
+            if m == HALF_WINDOWS - 2:
+                make_bias_columns()
             if more2:
                 flip_noise(m + 2)
             if m == HALF_WINDOWS:
                 finish_half(0)
             quantise_w(m)
             quantise_h(m)
+            matmuls(m, 0)
 
-            if m == BIAS_WINDOW:
-                make_bias_columns()
-            if m in (BIAS_WINDOW + 1, BIAS_WINDOW + 2):
-                spread_bias(m - BIAS_WINDOW - 1)
 
-        matmuls(WINDOWS - 1)
+        matmuls(WINDOWS - 1, 1)
         finish_half(1)

@@ -221,32 +221,39 @@ def tile_bnn_pb_k_kernel(tc, h0, wm1, wv1, bm1, bv1, we1, be1, out):
             )
             prod_t[m] = prod
 
-        def flip_back(m, slots=range(N_FLIPPED)):
+        def flip_back(m, s, add_mean=True):
+            w_ps = psum_t.tile([P, 2, 2, 2 * WORDS], F32, tag="t")
             mean = second_flipped[shared_window(m)][1]
-            for s in slots:
-                w_ps = psum_t.tile([P, 2, 2, 2 * WORDS], F32, tag="t")
-                for h in range(2):
-                    for e in range(2):
-                        first = h * 2 * P + e
-                        nc.tensor.matmul(
-                            out=w_ps[:, e, h, :],
-                            lhsT=prod_t[m][:, s, first : first + 2 * P - 1 : 2],
-                            rhs=ident_f32[:],
-                            is_transpose=True,
-                            start=True,
-                            stop=False,
-                        )
+            for h in range(2):
+                for e in range(2):
+                    first = h * 2 * P + e
+                    nc.tensor.matmul(
+                        out=w_ps[:, e, h, :],
+                        lhsT=prod_t[m][:, s, first : first + 2 * P - 1 : 2],
+                        rhs=ident_f32[:],
+                        is_transpose=True,
+                        start=True,
+                        stop=not add_mean,
+                    )
+                    if add_mean:
                         nc.tensor.matmul(
                             out=w_ps[:, e, h, :],
                             lhsT=mean[:, h, e, :],
                             rhs=ident_f32[:],
-                            is_transpose=(h, e) != (s, s),
+                            is_transpose=True,
                             start=False,
                             stop=True,
                         )
-                nc.scalar.copy(
-                    out=w_tile(m)[:, HALF + s].rearrange("p (v e) j -> p v e j", e=2),
-                    in_=w_ps[:].rearrange("p e h (i v) -> p v e (h i)", i=2),
+            w_slot = w_tile(m)[:, HALF + s].rearrange("p (v e) j -> p v e j", e=2)
+            w_sums = w_ps[:].rearrange("p e h (i v) -> p v e (h i)", i=2)
+            if add_mean:
+                nc.scalar.copy(out=w_slot, in_=w_sums)
+            else:
+                nc.vector.tensor_tensor(
+                    out=w_slot,
+                    in0=w_sums,
+                    in1=mean_rows[shared_window(m)][:].rearrange("p j (v e) -> p v e j", e=2),
+                    op=ALU.add,
                 )
 
         def gpsimd_multiply(m):
@@ -405,9 +412,11 @@ def tile_bnn_pb_k_kernel(tc, h0, wm1, wv1, bm1, bv1, we1, be1, out):
         multiply_flipped(1)
         std_in_sbuf(1)
         matmuls(0, 0)
+        matmuls(0, 1)
         gpsimd_multiply(1)
         vector_multiply(1, in_psum[1])
-        flip_back(1)
+        flip_back(1, 0, False)
+        flip_back(1, 1)
         mean_to_psum(1)
         flip_h(1, 0)
         flip_first(2)
@@ -420,6 +429,7 @@ def tile_bnn_pb_k_kernel(tc, h0, wm1, wv1, bm1, bv1, we1, be1, out):
         interleave_rows(1)
         gpsimd_multiply(2)
         flip_h(1, 1)
+        flip_h(1, 2)
 
         for m in range(1, WINDOWS):
             if m + 2 < WINDOWS:
@@ -434,28 +444,31 @@ def tile_bnn_pb_k_kernel(tc, h0, wm1, wv1, bm1, bv1, we1, be1, out):
 
             if more:
                 gpsimd_add(m + 1)
-            if more2:
-                if fresh:
-                    std_in_sbuf(m + 2)
-                gpsimd_multiply(m + 2)
             vector_add(m, in_psum[m])
-            flip_h(m, 2)
-            flip_h(m, 3)
+            if fresh:
+                std_in_sbuf(m + 2)
+            if more2:
+                gpsimd_multiply(m + 2)
+            if more:
+                flip_h(m, 3)
             if more:
                 multiply_flipped(m + 1)
                 std_to_psum(m + 1)
                 vector_multiply(m + 1, in_psum[m + 1])
                 interleave_rows(m + 1)
-                flip_back(m + 1)
+                flip_back(m + 1, 0, add_mean=m + 1 > HALF_WINDOWS)
+                flip_back(m + 1, 1)
                 flip_h(m + 1, 0)
                 mean_to_psum(m + 1)
-            if m in (HALF_WINDOWS, HALF_WINDOWS + 1):
-                spread_bias(m - HALF_WINDOWS)
-            matmuls(m - 1, 1)
+            if m in (HALF_WINDOWS - 1, HALF_WINDOWS + 1):
+                spread_bias(m // HALF_WINDOWS)
             if fresh:
                 flip_first(m + 2)
             if more:
                 flip_h(m + 1, 1)
+                flip_h(m + 1, 2)
+            if m + 2 == WINDOWS:
+                flip_h(m + 1, 3)
             if fresh:
                 flip_second(m + 2)
             if m == HALF_WINDOWS - 2:
@@ -464,10 +477,10 @@ def tile_bnn_pb_k_kernel(tc, h0, wm1, wv1, bm1, bv1, we1, be1, out):
                 flip_noise(m + 2)
             if m == HALF_WINDOWS:
                 finish_half(0)
-            quantise_w(m)
             quantise_h(m)
+            quantise_w(m)
             matmuls(m, 0)
+            matmuls(m, 1)
 
 
-        matmuls(WINDOWS - 1, 1)
         finish_half(1)

@@ -153,32 +153,30 @@ def tile_bnn_pb_k_kernel(tc, h0, wm1, wv1, bm1, bv1, we1, be1, out):
             std_ps = psum_a.tile([P, PACK, N], F32, tag="a")
             for j in range(PACK):
                 nc.tensor.transpose(std_ps[:, j, :], std[:, j * P : (j + 1) * P], ident_f32[:])
-            in_psum[m] = std_ps[:]
+            in_psum[m] = std_ps[:].rearrange("p (h i) n -> p h n i", h=2)
 
         def mean_to_psum(m):
             mean = first_flipped[shared_window(m)][1]
             mean_ps = psum_a.tile([P, PACK * WORDS], F32, tag="a")
             for h in range(2):
                 nc.tensor.transpose(mean_ps[:, 2 * WORDS * h : 2 * WORDS * (h + 1)], mean[:, h, :], ident_f32[:])
-            in_psum[m] = mean_ps[:].bitcast(BF16).rearrange("p (j n) -> p j n", j=PACK)
+            in_psum[m] = mean_ps[:].bitcast(BF16).rearrange("p (h i n) -> p n h i", h=2, i=2)
 
-        def vector_multiply(m, std_all, q=0, slots=range(HALF)):
+        def vector_multiply(m, std, q=0, slots=range(HALF)):
             we_raw = raws[m][2]
             first, count = slots.start, len(slots)
             prod = prod_v_pool.tile([P, 2, count, N, 2], F32, name="prod_v")
             for h in range(2):
-                std = std_all[:, 2 * h : 2 * h + 2, :].rearrange("p i n -> p n i")
                 nc.vector.tensor_tensor(
                     out=prod[:, h],
                     in0=we_raw[:, q, first : first + count, 2 * h : 2 * h + 2, :].rearrange("p s i n -> p s n i"),
-                    in1=std.unsqueeze(1).to_broadcast([P, count, N, 2]),
+                    in1=std[:, h].unsqueeze(1).to_broadcast([P, count, N, 2]),
                     op=ALU.mult,
                 )
             prod_v[m, q, first] = prod
 
-        def vector_add(m, mean_all, q=0, slots=range(HALF)):
+        def vector_add(m, mean, q=0, slots=range(HALF)):
             first, count = slots.start, len(slots)
-            mean = mean_all.rearrange("p (h i) n -> p n h i", h=2)
             nc.vector.tensor_tensor(
                 out=w_tile(m)[:, q * HALF + first : q * HALF + first + count].rearrange(
                     "p s n (h i) -> p s n h i", h=2
@@ -314,23 +312,24 @@ def tile_bnn_pb_k_kernel(tc, h0, wm1, wv1, bm1, bv1, we1, be1, out):
         def quantise_h(m):
             h_quantised[m] = quantise(h_flipped[m][:, 0 : SLOTS * B * PACK], "h")
 
-        def matmuls(m, q):
+        def matmuls(m):
             h_codes, h_scales = h_quantised[m]
             w_codes, w_scales = w_quantised[m]
-            c = (2 * m + q) % PASSES
             for s in range(HALF):
-                slot = q * HALF + s
-                if c == 0:
-                    banks[s] = psum_acc.tile([B, N], F32, tag="acc%d" % s, name="acc%d" % s)
-                nc.tensor.matmul_mx(
-                    out=banks[s][:],
-                    lhsT=h_codes[:, slot, :].bitcast(FP8X4),
-                    lhsT_scale=h_scales[:, slot, :],
-                    rhs=w_codes[:, slot, :].bitcast(FP8X4),
-                    rhs_scale=w_scales[:, slot, :],
-                    start=(c == 0),
-                    stop=(c == PASSES - 1),
-                )
+                for q in range(2):
+                    c = (2 * m + q) % PASSES
+                    slot = q * HALF + s
+                    if c == 0:
+                        banks[s] = psum_acc.tile([B, N], F32, tag="acc%d" % s, name="acc%d" % s)
+                    nc.tensor.matmul_mx(
+                        out=banks[s][:],
+                        lhsT=h_codes[:, slot, :].bitcast(FP8X4),
+                        lhsT_scale=h_scales[:, slot, :],
+                        rhs=w_codes[:, slot, :].bitcast(FP8X4),
+                        rhs_scale=w_scales[:, slot, :],
+                        start=(c == 0),
+                        stop=(c == PASSES - 1),
+                    )
 
         def finish_half(half):
             first = half * HALF
@@ -389,16 +388,19 @@ def tile_bnn_pb_k_kernel(tc, h0, wm1, wv1, bm1, bv1, we1, be1, out):
         load_h(1)
         load_weights(2)
 
-        first_std = consts.tile([P, 2, PACK, N], F32)
+        first_std = consts.tile([P, 2, 2, N, 2], F32)
+        first_mean = consts.tile([P, 2, N, 2, 2], BF16)
         for q in range(2):
-            nc.scalar.activation(out=first_std[:, q], in_=raws[0][0][:, q], func=ACT.Exp, scale=0.5)
-        wm_raw = raws[0][1]
+            wv_pairs = raws[0][0][:, q].rearrange("p (h i) n -> p h n i", h=2)
+            nc.scalar.activation(out=first_std[:, q], in_=wv_pairs, func=ACT.Exp, scale=0.5)
+            wm_rows_q = (raws[0][1] if q == 0 else mean_rows[0])[:]
+            nc.scalar.copy(out=first_mean[:, q], in_=wm_rows_q.rearrange("p (h i) n -> p n h i", h=2))
         for slots in (range(0, PAIR), range(PAIR, HALF)):
             vector_multiply(0, first_std[:, 0], slots=slots)
-        vector_add(0, wm_raw[:], slots=range(0, PAIR))
+        vector_add(0, first_mean[:, 0], slots=range(0, PAIR))
         vector_multiply(0, first_std[:, 1], q=1)
-        vector_add(0, wm_raw[:], slots=range(PAIR, HALF))
-        vector_add(0, mean_rows[0][:], q=1)
+        vector_add(0, first_mean[:, 0], slots=range(PAIR, HALF))
+        vector_add(0, first_mean[:, 1], q=1)
         for part in range(2):
             flip_h(0, part)
         flip_first(1)
@@ -411,8 +413,7 @@ def tile_bnn_pb_k_kernel(tc, h0, wm1, wv1, bm1, bv1, we1, be1, out):
         flip_noise(1)
         multiply_flipped(1)
         std_in_sbuf(1)
-        matmuls(0, 0)
-        matmuls(0, 1)
+        matmuls(0)
         gpsimd_multiply(1)
         vector_multiply(1, in_psum[1])
         flip_back(1, 0, False)
@@ -479,8 +480,7 @@ def tile_bnn_pb_k_kernel(tc, h0, wm1, wv1, bm1, bv1, we1, be1, out):
                 finish_half(0)
             quantise_h(m)
             quantise_w(m)
-            matmuls(m, 0)
-            matmuls(m, 1)
+            matmuls(m)
 
 
         finish_half(1)

@@ -22,7 +22,6 @@ HALF = 4
 PAIR = 2
 WINDOWS = (S // HALF) * PASSES // 2
 HALF_WINDOWS = PASSES // 2
-BIAS_WINDOW = HALF_WINDOWS - 4
 SLOTS = 2 * HALF
 N_FLIPPED = 2
 N_GPSIMD = HALF - N_FLIPPED
@@ -213,8 +212,8 @@ def tile_bnn_pb_k_kernel(tc, h0, wm1, wv1, bm1, bv1, we1, be1, out):
             prod = products.tile(shape, F32, name="prod_t")
             nc.vector.tensor_tensor(
                 out=prod[:],
-                in0=noise.rearrange("f (s x) -> f s x", s=N_FLIPPED),
-                in1=std.unsqueeze(1).to_broadcast(shape),
+                in0=std.unsqueeze(1).to_broadcast(shape),
+                in1=noise.rearrange("f (s x) -> f s x", s=N_FLIPPED),
                 op=ALU.mult,
             )
             prod_t[m] = prod
@@ -249,8 +248,8 @@ def tile_bnn_pb_k_kernel(tc, h0, wm1, wv1, bm1, bv1, we1, be1, out):
             else:
                 nc.vector.tensor_tensor(
                     out=w_slot,
-                    in0=w_sums,
-                    in1=mean_rows[shared_window(m)][:].rearrange("p j (v e) -> p v e j", e=2),
+                    in0=mean_rows[shared_window(m)][:].rearrange("p j (v e) -> p v e j", e=2),
+                    in1=w_sums,
                     op=ALU.add,
                 )
 
@@ -335,7 +334,7 @@ def tile_bnn_pb_k_kernel(tc, h0, wm1, wv1, bm1, bv1, we1, be1, out):
             first = half * HALF
             result = consts.tile([B, HALF, N], F32, name="result%d" % half)
             for s in range(HALF):
-                nc.vector.tensor_tensor(out=result[:, s, :], in0=banks[s][:], in1=b1_all[:, first + s, :], op=ALU.add)
+                nc.vector.tensor_tensor(out=result[:, s, :], in0=b1_all[:, first + s, :], in1=banks[s][:], op=ALU.add)
             for pair in range(HALF // PAIR):
                 part = result[:, pair * PAIR : (pair + 1) * PAIR, :]
                 nc.vector.tensor_scalar_max(part, part, 0.0)
@@ -415,21 +414,21 @@ def tile_bnn_pb_k_kernel(tc, h0, wm1, wv1, bm1, bv1, we1, be1, out):
         std_in_sbuf(1)
         matmuls(0)
         gpsimd_multiply(1)
-        vector_multiply(1, in_psum[1])
-        flip_back(1, 0, False)
-        flip_back(1, 1)
-        mean_to_psum(1)
-        flip_h(1, 0)
-        flip_first(2)
         gpsimd_add(1)
-        load_h(2)
         load_weights(3)
+        load_h(2)
+        vector_multiply(1, in_psum[1])
+        flip_back(1, 0)
+        flip_back(1, 1)
         std_in_sbuf(2)
+        gpsimd_multiply(2)
+        flip_h(1, 0)
+        mean_to_psum(1)
         flip_second(2)
         flip_noise(2)
-        interleave_rows(1)
-        gpsimd_multiply(2)
         flip_h(1, 1)
+        flip_first(2)
+        interleave_rows(1)
         flip_h(1, 2)
 
         for m in range(1, WINDOWS):
@@ -437,7 +436,7 @@ def tile_bnn_pb_k_kernel(tc, h0, wm1, wv1, bm1, bv1, we1, be1, out):
                 load_h(m + 2)
             if m + 3 < WINDOWS:
                 load_weights(m + 3)
-            if m == BIAS_WINDOW - 2:
+            if m == HALF_WINDOWS - 3:
                 load_bias()
             more = m + 1 < WINDOWS
             more2 = m + 2 < WINDOWS
@@ -457,7 +456,7 @@ def tile_bnn_pb_k_kernel(tc, h0, wm1, wv1, bm1, bv1, we1, be1, out):
                 std_to_psum(m + 1)
                 vector_multiply(m + 1, in_psum[m + 1])
                 interleave_rows(m + 1)
-                flip_back(m + 1, 0, add_mean=m + 1 > HALF_WINDOWS)
+                flip_back(m + 1, 0)
                 flip_back(m + 1, 1)
                 flip_h(m + 1, 0)
                 mean_to_psum(m + 1)

import concourse.mybir as mybir
from concourse.masks import make_identity

F32 = mybir.dt.float32
BF16 = mybir.dt.bfloat16
U32 = mybir.dt.uint32
U8 = mybir.dt.uint8
FP8X4 = mybir.dt.float8_e4m3fn_x4
ACT = mybir.ActivationFunctionType
ALU = mybir.AluOpType

S = 8
B = 128
K = 8192
N = 128

P = 128
PACK = 4
K_PASS = P * PACK
PASSES = K // K_PASS
HALF = 4
PAIR = 2
WINDOWS = (S // HALF) * PASSES // 2
HALF_WINDOWS = PASSES // 2
SLOTS = 2 * HALF
N_FLIPPED = 2
N_GPSIMD = HALF - N_FLIPPED
WORDS = N // 2

FLOPS = 2 * S * B * K * N


def tile_bnn_pb_k_kernel(tc, h0, wm1, wv1, bm1, bv1, we1, be1, out):
    nc = tc.nc

    wv_rows = wv1.rearrange("(c p j) n -> c p j n", p=P, j=PACK)
    wm_rows = wm1.rearrange("(c p j) n -> c p j n", p=P, j=PACK)
    we_rows = we1.rearrange("s (c p j) n -> c p s j n", p=P, j=PACK)
    h_rows = h0.rearrange("s b k -> b s k")
    out_rows = out.rearrange("s b n -> b s n")

    with (
        tc.tile_pool(name="consts", bufs=1) as consts,
        tc.tile_pool(name="kept", bufs=HALF_WINDOWS) as kept,
        tc.tile_pool(name="raw_v", bufs=3) as raw_v,
        tc.tile_pool(name="raw_e", bufs=3) as raw_e,
        tc.tile_pool(name="raw_h", bufs=3) as raw_h,
        tc.tile_pool(name="products", bufs=1) as products,
        tc.tile_pool(name="prod_v_pool", bufs=2) as prod_v_pool,
        tc.tile_pool(name="w_pool", bufs=2) as w_pool,
        tc.tile_pool(name="h_pool", bufs=2) as h_pool,
        tc.tile_pool(name="quantised", bufs=2) as quantised,
        tc.psum_pool(name="psum_t", bufs=3) as psum_t,
        tc.psum_pool(name="psum_a", bufs=1) as psum_a,
        tc.psum_pool(name="psum_acc", bufs=1) as psum_acc,
        tc.manual_schedule(),
    ):
        raws = {}
        h_raws = {}
        first_flipped = {}
        second_flipped = {}
        std_rows = {}
        mean_rows = {}
        w_rows = {}
        in_psum = {}
        noise_flipped = {}
        prod_v = {}
        prod_t = {}
        prod_g = {}
        h_flipped = {}
        w_tiles = {}
        h_quantised = {}
        w_quantised = {}
        banks = {}

        def samples(m):
            first = (m // HALF_WINDOWS) * HALF
            return slice(first, first + HALF)

        def shared_window(m):
            return m if m <= HALF_WINDOWS else m - HALF_WINDOWS

        def load_weights(m):
            wv_raw = raw_v.tile([P, 2, PACK, N], BF16)
            wm_raw = raw_v.tile([P, PACK, N], BF16)
            made = m <= HALF_WINDOWS
            if made:
                mean_rows[m] = (kept if m > 0 else consts).tile([P, PACK, N], BF16, name="mean_rows")
            we_raw = raw_e.tile([P, 2, HALF, PACK, N], BF16)
            for q in range(2):
                c = (2 * m + q) % PASSES
                if made:
                    nc.sync.dma_start(out=wv_raw[:, q], in_=wv_rows[c])
                pieces = 2 if m == 0 and q == 0 else 1
                first = samples(m).start
                for i in range(pieces):
                    part = slice(i * HALF // pieces, (i + 1) * HALF // pieces)
                    nc.sync.dma_start(
                        out=we_raw[:, q, part], in_=we_rows[c][:, first + part.start : first + part.stop]
                    )
                if made:
                    nc.sync.dma_start(out=(wm_raw if q == 0 else mean_rows[m])[:], in_=wm_rows[c])
            raws[m] = wv_raw, wm_raw, we_raw

        def load_h(m):
            c = (2 * m) % PASSES
            h_raw = raw_h.tile([B, HALF, 2, K_PASS], BF16)
            nc.sync.dma_start(
                out=h_raw[:].rearrange("b s q k -> b s (q k)"),
                in_=h_rows[:, samples(m), c * K_PASS : (c + 2) * K_PASS],
            )
            h_raws[m] = h_raw

        def std_in_sbuf(m):
            std = kept.tile([P, PACK, N], F32, name="std_rows")
            nc.scalar.activation(out=std[:], in_=raws[m][0][:, 1], func=ACT.Exp, scale=0.5)
            std_rows[m] = std

        def words_of(rows, h):
            return rows.rearrange("p j n -> p (j n)").bitcast(F32)[:, 2 * WORDS * h : 2 * WORDS * (h + 1)]

        def flip_first(m):
            wv_raw, wm_raw, we_raw = raws[m]
            flipped = psum_t.tile([P, 2, 2, P], F32, tag="t")
            wv_flipped = flipped[:, 0].rearrange("n h p -> n (h p)").bitcast(BF16)
            for j in range(PACK):
                nc.tensor.transpose(wv_flipped[:, j * P : (j + 1) * P], wv_raw[:, 0, j, :], ident_bf[:])
            for h in range(2):
                nc.tensor.transpose(flipped[:, 1, h, :], words_of(wm_raw[:], h), ident_f32[:])
            std = kept.tile([N, PACK * P], F32, name="std0")
            nc.scalar.activation(out=std[:], in_=wv_flipped, func=ACT.Exp, scale=0.5)
            mean = kept.tile([P, 2, P], F32, name="mean0")
            nc.scalar.copy(out=mean[:], in_=flipped[:, 1])
            first_flipped[m] = std, mean

        def flip_second(m):
            wv_raw, wm_raw, we_raw = raws[m]
            flipped = psum_t.tile([P, 2, 2, P], F32, tag="t")
            for i, rows in enumerate((wv_raw[:, 1], mean_rows[m][:])):
                for h in range(2):
                    nc.tensor.transpose(flipped[:, i, h, :], words_of(rows, h), ident_f32[:])
            wv_flipped = flipped[:, 0].rearrange("f h p -> f (h p)").bitcast(BF16)
            wm_flipped = flipped[:, 1].rearrange("f h p -> f (h p)").bitcast(BF16)
            std = kept.tile([P, 2 * P * 2], F32, name="std1")
            nc.scalar.activation(out=std[:], in_=wv_flipped, func=ACT.Exp, scale=0.5)
            mean = kept.tile([P, 2, 2, P], F32, name="mean1")
            nc.scalar.copy(out=mean[:], in_=wm_flipped.rearrange("f (h p e) -> f h e p", h=2, e=2))
            second_flipped[m] = std, mean

        def std_to_psum(m):
            std = first_flipped[shared_window(m)][0]
            std_ps = psum_a.tile([P, PACK, N], F32, tag="a")
            for j in range(PACK):
                nc.tensor.transpose(std_ps[:, j, :], std[:, j * P : (j + 1) * P], ident_f32[:])
            in_psum[m] = std_ps[:].rearrange("p (h i) n -> p h n i", h=2)

        def mean_to_psum(m):
            mean = first_flipped[shared_window(m)][1]
            mean_ps = psum_a.tile([P, PACK * WORDS], F32, tag="a")
            for h in range(2):
                nc.tensor.transpose(mean_ps[:, 2 * WORDS * h : 2 * WORDS * (h + 1)], mean[:, h, :], ident_f32[:])
            in_psum[m] = mean_ps[:].bitcast(BF16).rearrange("p (h i n) -> p n h i", h=2, i=2)

        def vector_multiply(m, std, q=0, slots=range(HALF)):
            we_raw = raws[m][2]
            first, count = slots.start, len(slots)
            prod = prod_v_pool.tile([P, 2, count, N, 2], F32, name="prod_v")
            for h in range(2):
                nc.vector.tensor_tensor(
                    out=prod[:, h],
                    in0=we_raw[:, q, first : first + count, 2 * h : 2 * h + 2, :].rearrange("p s i n -> p s n i"),
                    in1=std[:, h].unsqueeze(1).to_broadcast([P, count, N, 2]),
                    op=ALU.mult,
                )
            prod_v[m, q, first] = prod

        def vector_add(m, mean, q=0, slots=range(HALF)):
            first, count = slots.start, len(slots)
            nc.vector.tensor_tensor(
                out=w_tile(m)[:, q * HALF + first : q * HALF + first + count].rearrange(
                    "p s n (h i) -> p s n h i", h=2
                ),
                in0=prod_v[m, q, first][:].rearrange("p h s n i -> p s n h i"),
                in1=mean.unsqueeze(1).to_broadcast([P, count, N, 2, 2]),
                op=ALU.add,
            )

        def h_tile(m):
            if m not in h_flipped:
                h_flipped[m] = h_pool.tile(
                    [P, SLOTS * B * PACK + N_GPSIMD * PACK * N], BF16, align_bytes=64, name="h_bf"
                )
            return h_flipped[m]

        def w_tile(m):
            if m not in w_tiles:
                w_tiles[m] = w_pool.tile([P, SLOTS, N, PACK], BF16, align_bytes=64, name="w_bf")
            return w_tiles[m]

        def flip_noise(m):
            we_raw = raws[m][2]
            flipped = psum_t.tile([P, N_FLIPPED, 2, P], F32, tag="t")
            for s in range(N_FLIPPED):
                for h in range(2):
                    nc.tensor.transpose(flipped[:, s, h, :], words_of(we_raw[:, 1, s], h), ident_f32[:])
            noise_flipped[m] = flipped

        def multiply_flipped(m):
            shape = [P, N_FLIPPED, 2 * P * 2]
            noise = noise_flipped[m][:].rearrange("f s h p -> f (s h p)").bitcast(BF16)
            std = second_flipped[shared_window(m)][0][:]
            prod = products.tile(shape, F32, name="prod_t")
            nc.vector.tensor_tensor(
                out=prod[:],
                in0=std.unsqueeze(1).to_broadcast(shape),
                in1=noise.rearrange("f (s x) -> f s x", s=N_FLIPPED),
                op=ALU.mult,
            )
            prod_t[m] = prod

        def flip_back(m, s, add_mean=True):
            w_ps = psum_t.tile([P, 2, 2, 2 * WORDS], F32, tag="t")
            mean = second_flipped[shared_window(m)][1]
            for h in range(2):
                for e in range(2):
                    first = h * 2 * P + e
                    nc.tensor.matmul(
                        out=w_ps[:, e, h, :],
                        lhsT=prod_t[m][:, s, first : first + 2 * P - 1 : 2],
                        rhs=ident_f32[:],
                        is_transpose=True,
                        start=True,
                        stop=not add_mean,
                    )
                    if add_mean:
                        nc.tensor.matmul(
                            out=w_ps[:, e, h, :],
                            lhsT=mean[:, h, e, :],
                            rhs=ident_f32[:],
                            is_transpose=True,
                            start=False,
                            stop=True,
                        )
            w_slot = w_tile(m)[:, HALF + s].rearrange("p (v e) j -> p v e j", e=2)
            w_sums = w_ps[:].rearrange("p e h (i v) -> p v e (h i)", i=2)
            if add_mean:
                nc.scalar.copy(out=w_slot, in_=w_sums)
            else:
                nc.vector.tensor_tensor(
                    out=w_slot,
                    in0=mean_rows[shared_window(m)][:].rearrange("p j (v e) -> p v e j", e=2),
                    in1=w_sums,
                    op=ALU.add,
                )

        def gpsimd_multiply(m):
            prod = products.tile([P, N_GPSIMD, PACK * N], F32, name="prod_g")
            std = std_rows[shared_window(m)][:].rearrange("p j n -> p (j n)")
            nc.gpsimd.tensor_tensor(
                out=prod[:],
                in0=raws[m][2][:, 1, N_FLIPPED:HALF].rearrange("p s j n -> p s (j n)"),
                in1=std.unsqueeze(1).to_broadcast([P, N_GPSIMD, PACK * N]),
                op=ALU.mult,
            )
            prod_g[m] = prod

        def gpsimd_add(m):
            rows = h_tile(m)[:, SLOTS * B * PACK :]
            mean = mean_rows[shared_window(m)][:].rearrange("p j n -> p (j n)")
            nc.gpsimd.tensor_tensor(
                out=rows.rearrange("p (s x) -> p s x", s=N_GPSIMD),
                in0=prod_g[m][:],
                in1=mean.unsqueeze(1).to_broadcast([P, N_GPSIMD, PACK * N]),
                op=ALU.add,
            )
            w_rows[m] = rows

        def interleave_rows(m):
            nc.scalar.copy(
                out=w_tile(m)[:, SLOTS - N_GPSIMD : SLOTS], in_=w_rows[m].rearrange("p (s j n) -> p s n j", s=N_GPSIMD, j=PACK)
            )

        def flip_h(m, part):
            q, pair = part // 2, part % 2
            first = (q * HALF + pair * PAIR) * B * PACK
            h_words = h_tile(m)[:, first : first + PAIR * B * PACK].bitcast(F32)
            raw_words = h_raws[m][:, :, q].bitcast(F32)
            h_t = psum_t.tile([P, PAIR, 2, B], F32, tag="t")
            for i in range(PAIR):
                for u in range(2):
                    nc.tensor.transpose(
                        h_t[:, i, u, :], raw_words[:, pair * PAIR + i, u : K_PASS // 2 : 2], ident_f32[:]
                    )
            nc.scalar.copy(
                out=h_words.rearrange("p (i b u) -> p i b u", i=PAIR, u=2), in_=h_t[:].rearrange("p i u b -> p i b u")
            )

        def quantise(values, kind):
            codes = quantised.tile([P, SLOTS, P], U32, align_bytes=64, tag=kind + "_codes")
            scales = quantised.tile([P, SLOTS, P], U8, align_bytes=64, tag=kind + "_scales")
            nc.vector.quantize_mx(
                out=codes[:].rearrange("p s m -> p (s m)").bitcast(FP8X4),
                scales=scales[:].rearrange("p s m -> p (s m)"),
                in_=values,
            )
            return codes, scales

        def quantise_w(m):
            w_quantised[m] = quantise(w_tiles[m][:].rearrange("p s n j -> p (s n j)"), "w")

        def quantise_h(m):
            h_quantised[m] = quantise(h_flipped[m][:, 0 : SLOTS * B * PACK], "h")

        def matmuls(m):
            h_codes, h_scales = h_quantised[m]
            w_codes, w_scales = w_quantised[m]
            for s in range(HALF):
                for q in range(2):
                    c = (2 * m + q) % PASSES
                    slot = q * HALF + s
                    if c == 0:
                        banks[s] = psum_acc.tile([B, N], F32, tag="acc%d" % s, name="acc%d" % s)
                    nc.tensor.matmul_mx(
                        out=banks[s][:],
                        lhsT=h_codes[:, slot, :].bitcast(FP8X4),
                        lhsT_scale=h_scales[:, slot, :],
                        rhs=w_codes[:, slot, :].bitcast(FP8X4),
                        rhs_scale=w_scales[:, slot, :],
                        start=(c == 0),
                        stop=(c == PASSES - 1),
                    )

        def finish_half(half):
            first = half * HALF
            result = consts.tile([B, HALF, N], F32, name="result%d" % half)
            for s in range(HALF):
                nc.vector.tensor_tensor(out=result[:, s, :], in0=b1_all[:, first + s, :], in1=banks[s][:], op=ALU.add)
            for pair in range(HALF // PAIR):
                part = result[:, pair * PAIR : (pair + 1) * PAIR, :]
                nc.vector.tensor_scalar_max(part, part, 0.0)
                nc.sync.dma_start(out=out_rows[:, first + pair * PAIR : first + (pair + 1) * PAIR, :], in_=part)

        def load_bias():
            nc.sync.dma_start(out=bias_rows[0:S, :], in_=be1.rearrange("s o n -> (s o) n"))
            nc.sync.dma_start(out=bias_rows[S : S + 1, :], in_=bv1.unsqueeze(0))
            nc.sync.dma_start(out=bias_rows[S + 1 : S + 2, :], in_=bm1.unsqueeze(0))

        def make_bias_columns():
            bias_cols = psum_t.tile([N, P], BF16, tag="t")
            nc.tensor.transpose(bias_cols[:], bias_rows[:], ident_bf[:])
            b_std = consts.tile([N, 1], F32)
            nc.scalar.activation(out=b_std[:], in_=bias_cols[:, S : S + 1], func=ACT.Exp, scale=0.5)
            b_mean = consts.tile([N, 1], F32)
            nc.scalar.copy(out=b_mean[:], in_=bias_cols[:, S + 1 : S + 2])
            nc.scalar.activation(
                out=b1_cols[:], in_=bias_cols[:, 0:S], func=ACT.Identity, scale=b_std[:], bias=b_mean[:]
            )

        def spread_bias(half):
            b1_ps = psum_t.tile([B, HALF, N], F32, tag="t")
            for m in range(HALF):
                s = half * HALF + m
                nc.tensor.matmul(
                    out=b1_ps[:, m, :],
                    lhsT=b1_cols[:, s : s + 1].to_broadcast([N, B]),
                    rhs=ident_f32[:],
                    start=True,
                    stop=True,
                )
            nc.scalar.copy(out=b1_all[:, half * HALF : (half + 1) * HALF, :], in_=b1_ps[:])

        ident_bf = consts.tile([P, P], BF16)
        make_identity(nc, ident_bf[:])
        ident_f32 = consts.tile([P, P], F32)
        make_identity(nc, ident_f32[:])
        bias_rows = consts.tile([P, P], BF16)
        nc.vector.memset(bias_rows[:], 0.0)
        b1_cols = consts.tile([N, S], F32)
        b1_all = consts.tile([B, S, N], F32)
        warm = consts.tile([P, 1], F32)
        nc.vector.memset(warm[:], 0.0)
        nc.scalar.activation(out=warm[:], in_=warm[:], func=ACT.Exp)

        load_weights(0)
        load_h(0)
        load_weights(1)
        load_h(1)
        load_weights(2)

        first_std = consts.tile([P, 2, 2, N, 2], F32)
        first_mean = consts.tile([P, 2, N, 2, 2], BF16)
        for q in range(2):
            wv_pairs = raws[0][0][:, q].rearrange("p (h i) n -> p h n i", h=2)
            nc.scalar.activation(out=first_std[:, q], in_=wv_pairs, func=ACT.Exp, scale=0.5)
            wm_rows_q = (raws[0][1] if q == 0 else mean_rows[0])[:]
            nc.scalar.copy(out=first_mean[:, q], in_=wm_rows_q.rearrange("p (h i) n -> p n h i", h=2))
        for slots in (range(0, PAIR), range(PAIR, HALF)):
            vector_multiply(0, first_std[:, 0], slots=slots)
        vector_add(0, first_mean[:, 0], slots=range(0, PAIR))
        vector_multiply(0, first_std[:, 1], q=1)
        vector_add(0, first_mean[:, 0], slots=range(PAIR, HALF))
        vector_add(0, first_mean[:, 1], q=1)
        for part in range(2):
            flip_h(0, part)
        flip_first(1)
        flip_h(0, 2)
        flip_h(0, 3)
        std_to_psum(1)
        quantise_w(0)
        quantise_h(0)
        flip_second(1)
        flip_noise(1)
        multiply_flipped(1)
        std_in_sbuf(1)
        matmuls(0)
        gpsimd_multiply(1)
        gpsimd_add(1)
        load_weights(3)
        load_h(2)
        vector_multiply(1, in_psum[1])
        flip_back(1, 0)
        flip_back(1, 1)
        std_in_sbuf(2)
        gpsimd_multiply(2)
        flip_h(1, 0)
        mean_to_psum(1)
        flip_second(2)
        flip_noise(2)
        flip_h(1, 1)
        flip_first(2)
        interleave_rows(1)
        flip_h(1, 2)

        for m in range(1, WINDOWS):
            if m + 2 < WINDOWS:
                load_h(m + 2)
            if m + 3 < WINDOWS:
                load_weights(m + 3)
            if m == HALF_WINDOWS - 3:
                load_bias()
            more = m + 1 < WINDOWS
            more2 = m + 2 < WINDOWS
            fresh = m + 2 <= HALF_WINDOWS

            if more:
                gpsimd_add(m + 1)
            vector_add(m, in_psum[m])
            if fresh:
                std_in_sbuf(m + 2)
            if more2:
                gpsimd_multiply(m + 2)
            if more:
                flip_h(m, 3)
            if more:
                multiply_flipped(m + 1)
                std_to_psum(m + 1)
                vector_multiply(m + 1, in_psum[m + 1])
                interleave_rows(m + 1)
                flip_back(m + 1, 0)
                flip_back(m + 1, 1)
                flip_h(m + 1, 0)
                mean_to_psum(m + 1)
            if m in (HALF_WINDOWS - 1, HALF_WINDOWS + 1):
                spread_bias(m // HALF_WINDOWS)
            if fresh:
                flip_first(m + 2)
            if more:
                flip_h(m + 1, 1)
                flip_h(m + 1, 2)
            if m + 2 == WINDOWS:
                flip_h(m + 1, 3)
            if fresh:
                flip_second(m + 2)
            if m == HALF_WINDOWS - 2:
                make_bias_columns()
            if more2:
                flip_noise(m + 2)
            if m == HALF_WINDOWS:
                finish_half(0)
            quantise_h(m)
            quantise_w(m)
            matmuls(m)


        finish_half(1)
